import numpy as np
import ml_dtypes


def mxq(x, axis, fmt="e4m3"):
    dtype, down = {"e4m3": (ml_dtypes.float8_e4m3fn, 7), "e5m2": (ml_dtypes.float8_e5m2, 14)}[fmt]
    v = np.moveaxis(np.asarray(x, np.float32).astype(ml_dtypes.bfloat16).astype(np.float64), axis, -1)
    blocks = v.reshape(v.shape[:-1] + (-1, 32))
    amax = np.abs(blocks).max(-1, keepdims=True)
    byte = np.maximum(np.where(amax > 0, np.frexp(amax)[1] - 1 + 127, 0) - down, 1)
    scale = np.exp2(byte - 127.0)
    codes = (blocks / scale).astype(np.float32).astype(dtype).astype(np.float64)
    return np.moveaxis((codes * scale).reshape(v.shape), -1, axis)


WIDE = False


def mx_kscale(k):
    if not WIDE:
        return np.ones(k)
    levels = np.array([10, -10, 5, -5, 0])
    a = np.random.permutation(np.resize(levels, k // 512 * 4)).reshape(k // 512, 4)
    idx = np.arange(k)
    return np.exp2(a[idx // 512, idx % 128 // 32])


BF16 = ml_dtypes.bfloat16


def bf(x):
    return np.asarray(x, np.float32).astype(BF16)


def f64(x):
    return np.asarray(x).astype(np.float64)


B, S, N, C, H = 1, 512, 4, 1024, 8
D = C // H
EPS = 1e-5


def split_heads(x):
    return x.reshape(B, S, H, D).transpose(0, 2, 1, 3)


def split_ref_heads(x):
    return x.reshape(B, N, S, H, D).transpose(0, 3, 1, 2, 4)


def setup_inputs():
    s = mx_kscale(C)
    hs = np.random.standard_normal((B, S, C)) + 0.5 * np.random.standard_normal((B, 1, C))
    wv = np.random.standard_normal((C, C)) / np.sqrt(C) * np.exp(0.5 * np.random.standard_normal(C))
    rv = np.random.standard_normal((B, N, S, C)) * np.exp(0.5 * np.random.standard_normal((B, N, 1, C))) + np.random.standard_normal((B, N, 1, C))
    return {"hidden_states": bf(hs * s),
            "q": bf(1.5 * np.random.standard_normal((B, S, C))),
            "k": bf(1.5 * np.random.standard_normal((B, S, C))),
            "ref_key": bf(1.5 * np.random.standard_normal((B, N, S, C))),
            "ref_value": bf(rv),
            "Wv": bf(wv / s[:, None])}


def reference(hidden_states, q, k, ref_key, ref_value, Wv):
    v = mxq(f64(hidden_states), 2, "e4m3") @ mxq(f64(Wv), 0, "e4m3")
    qh, kh, vh = split_heads(f64(q)), split_heads(f64(k)), split_heads(v)
    rk = split_ref_heads(f64(ref_key)).reshape(B, H, N * S, D)
    rv = split_ref_heads(f64(ref_value))
    style_mean = vh.mean(axis=2, keepdims=True)[:, :, None]
    style_std = vh.std(axis=2, keepdims=True, ddof=1)[:, :, None] + EPS
    content_mean = rv.mean(axis=3, keepdims=True)
    content_std = rv.std(axis=3, keepdims=True, ddof=1) + EPS
    rv = (rv - content_mean) / content_std * style_std + style_mean
    v_ext = np.concatenate([vh, rv.reshape(B, H, N * S, D)], axis=2)
    sc = np.concatenate([qh @ kh.transpose(0, 1, 3, 2), qh @ rk.transpose(0, 1, 3, 2)], axis=3) * D ** -0.5
    e = np.exp(sc - sc.max(-1, keepdims=True))
    out = (mxq(e, 3, "e4m3") @ mxq(v_ext, 2, "e4m3")) / e.sum(-1, keepdims=True)
    return out.transpose(0, 2, 1, 3).reshape(B, S, C)

@@ -1,0 +1,282 @@
+from contextlib import ExitStack
+
+import concourse.mybir as mybir
+from concourse.masks import make_identity
+
+BF16 = mybir.dt.bfloat16
+F32 = mybir.dt.float32
+U32 = mybir.dt.uint32
+U8 = mybir.dt.uint8
+FP8X4 = mybir.dt.float8_e4m3fn_x4
+ALU = mybir.AluOpType
+ACT = mybir.ActivationFunctionType
+AXIS = mybir.AxisListType
+
+P = 128
+TOKENS = 512
+CHANNELS = 1024
+HEADS = 8
+HEAD_DIM = CHANNELS // HEADS
+REFS = 4
+SEQS = REFS + 1
+KEYS = SEQS * TOKENS
+ROW_TILES = TOKENS // P
+PACK = 4
+HALVES = 2
+CH_PASSES = CHANNELS // TOKENS
+EPS = 1e-5
+SCORE_SCALE = HEAD_DIM**-0.5
+UNBIASED = TOKENS / (TOKENS - 1.0)
+SMALLEST_VARIANCE = 1e-30
+
+FLOPS = 2 * TOKENS * CHANNELS * CHANNELS + 2 * (2 * HEADS * TOKENS * KEYS * HEAD_DIM)
+
+
+def load_sequence(nc, pool, rows, name):
+    seq = pool.tile([P, ROW_TILES, CHANNELS], BF16, name=name)
+    nc.sync.dma_start(out=seq[:], in_=rows.rearrange("(r p) c -> p r c", p=P))
+    return seq
+
+
+def words_view(grouped):
+    return grouped[:].bitcast(F32).rearrange("p (b r u) -> p b r u", r=P, u=HALVES)
+
+
+def transpose_passes(nc, psum, ident_f32, sources, grouped_words, copy):
+    bank = psum.tile([P, len(sources), HALVES, P], F32, tag="words")
+    for b, source in enumerate(sources):
+        for u in range(HALVES):
+            nc.tensor.transpose(bank[:, b, u, :], source[:, u * P : (u + 1) * P], ident_f32[:])
+    copy(out=grouped_words, in_=bank[:].rearrange("p b u r -> p b r u"))
+
+
+def transpose_head_pair(nc, psum, ident_bf16, seq, h0):
+    pair = psum.tile([P, 2, TOKENS], BF16, tag="plain")
+    for j in range(2):
+        for r in range(ROW_TILES):
+            nc.tensor.transpose(
+                pair[:, j, r * P : (r + 1) * P],
+                seq[:, r, (h0 + j) * HEAD_DIM : (h0 + j + 1) * HEAD_DIM],
+                ident_bf16[:],
+            )
+    return pair
+
+
+def std_plus_eps(nc, pool, mean_var, name):
+    std = pool.tile([P, HEADS], F32, name=name)
+    nc.vector.tensor_scalar(
+        out=std[:], in0=mean_var[:, :, 1], scalar1=UNBIASED, scalar2=SMALLEST_VARIANCE,
+        op0=ALU.mult, op1=ALU.max,
+    )
+    nc.scalar.activation(out=std[:], in_=std[:], func=ACT.Sqrt)
+    nc.vector.tensor_scalar_add(out=std[:], in0=std[:], scalar1=EPS)
+    return std
+
+
+def tile_sharedattnprocessor_pa_kernel(tc, hidden_states, q, k, ref_key, ref_value, Wv, out):
+    nc = tc.nc
+    with ExitStack() as whole:
+        const = whole.enter_context(tc.tile_pool(name="const", bufs=1))
+        keep = whole.enter_context(tc.tile_pool(name="keep", bufs=1))
+        psum = whole.enter_context(tc.psum_pool(name="psum", bufs=3))
+
+        ident_bf16 = const.tile([P, P], BF16)
+        make_identity(nc, ident_bf16[:])
+        ident_f32 = const.tile([P, P], F32)
+        make_identity(nc, ident_f32[:])
+
+        qT = keep.tile([P, HEADS, TOKENS], BF16)
+        kT = keep.tile([P, HEADS, KEYS], BF16)
+        v_codes = keep.tile([P, SEQS, CHANNELS], U32, align_bytes=64)
+        v_scales = keep.tile([P, SEQS, CHANNELS], U8, align_bytes=64)
+
+        with ExitStack() as prepare:
+            proj = prepare.enter_context(tc.tile_pool(name="proj", bufs=1))
+            seqs = prepare.enter_context(tc.tile_pool(name="seqs", bufs=1))
+            stage = prepare.enter_context(tc.tile_pool(name="stage", bufs=2))
+            stats = prepare.enter_context(tc.tile_pool(name="stats", bufs=1))
+
+            hs = load_sequence(nc, seqs, hidden_states[0], "hs")
+            wv_raw = proj.tile([P, CH_PASSES * HALVES, 2, CHANNELS], BF16)
+            wv_rows = Wv.rearrange("(a p e) c -> p a e c", p=P, e=2)
+            for g in range(CH_PASSES):
+                nc.sync.dma_start(
+                    out=wv_raw[:, g * HALVES : (g + 1) * HALVES], in_=wv_rows[:, g * HALVES : (g + 1) * HALVES]
+                )
+            values = [load_sequence(nc, seqs, ref_value[0, 0], "values0")]
+            queries = load_sequence(nc, seqs, q[0], "queries")
+            keys = [load_sequence(nc, seqs, k[0], "keys0")]
+            for n in range(1, REFS):
+                values.append(load_sequence(nc, seqs, ref_value[0, n], "values%d" % n))
+                keys.append(load_sequence(nc, seqs, ref_key[0, n - 1], "keys%d" % n))
+            keys.append(load_sequence(nc, seqs, ref_key[0, REFS - 1], "keys%d" % REFS))
+
+            hs_grouped = proj.tile([P, CH_PASSES * TOKENS * PACK], BF16, align_bytes=64)
+            hs_codes = proj.tile([P, CH_PASSES * TOKENS], U32, align_bytes=64)
+            hs_scales = proj.tile([P, CH_PASSES * TOKENS], U8, align_bytes=64)
+            hs_words = words_view(hs_grouped)
+            for g in range(CH_PASSES):
+                for r in range(0, ROW_TILES, 2):
+                    blocks = [hs[:, r + j, g * TOKENS : (g + 1) * TOKENS].bitcast(F32) for j in range(2)]
+                    b0 = g * ROW_TILES + r
+                    transpose_passes(nc, psum, ident_f32, blocks, hs_words[:, b0 : b0 + 2], nc.scalar.copy)
+            nc.vector.quantize_mx(out=hs_codes[:].bitcast(FP8X4), scales=hs_scales[:], in_=hs_grouped[:])
+
+            wv_codes = proj.tile([P, CH_PASSES * CHANNELS], U32, align_bytes=64)
+            wv_scales = proj.tile([P, CH_PASSES * CHANNELS], U8, align_bytes=64)
+            for g in range(CH_PASSES):
+                four_rows = wv_raw[:, g * HALVES : (g + 1) * HALVES].rearrange("p a e c -> p (a e) c")
+                for half in range(2):
+                    cols = slice(half * TOKENS, (half + 1) * TOKENS)
+                    wv_grouped = stage.tile([P, TOKENS, PACK], BF16, align_bytes=64)
+                    nc.vector.tensor_copy(
+                        out=wv_grouped[:].rearrange("p (c i) t -> p c t i", i=4),
+                        in_=four_rows[:, :, cols].rearrange("p t (c i) -> p c t i", i=4),
+                    )
+                    words = slice(g * CHANNELS + half * TOKENS, g * CHANNELS + (half + 1) * TOKENS)
+                    nc.vector.quantize_mx(
+                        out=wv_codes[:, words].bitcast(FP8X4),
+                        scales=wv_scales[:, words],
+                        in_=wv_grouped[:].rearrange("p c t -> p (c t)"),
+                    )
+
+            def quantise_values(g, channel_major_pair):
+                for quad in range(0, HEADS, 4):
+                    v_grouped = stage.tile([P, 4 * HEAD_DIM * PACK], BF16, align_bytes=64)
+                    v_words = words_view(v_grouped)
+                    for j0 in range(0, 4, 2):
+                        pair_bf16 = channel_major_pair(quad + j0)
+                        blocks = [pair_bf16[:, j, :].bitcast(F32) for j in range(2)]
+                        transpose_passes(nc, psum, ident_f32, blocks, v_words[:, j0 : j0 + 2], nc.vector.tensor_copy)
+                    cols = slice(quad * HEAD_DIM, (quad + 4) * HEAD_DIM)
+                    nc.vector.quantize_mx(
+                        out=v_codes[:, g, cols].bitcast(FP8X4), scales=v_scales[:, g, cols], in_=v_grouped[:]
+                    )
+
+            style_stats = stats.tile([P, HEADS, 6], F32)
+            style_mv = stats.tile([P, HEADS, 2], F32)
+
+            def projected_pair(h0):
+                pair_bf16 = stage.tile([P, 2, TOKENS], BF16, tag="pair_bf16", bufs=3)
+                for j in range(2):
+                    h = h0 + j
+                    vT = psum.tile([P, TOKENS], F32, tag="mx", bufs=2)
+                    for g in range(CH_PASSES):
+                        w_cols = slice(g * CHANNELS + h * HEAD_DIM, g * CHANNELS + (h + 1) * HEAD_DIM)
+                        t_cols = slice(g * TOKENS, (g + 1) * TOKENS)
+                        nc.tensor.matmul_mx(
+                            out=vT[:],
+                            lhsT=wv_codes[:, w_cols].bitcast(FP8X4),
+                            lhsT_scale=wv_scales[:, w_cols],
+                            rhs=hs_codes[:, t_cols].bitcast(FP8X4),
+                            rhs_scale=hs_scales[:, t_cols],
+                            start=(g == 0),
+                            stop=(g == CH_PASSES - 1),
+                        )
+                    nc.vector.bn_stats(out=style_stats[:, h, :], in_=vT[:])
+                    nc.vector.bn_aggr(out=style_mv[:, h, :], in_=style_stats[:, h, :])
+                    nc.scalar.copy(out=pair_bf16[:, j, :], in_=vT[:])
+                return pair_bf16
+
+            quantise_values(0, projected_pair)
+            style_std = std_plus_eps(nc, stats, style_mv, "style_std")
+
+            for n in range(REFS):
+                content_stats = stats.tile([P, HEADS, 6], F32, tag="content_stats", bufs=2)
+                content_mv = stats.tile([P, HEADS, 2], F32, tag="content_mv", bufs=2)
+                for h0 in range(0, HEADS, 2):
+                    pair = transpose_head_pair(nc, psum, ident_bf16, values[n], h0)
+                    for j in range(2):
+                        nc.vector.bn_stats(out=content_stats[:, h0 + j, :], in_=pair[:, j, :])
+                        nc.vector.bn_aggr(out=content_mv[:, h0 + j, :], in_=content_stats[:, h0 + j, :])
+                content_std = std_plus_eps(nc, stats, content_mv, "content_std%d" % n)
+                gain = stats.tile([P, HEADS], F32, tag="gain", bufs=2)
+                shift = stats.tile([P, HEADS], F32, tag="shift", bufs=2)
+                nc.vector.reciprocal(out=gain[:], in_=content_std[:])
+                nc.vector.tensor_mul(out=gain[:], in0=gain[:], in1=style_std[:])
+                nc.vector.tensor_mul(out=shift[:], in0=content_mv[:, :, 0], in1=gain[:])
+                nc.vector.tensor_sub(out=shift[:], in0=style_mv[:, :, 0], in1=shift[:])
+
+                def adain_pair(h0):
+                    pair = transpose_head_pair(nc, psum, ident_bf16, values[n], h0)
+                    pair_bf16 = stage.tile([P, 2, TOKENS], BF16, tag="pair_bf16", bufs=3)
+                    for j in range(2):
+                        nc.scalar.activation(
+                            out=pair_bf16[:, j, :], in_=pair[:, j, :], func=ACT.Identity,
+                            scale=gain[:, h0 + j : h0 + j + 1], bias=shift[:, h0 + j : h0 + j + 1],
+                        )
+                    return pair_bf16
+
+                quantise_values(n + 1, adain_pair)
+
+            for h0 in range(0, HEADS, 2):
+                pair = transpose_head_pair(nc, psum, ident_bf16, queries, h0)
+                nc.scalar.copy(out=qT[:, h0 : h0 + 2, :], in_=pair[:])
+                for g in range(SEQS):
+                    pair = transpose_head_pair(nc, psum, ident_bf16, keys[g], h0)
+                    nc.scalar.copy(out=kT[:, h0 : h0 + 2, g * TOKENS : (g + 1) * TOKENS], in_=pair[:])
+
+        with ExitStack() as attend:
+            work = attend.enter_context(tc.tile_pool(name="work", bufs=3, reuse_waits="tile"))
+            small = attend.enter_context(tc.tile_pool(name="small", bufs=4, reuse_waits="tile"))
+            for h in range(HEADS):
+                for qt in range(ROW_TILES):
+                    scores = work.tile([P, KEYS], F32)
+                    bank_max = small.tile([P, SEQS], F32)
+                    for g in range(SEQS):
+                        s_bank = psum.tile([P, TOKENS], F32, tag="plain")
+                        nc.tensor.matmul(
+                            s_bank[:],
+                            lhsT=qT[:, h, qt * P : (qt + 1) * P],
+                            rhs=kT[:, h, g * TOKENS : (g + 1) * TOKENS],
+                            start=True,
+                            stop=True,
+                        )
+                        nc.vector.tensor_scalar(
+                            out=scores[:, g * TOKENS : (g + 1) * TOKENS], in0=s_bank[:],
+                            scalar1=SCORE_SCALE, scalar2=None, op0=ALU.mult, op1=ALU.max,
+                            accum_out=bank_max[:, g : g + 1],
+                        )
+                    neg_max = small.tile([P, 1], F32)
+                    nc.vector.tensor_reduce(out=neg_max[:], in_=bank_max[:], axis=AXIS.X, op=ALU.max, negate=True)
+
+                    e = work.tile([P, KEYS], BF16)
+                    row_sum = small.tile([P, 1], F32)
+                    nc.scalar.activation(
+                        out=e[:], in_=scores[:], func=ACT.Exp, bias=neg_max[:], scale=1.0, accum_out=row_sum[:]
+                    )
+
+                    e_grouped = work.tile([P, KEYS], BF16, align_bytes=64)
+                    e_codes = work.tile([P, SEQS * P], U32, align_bytes=64)
+                    e_scales = work.tile([P, SEQS * P], U8, align_bytes=64)
+                    e_words = words_view(e_grouped)
+                    for g0 in range(0, SEQS, 2):
+                        passes = range(g0, min(g0 + 2, SEQS))
+                        blocks = [e[:, g * TOKENS : (g + 1) * TOKENS].bitcast(F32) for g in passes]
+                        transpose_passes(nc, psum, ident_f32, blocks, e_words[:, g0 : g0 + len(blocks)], nc.scalar.copy)
+                    for first, count in ((0, 4), (4, 1)):
+                        cols = slice(first * P, (first + count) * P)
+                        nc.vector.quantize_mx(
+                            out=e_codes[:, cols].bitcast(FP8X4),
+                            scales=e_scales[:, cols],
+                            in_=e_grouped[:, first * P * PACK : (first + count) * P * PACK],
+                        )
+
+                    o_bank = psum.tile([P, HEAD_DIM], F32, tag="mx", bufs=2)
+                    for g in range(SEQS):
+                        nc.tensor.matmul_mx(
+                            out=o_bank[:],
+                            lhsT=e_codes[:, g * P : (g + 1) * P].bitcast(FP8X4),
+                            lhsT_scale=e_scales[:, g * P : (g + 1) * P],
+                            rhs=v_codes[:, g, h * HEAD_DIM : (h + 1) * HEAD_DIM].bitcast(FP8X4),
+                            rhs_scale=v_scales[:, g, h * HEAD_DIM : (h + 1) * HEAD_DIM],
+                            start=(g == 0),
+                            stop=(g == SEQS - 1),
+                        )
+                    inv_sum = small.tile([P, 1], F32)
+                    nc.vector.reciprocal(out=inv_sum[:], in_=row_sum[:])
+                    o = work.tile([P, HEAD_DIM], F32)
+                    nc.vector.tensor_scalar_mul(out=o[:], in0=o_bank[:], scalar1=inv_sum[:])
+                    nc.sync.dma_start(
+                        out=out[0, qt * P : (qt + 1) * P, h * HEAD_DIM : (h + 1) * HEAD_DIM], in_=o[:]
+                    )

@@ -22,12 +22,15 @@ SEQS = REFS + 1
 KEYS = SEQS * TOKENS
 ROW_TILES = TOKENS // P
 PACK = 4
+PAIR = 2
 HALVES = 2
 CH_PASSES = CHANNELS // TOKENS
 EPS = 1e-5
 SCORE_SCALE = HEAD_DIM**-0.5
 UNBIASED = TOKENS / (TOKENS - 1.0)
 SMALLEST_VARIANCE = 1e-30
+
+UNITS = HEADS * ROW_TILES
 
 FLOPS = 2 * TOKENS * CHANNELS * CHANNELS + 2 * (2 * HEADS * TOKENS * KEYS * HEAD_DIM)
 
@@ -42,17 +45,19 @@ def words_view(grouped):
     return grouped[:].bitcast(F32).rearrange("p (b r u) -> p b r u", r=P, u=HALVES)
 
 
-def transpose_passes(nc, psum, ident_f32, sources, grouped_words, copy):
-    bank = psum.tile([P, len(sources), HALVES, P], F32, tag="words")
-    for b, source in enumerate(sources):
-        for u in range(HALVES):
-            nc.tensor.transpose(bank[:, b, u, :], source[:, u * P : (u + 1) * P], ident_f32[:])
-    copy(out=grouped_words, in_=bank[:].rearrange("p b u r -> p b r u"))
+def transpose_pass(nc, half_bank, block, ident_f32):
+    block_words = block.bitcast(F32)
+    for u in range(HALVES):
+        nc.tensor.transpose(half_bank[:, u, :], block_words[:, u * P : (u + 1) * P], ident_f32[:])
 
 
-def transpose_head_pair(nc, psum, ident_bf16, seq, h0):
-    pair = psum.tile([P, 2, TOKENS], BF16, tag="plain")
-    for j in range(2):
+def group_words(copy, grouped_words, bank):
+    copy(out=grouped_words, in_=bank.rearrange("p b u r -> p b r u"))
+
+
+def transpose_head_pair(nc, psum, tag, ident_bf16, seq, h0):
+    pair = psum.tile([P, PAIR, TOKENS], BF16, tag=tag)
+    for j in range(PAIR):
         for r in range(ROW_TILES):
             nc.tensor.transpose(
                 pair[:, j, r * P : (r + 1) * P],
@@ -62,23 +67,12 @@ def transpose_head_pair(nc, psum, ident_bf16, seq, h0):
     return pair
 
 
-def std_plus_eps(nc, pool, mean_var, name):
-    std = pool.tile([P, HEADS], F32, name=name)
-    nc.vector.tensor_scalar(
-        out=std[:], in0=mean_var[:, :, 1], scalar1=UNBIASED, scalar2=SMALLEST_VARIANCE,
-        op0=ALU.mult, op1=ALU.max,
-    )
-    nc.scalar.activation(out=std[:], in_=std[:], func=ACT.Sqrt)
-    nc.vector.tensor_scalar_add(out=std[:], in0=std[:], scalar1=EPS)
-    return std
-
-
 def tile_sharedattnprocessor_pa_kernel(tc, hidden_states, q, k, ref_key, ref_value, Wv, out):
     nc = tc.nc
     with ExitStack() as whole:
+        whole.enter_context(tc.manual_schedule())
         const = whole.enter_context(tc.tile_pool(name="const", bufs=1))
         keep = whole.enter_context(tc.tile_pool(name="keep", bufs=1))
-        psum = whole.enter_context(tc.psum_pool(name="psum", bufs=3))
 
         ident_bf16 = const.tile([P, P], BF16)
         make_identity(nc, ident_bf16[:])
@@ -91,140 +85,183 @@ def tile_sharedattnprocessor_pa_kernel(tc, hidden_states, q, k, ref_key, ref_val
         v_scales = keep.tile([P, SEQS, CHANNELS], U8, align_bytes=64)
 
         with ExitStack() as prepare:
-            proj = prepare.enter_context(tc.tile_pool(name="proj", bufs=1))
             seqs = prepare.enter_context(tc.tile_pool(name="seqs", bufs=1))
-            stage = prepare.enter_context(tc.tile_pool(name="stage", bufs=2))
             stats = prepare.enter_context(tc.tile_pool(name="stats", bufs=1))
+            psum = prepare.enter_context(tc.psum_pool(name="psum_prepare", bufs=2))
+            hs_codes = stats.tile([P, CH_PASSES * TOKENS], U32, align_bytes=64)
+            hs_scales = stats.tile([P, CH_PASSES * TOKENS], U8, align_bytes=64)
+            wv_codes = stats.tile([P, CH_PASSES * CHANNELS], U32, align_bytes=64)
+            wv_scales = stats.tile([P, CH_PASSES * CHANNELS], U8, align_bytes=64)
 
-            hs = load_sequence(nc, seqs, hidden_states[0], "hs")
-            wv_raw = proj.tile([P, CH_PASSES * HALVES, 2, CHANNELS], BF16)
-            wv_rows = Wv.rearrange("(a p e) c -> p a e c", p=P, e=2)
-            for g in range(CH_PASSES):
-                nc.sync.dma_start(
-                    out=wv_raw[:, g * HALVES : (g + 1) * HALVES], in_=wv_rows[:, g * HALVES : (g + 1) * HALVES]
-                )
-            values = [load_sequence(nc, seqs, ref_value[0, 0], "values0")]
-            queries = load_sequence(nc, seqs, q[0], "queries")
-            keys = [load_sequence(nc, seqs, k[0], "keys0")]
-            for n in range(1, REFS):
-                values.append(load_sequence(nc, seqs, ref_value[0, n], "values%d" % n))
-                keys.append(load_sequence(nc, seqs, ref_key[0, n - 1], "keys%d" % n))
-            keys.append(load_sequence(nc, seqs, ref_key[0, REFS - 1], "keys%d" % REFS))
+            with tc.tile_pool(name="early", bufs=1) as early:
+                hs = load_sequence(nc, early, hidden_states[0], "hs")
+                wv_raw = early.tile([P, CH_PASSES * HALVES, 2, CHANNELS], BF16)
+                wv_rows = Wv.rearrange("(a p e) c -> p a e c", p=P, e=2)
+                for g in range(CH_PASSES):
+                    places = slice(g * HALVES, (g + 1) * HALVES)
+                    nc.sync.dma_start(out=wv_raw[:, places], in_=wv_rows[:, places])
+                key_side = [load_sequence(nc, seqs, q[0], "queries")]
+                values = [load_sequence(nc, seqs, ref_value[0, 0], "values0")]
+                key_side.append(load_sequence(nc, seqs, k[0], "keys"))
+                for n in range(1, REFS):
+                    values.append(load_sequence(nc, seqs, ref_value[0, n], "values%d" % n))
+                    key_side.append(load_sequence(nc, seqs, ref_key[0, n - 1], "ref_keys%d" % (n - 1)))
+                key_side.append(load_sequence(nc, seqs, ref_key[0, REFS - 1], "ref_keys%d" % (REFS - 1)))
 
-            hs_grouped = proj.tile([P, CH_PASSES * TOKENS * PACK], BF16, align_bytes=64)
-            hs_codes = proj.tile([P, CH_PASSES * TOKENS], U32, align_bytes=64)
-            hs_scales = proj.tile([P, CH_PASSES * TOKENS], U8, align_bytes=64)
-            hs_words = words_view(hs_grouped)
-            for g in range(CH_PASSES):
-                for r in range(0, ROW_TILES, 2):
-                    blocks = [hs[:, r + j, g * TOKENS : (g + 1) * TOKENS].bitcast(F32) for j in range(2)]
-                    b0 = g * ROW_TILES + r
-                    transpose_passes(nc, psum, ident_f32, blocks, hs_words[:, b0 : b0 + 2], nc.scalar.copy)
-            nc.vector.quantize_mx(out=hs_codes[:].bitcast(FP8X4), scales=hs_scales[:], in_=hs_grouped[:])
+                hs_grouped = early.tile([P, CH_PASSES * TOKENS * PACK], BF16, align_bytes=64)
+                hs_words = words_view(hs_grouped)
+                for g in range(CH_PASSES):
+                    for r in range(0, ROW_TILES, 2):
+                        bank = psum.tile([P, 2, HALVES, P], F32, tag="words")
+                        for j in range(2):
+                            transpose_pass(nc, bank[:, j], hs[:, r + j, g * TOKENS : (g + 1) * TOKENS], ident_f32)
+                        b0 = g * ROW_TILES + r
+                        group_words(nc.scalar.copy, hs_words[:, b0 : b0 + 2], bank[:])
 
-            wv_codes = proj.tile([P, CH_PASSES * CHANNELS], U32, align_bytes=64)
-            wv_scales = proj.tile([P, CH_PASSES * CHANNELS], U8, align_bytes=64)
-            for g in range(CH_PASSES):
-                four_rows = wv_raw[:, g * HALVES : (g + 1) * HALVES].rearrange("p a e c -> p (a e) c")
-                for half in range(2):
-                    cols = slice(half * TOKENS, (half + 1) * TOKENS)
-                    wv_grouped = stage.tile([P, TOKENS, PACK], BF16, align_bytes=64)
-                    nc.vector.tensor_copy(
-                        out=wv_grouped[:].rearrange("p (c i) t -> p c t i", i=4),
-                        in_=four_rows[:, :, cols].rearrange("p t (c i) -> p c t i", i=4),
-                    )
+                chunks = [(g, half) for g in range(CH_PASSES) for half in range(2)]
+                wv_grouped = {}
+
+                def quantise_wv(c):
+                    g, half = chunks[c]
                     words = slice(g * CHANNELS + half * TOKENS, g * CHANNELS + (half + 1) * TOKENS)
                     nc.vector.quantize_mx(
                         out=wv_codes[:, words].bitcast(FP8X4),
                         scales=wv_scales[:, words],
-                        in_=wv_grouped[:].rearrange("p c t -> p (c t)"),
+                        in_=wv_grouped[c][:].rearrange("p c t -> p (c t)"),
                     )
 
-            def quantise_values(g, channel_major_pair):
-                for quad in range(0, HEADS, 4):
-                    v_grouped = stage.tile([P, 4 * HEAD_DIM * PACK], BF16, align_bytes=64)
-                    v_words = words_view(v_grouped)
-                    for j0 in range(0, 4, 2):
-                        pair_bf16 = channel_major_pair(quad + j0)
-                        blocks = [pair_bf16[:, j, :].bitcast(F32) for j in range(2)]
-                        transpose_passes(nc, psum, ident_f32, blocks, v_words[:, j0 : j0 + 2], nc.vector.tensor_copy)
-                    cols = slice(quad * HEAD_DIM, (quad + 4) * HEAD_DIM)
-                    nc.vector.quantize_mx(
-                        out=v_codes[:, g, cols].bitcast(FP8X4), scales=v_scales[:, g, cols], in_=v_grouped[:]
+                for c, (g, half) in enumerate(chunks):
+                    four_rows = wv_raw[:, g * HALVES : (g + 1) * HALVES].rearrange("p a e c -> p (a e) c")
+                    wv_grouped[c] = early.tile([P, TOKENS, PACK], BF16, align_bytes=64, name="wv_grouped", bufs=2)
+                    nc.vector.tensor_copy(
+                        out=wv_grouped[c][:].rearrange("p (c i) t -> p c t i", i=4),
+                        in_=four_rows[:, :, half * TOKENS : (half + 1) * TOKENS].rearrange("p t (c i) -> p c t i", i=4),
                     )
+                    if c == 0:
+                        nc.vector.quantize_mx(out=hs_codes[:].bitcast(FP8X4), scales=hs_scales[:], in_=hs_grouped[:])
+                    else:
+                        quantise_wv(c - 1)
+                quantise_wv(len(chunks) - 1)
 
-            style_stats = stats.tile([P, HEADS, 6], F32)
-            style_mv = stats.tile([P, HEADS, 2], F32)
+            stage = prepare.enter_context(tc.tile_pool(name="stage", bufs=3, reuse_waits="tile"))
 
-            def projected_pair(h0):
-                pair_bf16 = stage.tile([P, 2, TOKENS], BF16, tag="pair_bf16", bufs=3)
-                for j in range(2):
-                    h = h0 + j
-                    vT = psum.tile([P, TOKENS], F32, tag="mx", bufs=2)
-                    for g in range(CH_PASSES):
-                        w_cols = slice(g * CHANNELS + h * HEAD_DIM, g * CHANNELS + (h + 1) * HEAD_DIM)
-                        t_cols = slice(g * TOKENS, (g + 1) * TOKENS)
-                        nc.tensor.matmul_mx(
-                            out=vT[:],
-                            lhsT=wv_codes[:, w_cols].bitcast(FP8X4),
-                            lhsT_scale=wv_scales[:, w_cols],
-                            rhs=hs_codes[:, t_cols].bitcast(FP8X4),
-                            rhs_scale=hs_scales[:, t_cols],
-                            start=(g == 0),
-                            stop=(g == CH_PASSES - 1),
-                        )
-                    nc.vector.bn_stats(out=style_stats[:, h, :], in_=vT[:])
-                    nc.vector.bn_aggr(out=style_mv[:, h, :], in_=style_stats[:, h, :])
-                    nc.scalar.copy(out=pair_bf16[:, j, :], in_=vT[:])
-                return pair_bf16
+            six = stats.tile([P, SEQS, HEADS, 6], F32)
+            mean_var = stats.tile([P, SEQS, HEADS, 2], F32)
+            v_bf16 = stage.tile([P, HEADS, TOKENS], BF16, bufs=1)
+            for s in range(SEQS + 1):
+                for h0 in range(0, HEADS, PAIR):
+                    pair = transpose_head_pair(nc, psum, "key_pair", ident_bf16, key_side[s], h0)
+                    if s == 0:
+                        nc.scalar.copy(out=qT[:, h0 : h0 + PAIR, :], in_=pair[:])
+                    else:
+                        nc.scalar.copy(out=kT[:, h0 : h0 + PAIR, (s - 1) * TOKENS : s * TOKENS], in_=pair[:])
+                    if s == 0:
+                        for h in range(h0, h0 + PAIR):
+                            vT = psum.tile([P, TOKENS], F32, tag="mx")
+                            for g in range(CH_PASSES):
+                                w_cols = slice(g * CHANNELS + h * HEAD_DIM, g * CHANNELS + (h + 1) * HEAD_DIM)
+                                t_cols = slice(g * TOKENS, (g + 1) * TOKENS)
+                                nc.tensor.matmul_mx(
+                                    out=vT[:],
+                                    lhsT=wv_codes[:, w_cols].bitcast(FP8X4),
+                                    lhsT_scale=wv_scales[:, w_cols],
+                                    rhs=hs_codes[:, t_cols].bitcast(FP8X4),
+                                    rhs_scale=hs_scales[:, t_cols],
+                                    start=(g == 0),
+                                    stop=(g == CH_PASSES - 1),
+                                )
+                            nc.vector.bn_stats(out=six[:, 0, h, :], in_=vT[:])
+                            nc.scalar.copy(out=v_bf16[:, h, :], in_=vT[:])
+                    elif s <= REFS:
+                        pair = transpose_head_pair(nc, psum, "value_pair", ident_bf16, values[s - 1], h0)
+                        for j in range(PAIR):
+                            nc.vector.bn_stats(out=six[:, s, h0 + j, :], in_=pair[:, j, :])
+                    if s <= REFS:
+                        for h in range(h0, h0 + PAIR):
+                            nc.vector.bn_aggr(out=mean_var[:, s, h, :], in_=six[:, s, h, :])
 
-            quantise_values(0, projected_pair)
-            style_std = std_plus_eps(nc, stats, style_mv, "style_std")
+            std = stats.tile([P, SEQS, HEADS], F32)
+            gain = stats.tile([P, REFS, HEADS], F32)
+            shift = stats.tile([P, REFS, HEADS], F32)
+            nc.vector.tensor_scalar(
+                out=std[:], in0=mean_var[:, :, :, 1], scalar1=UNBIASED, scalar2=SMALLEST_VARIANCE,
+                op0=ALU.mult, op1=ALU.max,
+            )
+            nc.scalar.activation(out=std[:], in_=std[:], func=ACT.Sqrt)
+            nc.vector.tensor_scalar_add(out=std[:], in0=std[:], scalar1=EPS)
+            nc.vector.reciprocal(out=gain[:], in_=std[:, 1:, :])
+            nc.vector.tensor_mul(out=gain[:], in0=gain[:], in1=std[:, 0:1, :].to_broadcast([P, REFS, HEADS]))
+            nc.vector.tensor_mul(out=shift[:], in0=mean_var[:, 1:, :, 0], in1=gain[:])
+            nc.vector.tensor_sub(
+                out=shift[:], in0=mean_var[:, 0:1, :, 0].to_broadcast([P, REFS, HEADS]), in1=shift[:]
+            )
 
-            for n in range(REFS):
-                content_stats = stats.tile([P, HEADS, 6], F32, tag="content_stats", bufs=2)
-                content_mv = stats.tile([P, HEADS, 2], F32, tag="content_mv", bufs=2)
-                for h0 in range(0, HEADS, 2):
-                    pair = transpose_head_pair(nc, psum, ident_bf16, values[n], h0)
-                    for j in range(2):
-                        nc.vector.bn_stats(out=content_stats[:, h0 + j, :], in_=pair[:, j, :])
-                        nc.vector.bn_aggr(out=content_mv[:, h0 + j, :], in_=content_stats[:, h0 + j, :])
-                content_std = std_plus_eps(nc, stats, content_mv, "content_std%d" % n)
-                gain = stats.tile([P, HEADS], F32, tag="gain", bufs=2)
-                shift = stats.tile([P, HEADS], F32, tag="shift", bufs=2)
-                nc.vector.reciprocal(out=gain[:], in_=content_std[:])
-                nc.vector.tensor_mul(out=gain[:], in0=gain[:], in1=style_std[:])
-                nc.vector.tensor_mul(out=shift[:], in0=content_mv[:, :, 0], in1=gain[:])
-                nc.vector.tensor_sub(out=shift[:], in0=style_mv[:, :, 0], in1=shift[:])
+            jobs = [(g, h0) for g in range(SEQS) for h0 in range(0, HEADS, PAIR)]
 
-                def adain_pair(h0):
-                    pair = transpose_head_pair(nc, psum, ident_bf16, values[n], h0)
-                    pair_bf16 = stage.tile([P, 2, TOKENS], BF16, tag="pair_bf16", bufs=3)
-                    for j in range(2):
+            def fill(job):
+                g, h0 = job
+                return transpose_head_pair(nc, psum, "value_pair", ident_bf16, values[g - 1], h0) if g > 0 else None
+
+            def quantise_quad(g, quad, v_grouped):
+                cols = slice(quad * HEAD_DIM, (quad + 4) * HEAD_DIM)
+                nc.vector.quantize_mx(
+                    out=v_codes[:, g, cols].bitcast(FP8X4), scales=v_scales[:, g, cols], in_=v_grouped[:]
+                )
+
+            waiting = None
+            pair = fill(jobs[0])
+            for number, (g, h0) in enumerate(jobs):
+                next_pair = fill(jobs[number + 1]) if number + 1 < len(jobs) else None
+                if g == 0:
+                    channel_major = v_bf16[:, h0 : h0 + PAIR, :]
+                else:
+                    rv_bf16 = stage.tile([P, PAIR, TOKENS], BF16)
+                    for j in range(PAIR):
                         nc.scalar.activation(
-                            out=pair_bf16[:, j, :], in_=pair[:, j, :], func=ACT.Identity,
-                            scale=gain[:, h0 + j : h0 + j + 1], bias=shift[:, h0 + j : h0 + j + 1],
+                            out=rv_bf16[:, j, :], in_=pair[:, j, :], func=ACT.Identity,
+                            scale=gain[:, g - 1, h0 + j : h0 + j + 1], bias=shift[:, g - 1, h0 + j : h0 + j + 1],
                         )
-                    return pair_bf16
-
-                quantise_values(n + 1, adain_pair)
-
-            for h0 in range(0, HEADS, 2):
-                pair = transpose_head_pair(nc, psum, ident_bf16, queries, h0)
-                nc.scalar.copy(out=qT[:, h0 : h0 + 2, :], in_=pair[:])
-                for g in range(SEQS):
-                    pair = transpose_head_pair(nc, psum, ident_bf16, keys[g], h0)
-                    nc.scalar.copy(out=kT[:, h0 : h0 + 2, g * TOKENS : (g + 1) * TOKENS], in_=pair[:])
+                    channel_major = rv_bf16[:]
+                quad = h0 - h0 % 4
+                if h0 == quad:
+                    v_grouped = stage.tile([P, 4 * HEAD_DIM * PACK], BF16, align_bytes=64)
+                bank = psum.tile([P, PAIR, HALVES, P], F32, tag="words")
+                for j in range(PAIR):
+                    transpose_pass(nc, bank[:, j], channel_major[:, j, :], ident_f32)
+                group_words(nc.vector.tensor_copy, words_view(v_grouped)[:, h0 - quad : h0 - quad + PAIR], bank[:])
+                if h0 != quad:
+                    if waiting is not None:
+                        quantise_quad(*waiting)
+                    waiting = (g, quad, v_grouped)
+                pair = next_pair
+            quantise_quad(*waiting)
 
         with ExitStack() as attend:
-            work = attend.enter_context(tc.tile_pool(name="work", bufs=3, reuse_waits="tile"))
-            small = attend.enter_context(tc.tile_pool(name="small", bufs=4, reuse_waits="tile"))
-            for h in range(HEADS):
-                for qt in range(ROW_TILES):
-                    scores = work.tile([P, KEYS], F32)
-                    bank_max = small.tile([P, SEQS], F32)
-                    for g in range(SEQS):
-                        s_bank = psum.tile([P, TOKENS], F32, tag="plain")
+            work = attend.enter_context(tc.tile_pool(name="work", bufs=2, reuse_waits="tile"))
+            small = attend.enter_context(tc.tile_pool(name="small", bufs=3, reuse_waits="tile"))
+            psum = attend.enter_context(tc.psum_pool(name="psum_attend", bufs=3, reuse_waits="tile"))
+            scores, bank_max, neg_max, e, row_sum, inv_sum = {}, {}, {}, {}, {}, {}
+            e_grouped, e_codes, e_scales, o_bank = {}, {}, {}, {}
+
+            def exponential(i):
+                e[i] = work.tile([P, KEYS], BF16, name="e")
+                row_sum[i] = small.tile([P, 1], F32, name="row_sum", bufs=5)
+                nc.scalar.activation(
+                    out=e[i][:], in_=scores[i][:], func=ACT.Exp, bias=neg_max[i][:], scale=1.0,
+                    accum_out=row_sum[i][:],
+                )
+
+            def scores_and_transposes(new, old):
+                if new < UNITS:
+                    h, qt = divmod(new, ROW_TILES)
+                    scores[new] = work.tile([P, KEYS], F32, name="scores")
+                    bank_max[new] = small.tile([P, SEQS], F32, name="bank_max")
+                if old >= 0:
+                    e_grouped[old] = work.tile([P, KEYS], BF16, align_bytes=64, name="e_grouped")
+                    e_words = words_view(e_grouped[old])
+                for g in range(SEQS):
+                    if new < UNITS:
+                        s_bank = psum.tile([P, TOKENS], F32)
                         nc.tensor.matmul(
                             s_bank[:],
                             lhsT=qT[:, h, qt * P : (qt + 1) * P],
@@ -233,50 +270,69 @@ def tile_sharedattnprocessor_pa_kernel(tc, hidden_states, q, k, ref_key, ref_val
                             stop=True,
                         )
                         nc.vector.tensor_scalar(
-                            out=scores[:, g * TOKENS : (g + 1) * TOKENS], in0=s_bank[:],
+                            out=scores[new][:, g * TOKENS : (g + 1) * TOKENS], in0=s_bank[:],
                             scalar1=SCORE_SCALE, scalar2=None, op0=ALU.mult, op1=ALU.max,
-                            accum_out=bank_max[:, g : g + 1],
+                            accum_out=bank_max[new][:, g : g + 1],
                         )
-                    neg_max = small.tile([P, 1], F32)
-                    nc.vector.tensor_reduce(out=neg_max[:], in_=bank_max[:], axis=AXIS.X, op=ALU.max, negate=True)
+                    if old >= 0:
+                        if g % 2 == 0:
+                            bank = psum.tile([P, 2, HALVES, P], F32, tag="words")
+                        transpose_pass(nc, bank[:, g % 2], e[old][:, g * TOKENS : (g + 1) * TOKENS], ident_f32)
+                        if g % 2 == 1 or g == SEQS - 1:
+                            first = g - g % 2
+                            group_words(nc.scalar.copy, e_words[:, first : g + 1], bank[:, 0 : g + 1 - first])
 
-                    e = work.tile([P, KEYS], BF16)
-                    row_sum = small.tile([P, 1], F32)
-                    nc.scalar.activation(
-                        out=e[:], in_=scores[:], func=ACT.Exp, bias=neg_max[:], scale=1.0, accum_out=row_sum[:]
+            def invert_sum(i):
+                inv_sum[i] = small.tile([P, 1], F32, name="inv_sum")
+                nc.vector.reciprocal(out=inv_sum[i][:], in_=row_sum[i][:])
+
+            def negate_maximum(i):
+                neg_max[i] = small.tile([P, 1], F32, name="neg_max")
+                nc.vector.tensor_reduce(out=neg_max[i][:], in_=bank_max[i][:], axis=AXIS.X, op=ALU.max, negate=True)
+
+            def quantise(i):
+                e_codes[i] = work.tile([P, SEQS * P], U32, align_bytes=64, name="e_codes")
+                e_scales[i] = work.tile([P, SEQS * P], U8, align_bytes=64, name="e_scales")
+                for first, count in ((0, 4), (4, 1)):
+                    cols = slice(first * P, (first + count) * P)
+                    nc.vector.quantize_mx(
+                        out=e_codes[i][:, cols].bitcast(FP8X4),
+                        scales=e_scales[i][:, cols],
+                        in_=e_grouped[i][:, first * P * PACK : (first + count) * P * PACK],
                     )
 
-                    e_grouped = work.tile([P, KEYS], BF16, align_bytes=64)
-                    e_codes = work.tile([P, SEQS * P], U32, align_bytes=64)
-                    e_scales = work.tile([P, SEQS * P], U8, align_bytes=64)
-                    e_words = words_view(e_grouped)
-                    for g0 in range(0, SEQS, 2):
-                        passes = range(g0, min(g0 + 2, SEQS))
-                        blocks = [e[:, g * TOKENS : (g + 1) * TOKENS].bitcast(F32) for g in passes]
-                        transpose_passes(nc, psum, ident_f32, blocks, e_words[:, g0 : g0 + len(blocks)], nc.scalar.copy)
-                    for first, count in ((0, 4), (4, 1)):
-                        cols = slice(first * P, (first + count) * P)
-                        nc.vector.quantize_mx(
-                            out=e_codes[:, cols].bitcast(FP8X4),
-                            scales=e_scales[:, cols],
-                            in_=e_grouped[:, first * P * PACK : (first + count) * P * PACK],
-                        )
-
-                    o_bank = psum.tile([P, HEAD_DIM], F32, tag="mx", bufs=2)
-                    for g in range(SEQS):
-                        nc.tensor.matmul_mx(
-                            out=o_bank[:],
-                            lhsT=e_codes[:, g * P : (g + 1) * P].bitcast(FP8X4),
-                            lhsT_scale=e_scales[:, g * P : (g + 1) * P],
-                            rhs=v_codes[:, g, h * HEAD_DIM : (h + 1) * HEAD_DIM].bitcast(FP8X4),
-                            rhs_scale=v_scales[:, g, h * HEAD_DIM : (h + 1) * HEAD_DIM],
-                            start=(g == 0),
-                            stop=(g == SEQS - 1),
-                        )
-                    inv_sum = small.tile([P, 1], F32)
-                    nc.vector.reciprocal(out=inv_sum[:], in_=row_sum[:])
-                    o = work.tile([P, HEAD_DIM], F32)
-                    nc.vector.tensor_scalar_mul(out=o[:], in0=o_bank[:], scalar1=inv_sum[:])
-                    nc.sync.dma_start(
-                        out=out[0, qt * P : (qt + 1) * P, h * HEAD_DIM : (h + 1) * HEAD_DIM], in_=o[:]
+            def weigh_values(i):
+                h = i // ROW_TILES
+                o_bank[i] = psum.tile([P, HEAD_DIM], F32, name="o_bank", bufs=2)
+                for g in range(SEQS):
+                    nc.tensor.matmul_mx(
+                        out=o_bank[i][:],
+                        lhsT=e_codes[i][:, g * P : (g + 1) * P].bitcast(FP8X4),
+                        lhsT_scale=e_scales[i][:, g * P : (g + 1) * P],
+                        rhs=v_codes[:, g, h * HEAD_DIM : (h + 1) * HEAD_DIM].bitcast(FP8X4),
+                        rhs_scale=v_scales[:, g, h * HEAD_DIM : (h + 1) * HEAD_DIM],
+                        start=(g == 0),
+                        stop=(g == SEQS - 1),
                     )
+
+            def finish(i):
+                h, qt = divmod(i, ROW_TILES)
+                o = work.tile([P, HEAD_DIM], F32)
+                nc.vector.tensor_scalar_mul(out=o[:], in0=o_bank[i][:], scalar1=inv_sum[i][:])
+                nc.sync.dma_start(out=out[0, qt * P : (qt + 1) * P, h * HEAD_DIM : (h + 1) * HEAD_DIM], in_=o[:])
+
+            for i in range(-1, UNITS + 3):
+                if 0 <= i < UNITS:
+                    exponential(i)
+                if 0 <= i - 3 < UNITS:
+                    weigh_values(i - 3)
+                if i + 1 < UNITS or 0 <= i - 1 < UNITS:
+                    scores_and_transposes(i + 1, i - 1 if i - 1 < UNITS else -1)
+                if 0 <= i - 2 < UNITS:
+                    invert_sum(i - 2)
+                if i + 1 < UNITS:
+                    negate_maximum(i + 1)
+                if 0 <= i - 2 < UNITS:
+                    quantise(i - 2)
+                if 0 <= i - 3 < UNITS:
+                    finish(i - 3)

@@ -73,6 +73,7 @@ def tile_sharedattnprocessor_pa_kernel(tc, hidden_states, q, k, ref_key, ref_val
         whole.enter_context(tc.manual_schedule())
         const = whole.enter_context(tc.tile_pool(name="const", bufs=1))
         keep = whole.enter_context(tc.tile_pool(name="keep", bufs=1))
+        key_seqs = whole.enter_context(tc.tile_pool(name="key_seqs", bufs=1))
 
         ident_bf16 = const.tile([P, P], BF16)
         make_identity(nc, ident_bf16[:])
@@ -83,6 +84,11 @@ def tile_sharedattnprocessor_pa_kernel(tc, hidden_states, q, k, ref_key, ref_val
         kT = keep.tile([P, HEADS, KEYS], BF16)
         v_codes = keep.tile([P, SEQS, CHANNELS], U32, align_bytes=64)
         v_scales = keep.tile([P, SEQS, CHANNELS], U8, align_bytes=64)
+
+        def channel_major_home(s, h0):
+            if s == 0:
+                return qT[:, h0 : h0 + PAIR, :]
+            return kT[:, h0 : h0 + PAIR, (s - 1) * TOKENS : s * TOKENS]
 
         with ExitStack() as prepare:
             seqs = prepare.enter_context(tc.tile_pool(name="seqs", bufs=1))
@@ -100,13 +106,13 @@ def tile_sharedattnprocessor_pa_kernel(tc, hidden_states, q, k, ref_key, ref_val
                 for g in range(CH_PASSES):
                     places = slice(g * HALVES, (g + 1) * HALVES)
                     nc.sync.dma_start(out=wv_raw[:, places], in_=wv_rows[:, places])
-                key_side = [load_sequence(nc, seqs, q[0], "queries")]
+                key_side = [load_sequence(nc, key_seqs, q[0], "queries")]
                 values = [load_sequence(nc, seqs, ref_value[0, 0], "values0")]
-                key_side.append(load_sequence(nc, seqs, k[0], "keys"))
+                key_side.append(load_sequence(nc, key_seqs, k[0], "keys"))
                 for n in range(1, REFS):
                     values.append(load_sequence(nc, seqs, ref_value[0, n], "values%d" % n))
-                    key_side.append(load_sequence(nc, seqs, ref_key[0, n - 1], "ref_keys%d" % (n - 1)))
-                key_side.append(load_sequence(nc, seqs, ref_key[0, REFS - 1], "ref_keys%d" % (REFS - 1)))
+                    key_side.append(load_sequence(nc, key_seqs, ref_key[0, n - 1], "ref_keys%d" % (n - 1)))
+                key_side.append(load_sequence(nc, key_seqs, ref_key[0, REFS - 1], "ref_keys%d" % (REFS - 1)))
 
                 hs_grouped = early.tile([P, CH_PASSES * TOKENS * PACK], BF16, align_bytes=64)
                 hs_words = words_view(hs_grouped)
@@ -150,11 +156,9 @@ def tile_sharedattnprocessor_pa_kernel(tc, hidden_states, q, k, ref_key, ref_val
             v_bf16 = stage.tile([P, HEADS, TOKENS], BF16, bufs=1)
             for s in range(SEQS + 1):
                 for h0 in range(0, HEADS, PAIR):
-                    pair = transpose_head_pair(nc, psum, "key_pair", ident_bf16, key_side[s], h0)
-                    if s == 0:
-                        nc.scalar.copy(out=qT[:, h0 : h0 + PAIR, :], in_=pair[:])
-                    else:
-                        nc.scalar.copy(out=kT[:, h0 : h0 + PAIR, (s - 1) * TOKENS : s * TOKENS], in_=pair[:])
+                    if h0 == 0:
+                        pair = transpose_head_pair(nc, psum, "key_pair", ident_bf16, key_side[s], h0)
+                        nc.scalar.copy(out=channel_major_home(s, h0), in_=pair[:])
                     if s == 0:
                         for h in range(h0, h0 + PAIR):
                             vT = psum.tile([P, TOKENS], F32, tag="mx")
@@ -239,9 +243,12 @@ def tile_sharedattnprocessor_pa_kernel(tc, hidden_states, q, k, ref_key, ref_val
         with ExitStack() as attend:
             work = attend.enter_context(tc.tile_pool(name="work", bufs=2, reuse_waits="tile"))
             small = attend.enter_context(tc.tile_pool(name="small", bufs=3, reuse_waits="tile"))
-            psum = attend.enter_context(tc.psum_pool(name="psum_attend", bufs=3, reuse_waits="tile"))
+            psum = attend.enter_context(tc.psum_pool(name="psum_attend", bufs=2, reuse_waits="tile"))
             scores, bank_max, neg_max, e, row_sum, inv_sum = {}, {}, {}, {}, {}, {}
             e_grouped, e_codes, e_scales, o_bank = {}, {}, {}, {}
+
+            def live(unit):
+                return 0 <= unit < UNITS
 
             def exponential(i):
                 e[i] = work.tile([P, KEYS], BF16, name="e")
@@ -251,59 +258,33 @@ def tile_sharedattnprocessor_pa_kernel(tc, hidden_states, q, k, ref_key, ref_val
                     accum_out=row_sum[i][:],
                 )
 
-            def scores_and_transposes(new, old):
-                if new < UNITS:
-                    h, qt = divmod(new, ROW_TILES)
-                    scores[new] = work.tile([P, KEYS], F32, name="scores")
-                    bank_max[new] = small.tile([P, SEQS], F32, name="bank_max")
-                if old >= 0:
-                    e_grouped[old] = work.tile([P, KEYS], BF16, align_bytes=64, name="e_grouped")
-                    e_words = words_view(e_grouped[old])
-                for g in range(SEQS):
-                    if new < UNITS:
-                        s_bank = psum.tile([P, TOKENS], F32)
-                        nc.tensor.matmul(
-                            s_bank[:],
-                            lhsT=qT[:, h, qt * P : (qt + 1) * P],
-                            rhs=kT[:, h, g * TOKENS : (g + 1) * TOKENS],
-                            start=True,
-                            stop=True,
-                        )
-                        nc.vector.tensor_scalar(
-                            out=scores[new][:, g * TOKENS : (g + 1) * TOKENS], in0=s_bank[:],
-                            scalar1=SCORE_SCALE, scalar2=None, op0=ALU.mult, op1=ALU.max,
-                            accum_out=bank_max[new][:, g : g + 1],
-                        )
-                    if old >= 0:
-                        if g % 2 == 0:
-                            bank = psum.tile([P, 2, HALVES, P], F32, tag="words")
-                        transpose_pass(nc, bank[:, g % 2], e[old][:, g * TOKENS : (g + 1) * TOKENS], ident_f32)
-                        if g % 2 == 1 or g == SEQS - 1:
-                            first = g - g % 2
-                            group_words(nc.scalar.copy, e_words[:, first : g + 1], bank[:, 0 : g + 1 - first])
+            def score_bank(i, g):
+                h, qt = divmod(i, ROW_TILES)
+                s_bank = psum.tile([P, TOKENS], F32)
+                nc.tensor.matmul(
+                    s_bank[:],
+                    lhsT=qT[:, h, qt * P : (qt + 1) * P],
+                    rhs=kT[:, h, g * TOKENS : (g + 1) * TOKENS],
+                    start=True,
+                    stop=True,
+                )
+                nc.vector.tensor_scalar(
+                    out=scores[i][:, g * TOKENS : (g + 1) * TOKENS], in0=s_bank[:],
+                    scalar1=SCORE_SCALE, scalar2=None, op0=ALU.mult, op1=ALU.max,
+                    accum_out=bank_max[i][:, g : g + 1],
+                )
 
-            def invert_sum(i):
-                inv_sum[i] = small.tile([P, 1], F32, name="inv_sum")
-                nc.vector.reciprocal(out=inv_sum[i][:], in_=row_sum[i][:])
-
-            def negate_maximum(i):
-                neg_max[i] = small.tile([P, 1], F32, name="neg_max")
-                nc.vector.tensor_reduce(out=neg_max[i][:], in_=bank_max[i][:], axis=AXIS.X, op=ALU.max, negate=True)
-
-            def quantise(i):
-                e_codes[i] = work.tile([P, SEQS * P], U32, align_bytes=64, name="e_codes")
-                e_scales[i] = work.tile([P, SEQS * P], U8, align_bytes=64, name="e_scales")
-                for first, count in ((0, 4), (4, 1)):
-                    cols = slice(first * P, (first + count) * P)
-                    nc.vector.quantize_mx(
-                        out=e_codes[i][:, cols].bitcast(FP8X4),
-                        scales=e_scales[i][:, cols],
-                        in_=e_grouped[i][:, first * P * PACK : (first + count) * P * PACK],
-                    )
+            def quantise(i, first, count):
+                cols = slice(first * P, (first + count) * P)
+                nc.vector.quantize_mx(
+                    out=e_codes[i][:, cols].bitcast(FP8X4),
+                    scales=e_scales[i][:, cols],
+                    in_=e_grouped[i][:, first * P * PACK : (first + count) * P * PACK],
+                )
 
             def weigh_values(i):
                 h = i // ROW_TILES
-                o_bank[i] = psum.tile([P, HEAD_DIM], F32, name="o_bank", bufs=2)
+                o_bank[i] = psum.tile([P, HEAD_DIM], F32, name="o_bank")
                 for g in range(SEQS):
                     nc.tensor.matmul_mx(
                         out=o_bank[i][:],
@@ -321,18 +302,48 @@ def tile_sharedattnprocessor_pa_kernel(tc, hidden_states, q, k, ref_key, ref_val
                 nc.vector.tensor_scalar_mul(out=o[:], in0=o_bank[i][:], scalar1=inv_sum[i][:])
                 nc.sync.dma_start(out=out[0, qt * P : (qt + 1) * P, h * HEAD_DIM : (h + 1) * HEAD_DIM], in_=o[:])
 
+            rounds_of_a_pair = PAIR * ROW_TILES
             for i in range(-1, UNITS + 3):
-                if 0 <= i < UNITS:
+                if live(i):
                     exponential(i)
-                if 0 <= i - 3 < UNITS:
-                    weigh_values(i - 3)
-                if i + 1 < UNITS or 0 <= i - 1 < UNITS:
-                    scores_and_transposes(i + 1, i - 1 if i - 1 < UNITS else -1)
-                if 0 <= i - 2 < UNITS:
-                    invert_sum(i - 2)
-                if i + 1 < UNITS:
-                    negate_maximum(i + 1)
-                if 0 <= i - 2 < UNITS:
-                    quantise(i - 2)
-                if 0 <= i - 3 < UNITS:
-                    finish(i - 3)
+                next_h0 = (i // rounds_of_a_pair + 1) * PAIR
+                s = i % rounds_of_a_pair
+                keys_to_do = live(i) and next_h0 < HEADS and s < len(key_side)
+                if live(i + 1):
+                    scores[i + 1] = work.tile([P, KEYS], F32, name="scores")
+                    bank_max[i + 1] = small.tile([P, SEQS], F32, name="bank_max")
+                if live(i - 1):
+                    e_grouped[i - 1] = work.tile([P, KEYS], BF16, align_bytes=64, name="e_grouped")
+                    e_words = words_view(e_grouped[i - 1])
+                if live(i - 2):
+                    e_codes[i - 2] = work.tile([P, SEQS * P], U32, align_bytes=64, name="e_codes")
+                    e_scales[i - 2] = work.tile([P, SEQS * P], U8, align_bytes=64, name="e_scales")
+                for g in range(SEQS):
+                    if live(i + 1):
+                        score_bank(i + 1, g)
+                    if live(i - 1):
+                        if g % 2 == 0:
+                            bank = psum.tile([P, 2, HALVES, P], F32, tag="words")
+                        transpose_pass(nc, bank[:, g % 2], e[i - 1][:, g * TOKENS : (g + 1) * TOKENS], ident_f32)
+                        if g % 2 == 1 or g == SEQS - 1:
+                            first = g - g % 2
+                            group_words(nc.scalar.copy, e_words[:, first : g + 1], bank[:, 0 : g + 1 - first])
+                    if g == 0 and live(i - 3):
+                        weigh_values(i - 3)
+                    if g == 1 and keys_to_do:
+                        key_pair = transpose_head_pair(nc, psum, "key_pair", ident_bf16, key_side[s], next_h0)
+                    if g == 1 and live(i - 2):
+                        quantise(i - 2, 0, 4)
+                    if g == 2 and live(i - 2):
+                        quantise(i - 2, 4, 1)
+                        inv_sum[i - 2] = small.tile([P, 1], F32, name="inv_sum")
+                        nc.vector.reciprocal(out=inv_sum[i - 2][:], in_=row_sum[i - 2][:])
+                    if g == 3 and keys_to_do:
+                        nc.vector.tensor_copy(out=channel_major_home(s, next_h0), in_=key_pair[:])
+                    if g == 4 and live(i - 3):
+                        finish(i - 3)
+                if live(i + 1):
+                    neg_max[i + 1] = small.tile([P, 1], F32, name="neg_max")
+                    nc.vector.tensor_reduce(
+                        out=neg_max[i + 1][:], in_=bank_max[i + 1][:], axis=AXIS.X, op=ALU.max, negate=True
+                    )

@@ -30,7 +30,8 @@ SCORE_SCALE = HEAD_DIM**-0.5
 UNBIASED = TOKENS / (TOKENS - 1.0)
 SMALLEST_VARIANCE = 1e-30
 
-UNITS = HEADS * ROW_TILES
+REAL_UNITS = HEADS * ROW_TILES
+UNITS = REAL_UNITS + 4
 
 FLOPS = 2 * TOKENS * CHANNELS * CHANNELS + 2 * (2 * HEADS * TOKENS * KEYS * HEAD_DIM)
 
@@ -259,7 +260,7 @@ def tile_sharedattnprocessor_pa_kernel(tc, hidden_states, q, k, ref_key, ref_val
                 )
 
             def score_bank(i, g):
-                h, qt = divmod(i, ROW_TILES)
+                h, qt = divmod(i % REAL_UNITS, ROW_TILES)
                 s_bank = psum.tile([P, TOKENS], F32)
                 nc.tensor.matmul(
                     s_bank[:],
@@ -283,7 +284,7 @@ def tile_sharedattnprocessor_pa_kernel(tc, hidden_states, q, k, ref_key, ref_val
                 )
 
             def weigh_values(i):
-                h = i // ROW_TILES
+                h = (i % REAL_UNITS) // ROW_TILES
                 o_bank[i] = psum.tile([P, HEAD_DIM], F32, name="o_bank")
                 for g in range(SEQS):
                     nc.tensor.matmul_mx(
@@ -297,7 +298,7 @@ def tile_sharedattnprocessor_pa_kernel(tc, hidden_states, q, k, ref_key, ref_val
                     )
 
             def finish(i):
-                h, qt = divmod(i, ROW_TILES)
+                h, qt = divmod(i % REAL_UNITS, ROW_TILES)
                 o = work.tile([P, HEAD_DIM], F32)
                 nc.vector.tensor_scalar_mul(out=o[:], in0=o_bank[i][:], scalar1=inv_sum[i][:])
                 nc.sync.dma_start(out=out[0, qt * P : (qt + 1) * P, h * HEAD_DIM : (h + 1) * HEAD_DIM], in_=o[:])

@@ -23,6 +23,7 @@ KEYS = SEQS * TOKENS
 ROW_TILES = TOKENS // P
 PACK = 4
 PAIR = 2
+QUAD = 4
 HALVES = 2
 CH_PASSES = CHANNELS // TOKENS
 EPS = 1e-5
@@ -30,8 +31,7 @@ SCORE_SCALE = HEAD_DIM**-0.5
 UNBIASED = TOKENS / (TOKENS - 1.0)
 SMALLEST_VARIANCE = 1e-30
 
-REAL_UNITS = HEADS * ROW_TILES
-UNITS = REAL_UNITS + 4
+UNITS = HEADS * ROW_TILES
 
 FLOPS = 2 * TOKENS * CHANNELS * CHANNELS + 2 * (2 * HEADS * TOKENS * KEYS * HEAD_DIM)
 
@@ -56,8 +56,8 @@ def group_words(copy, grouped_words, bank):
     copy(out=grouped_words, in_=bank.rearrange("p b u r -> p b r u"))
 
 
-def transpose_head_pair(nc, psum, tag, ident_bf16, seq, h0):
-    pair = psum.tile([P, PAIR, TOKENS], BF16, tag=tag)
+def transpose_head_pair(nc, psum, tag, bufs, ident_bf16, seq, h0):
+    pair = psum.tile([P, PAIR, TOKENS], BF16, tag=tag, bufs=bufs)
     for j in range(PAIR):
         for r in range(ROW_TILES):
             nc.tensor.transpose(
@@ -92,13 +92,70 @@ def tile_sharedattnprocessor_pa_kernel(tc, hidden_states, q, k, ref_key, ref_val
             return kT[:, h0 : h0 + PAIR, (s - 1) * TOKENS : s * TOKENS]
 
         with ExitStack() as prepare:
-            seqs = prepare.enter_context(tc.tile_pool(name="seqs", bufs=1))
+            value_seqs = prepare.enter_context(tc.tile_pool(name="value_seqs", bufs=1))
             stats = prepare.enter_context(tc.tile_pool(name="stats", bufs=1))
             psum = prepare.enter_context(tc.psum_pool(name="psum_prepare", bufs=2))
             hs_codes = stats.tile([P, CH_PASSES * TOKENS], U32, align_bytes=64)
             hs_scales = stats.tile([P, CH_PASSES * TOKENS], U8, align_bytes=64)
             wv_codes = stats.tile([P, CH_PASSES * CHANNELS], U32, align_bytes=64)
             wv_scales = stats.tile([P, CH_PASSES * CHANNELS], U8, align_bytes=64)
+            six = stats.tile([P, SEQS, HEADS, 6], F32)
+            mean_var = stats.tile([P, SEQS, HEADS, 2], F32)
+            value_pairs, root, gain, shift, rv_bf16, v_grouped = {}, {}, {}, {}, {}, {}
+
+            def place(st):
+                return st // 2, QUAD * (st % 2)
+
+            def transpose_values(st):
+                n, h0 = place(st)
+                value_pairs[st] = [
+                    transpose_head_pair(nc, psum, "values", 6, ident_bf16, values[n], h0 + PAIR * b)
+                    for b in range(QUAD // PAIR)
+                ]
+
+            def measure_calls(st):
+                n, h0 = place(st)
+                root[st] = stats.tile([P, QUAD], F32, name="root", bufs=3)
+                calls = []
+                for j in range(QUAD):
+                    calls.append(
+                        lambda j=j: nc.vector.bn_stats(
+                            out=six[:, n + 1, h0 + j, :], in_=value_pairs[st][j // PAIR][:, j % PAIR, :]
+                        )
+                    )
+                for j in range(QUAD):
+                    calls.append(
+                        lambda j=j: nc.vector.bn_aggr(out=mean_var[:, n + 1, h0 + j, :], in_=six[:, n + 1, h0 + j, :])
+                    )
+                return calls
+
+            def unbiased_variance(out, variances):
+                nc.vector.tensor_scalar(
+                    out=out, in0=variances, scalar1=UNBIASED, scalar2=SMALLEST_VARIANCE, op0=ALU.mult, op1=ALU.max
+                )
+
+            def factor_calls(st):
+                n, h0 = place(st)
+                quad = slice(h0, h0 + QUAD)
+                gain[st] = stats.tile([P, QUAD], F32, name="gain", bufs=3)
+                shift[st] = stats.tile([P, QUAD], F32, name="shift", bufs=3)
+                return [
+                    lambda: nc.vector.tensor_scalar_add(out=root[st][:], in0=root[st][:], scalar1=EPS),
+                    lambda: nc.vector.reciprocal(out=gain[st][:], in_=root[st][:]),
+                    lambda: nc.vector.tensor_mul(out=gain[st][:], in0=gain[st][:], in1=style_std[:, quad]),
+                    lambda: nc.vector.tensor_mul(out=shift[st][:], in0=mean_var[:, n + 1, quad, 0], in1=gain[st][:]),
+                    lambda: nc.vector.tensor_sub(out=shift[st][:], in0=mean_var[:, 0, quad, 0], in1=shift[st][:]),
+                ]
+
+            def deal(independent, chain):
+                dealt = 0
+                for number, call in enumerate(independent):
+                    call()
+                    if number % 2 == 1 and dealt < len(chain):
+                        chain[dealt]()
+                        dealt += 1
+                for call in chain[dealt:]:
+                    call()
 
             with tc.tile_pool(name="early", bufs=1) as early:
                 hs = load_sequence(nc, early, hidden_states[0], "hs")
@@ -107,139 +164,126 @@ def tile_sharedattnprocessor_pa_kernel(tc, hidden_states, q, k, ref_key, ref_val
                 for g in range(CH_PASSES):
                     places = slice(g * HALVES, (g + 1) * HALVES)
                     nc.sync.dma_start(out=wv_raw[:, places], in_=wv_rows[:, places])
-                key_side = [load_sequence(nc, key_seqs, q[0], "queries")]
-                values = [load_sequence(nc, seqs, ref_value[0, 0], "values0")]
-                key_side.append(load_sequence(nc, key_seqs, k[0], "keys"))
+                values = [load_sequence(nc, value_seqs, ref_value[0, 0], "values0")]
+                key_side = [load_sequence(nc, key_seqs, q[0], "queries"), load_sequence(nc, key_seqs, k[0], "keys")]
+                for n in range(REFS):
+                    key_side.append(load_sequence(nc, key_seqs, ref_key[0, n], "ref_keys%d" % n))
                 for n in range(1, REFS):
-                    values.append(load_sequence(nc, seqs, ref_value[0, n], "values%d" % n))
-                    key_side.append(load_sequence(nc, key_seqs, ref_key[0, n - 1], "ref_keys%d" % (n - 1)))
-                key_side.append(load_sequence(nc, key_seqs, ref_key[0, REFS - 1], "ref_keys%d" % (REFS - 1)))
+                    values.append(load_sequence(nc, value_seqs, ref_value[0, n], "values%d" % n))
 
                 hs_grouped = early.tile([P, CH_PASSES * TOKENS * PACK], BF16, align_bytes=64)
                 hs_words = words_view(hs_grouped)
                 for g in range(CH_PASSES):
                     for r in range(0, ROW_TILES, 2):
-                        bank = psum.tile([P, 2, HALVES, P], F32, tag="words")
+                        bank = psum.tile([P, 2, HALVES, P], F32, tag="short")
                         for j in range(2):
                             transpose_pass(nc, bank[:, j], hs[:, r + j, g * TOKENS : (g + 1) * TOKENS], ident_f32)
                         b0 = g * ROW_TILES + r
                         group_words(nc.scalar.copy, hs_words[:, b0 : b0 + 2], bank[:])
+                nc.vector.quantize_mx(out=hs_codes[:].bitcast(FP8X4), scales=hs_scales[:], in_=hs_grouped[:])
 
-                chunks = [(g, half) for g in range(CH_PASSES) for half in range(2)]
-                wv_grouped = {}
-
-                def quantise_wv(c):
-                    g, half = chunks[c]
-                    words = slice(g * CHANNELS + half * TOKENS, g * CHANNELS + (half + 1) * TOKENS)
-                    nc.vector.quantize_mx(
-                        out=wv_codes[:, words].bitcast(FP8X4),
-                        scales=wv_scales[:, words],
-                        in_=wv_grouped[c][:].rearrange("p c t -> p (c t)"),
-                    )
-
-                for c, (g, half) in enumerate(chunks):
+                transpose_values(0)
+                transpose_values(1)
+                for g in range(CH_PASSES):
                     four_rows = wv_raw[:, g * HALVES : (g + 1) * HALVES].rearrange("p a e c -> p (a e) c")
-                    wv_grouped[c] = early.tile([P, TOKENS, PACK], BF16, align_bytes=64, name="wv_grouped", bufs=2)
-                    nc.vector.tensor_copy(
-                        out=wv_grouped[c][:].rearrange("p (c i) t -> p c t i", i=4),
-                        in_=four_rows[:, :, half * TOKENS : (half + 1) * TOKENS].rearrange("p t (c i) -> p c t i", i=4),
-                    )
-                    if c == 0:
-                        nc.vector.quantize_mx(out=hs_codes[:].bitcast(FP8X4), scales=hs_scales[:], in_=hs_grouped[:])
-                    else:
-                        quantise_wv(c - 1)
-                quantise_wv(len(chunks) - 1)
+                    for half in range(2):
+                        wv_grouped = early.tile([P, TOKENS, PACK], BF16, align_bytes=64, bufs=4)
+                        nc.scalar.copy(
+                            out=wv_grouped[:].rearrange("p (c i) t -> p c t i", i=4),
+                            in_=four_rows[:, :, half * TOKENS : (half + 1) * TOKENS].rearrange(
+                                "p t (c i) -> p c t i", i=4
+                            ),
+                        )
+                        words = slice(g * CHANNELS + half * TOKENS, g * CHANNELS + (half + 1) * TOKENS)
+                        nc.vector.quantize_mx(
+                            out=wv_codes[:, words].bitcast(FP8X4),
+                            scales=wv_scales[:, words],
+                            in_=wv_grouped[:].rearrange("p c t -> p (c t)"),
+                        )
+                    deal(measure_calls(g), [])
+                    unbiased_variance(root[g][:], mean_var[:, 1, QUAD * g : QUAD * (g + 1), 1])
 
             stage = prepare.enter_context(tc.tile_pool(name="stage", bufs=3, reuse_waits="tile"))
 
-            six = stats.tile([P, SEQS, HEADS, 6], F32)
-            mean_var = stats.tile([P, SEQS, HEADS, 2], F32)
+            def key_job(s):
+                pair = transpose_head_pair(nc, psum, "short", 2, ident_bf16, key_side[s], 0)
+                nc.scalar.copy(out=channel_major_home(s, 0), in_=pair[:])
+
+            key_job(0)
+            key_job(1)
             v_bf16 = stage.tile([P, HEADS, TOKENS], BF16, bufs=1)
-            for s in range(SEQS + 1):
-                for h0 in range(0, HEADS, PAIR):
-                    if h0 == 0:
-                        pair = transpose_head_pair(nc, psum, "key_pair", ident_bf16, key_side[s], h0)
-                        nc.scalar.copy(out=channel_major_home(s, h0), in_=pair[:])
-                    if s == 0:
-                        for h in range(h0, h0 + PAIR):
-                            vT = psum.tile([P, TOKENS], F32, tag="mx")
-                            for g in range(CH_PASSES):
-                                w_cols = slice(g * CHANNELS + h * HEAD_DIM, g * CHANNELS + (h + 1) * HEAD_DIM)
-                                t_cols = slice(g * TOKENS, (g + 1) * TOKENS)
-                                nc.tensor.matmul_mx(
-                                    out=vT[:],
-                                    lhsT=wv_codes[:, w_cols].bitcast(FP8X4),
-                                    lhsT_scale=wv_scales[:, w_cols],
-                                    rhs=hs_codes[:, t_cols].bitcast(FP8X4),
-                                    rhs_scale=hs_scales[:, t_cols],
-                                    start=(g == 0),
-                                    stop=(g == CH_PASSES - 1),
-                                )
-                            nc.vector.bn_stats(out=six[:, 0, h, :], in_=vT[:])
-                            nc.scalar.copy(out=v_bf16[:, h, :], in_=vT[:])
-                    elif s <= REFS:
-                        pair = transpose_head_pair(nc, psum, "value_pair", ident_bf16, values[s - 1], h0)
-                        for j in range(PAIR):
-                            nc.vector.bn_stats(out=six[:, s, h0 + j, :], in_=pair[:, j, :])
-                    if s <= REFS:
-                        for h in range(h0, h0 + PAIR):
-                            nc.vector.bn_aggr(out=mean_var[:, s, h, :], in_=six[:, s, h, :])
+            for h in range(HEADS):
+                vT = psum.tile([P, TOKENS], F32, tag="short")
+                for g in range(CH_PASSES):
+                    w_cols = slice(g * CHANNELS + h * HEAD_DIM, g * CHANNELS + (h + 1) * HEAD_DIM)
+                    t_cols = slice(g * TOKENS, (g + 1) * TOKENS)
+                    nc.tensor.matmul_mx(
+                        out=vT[:],
+                        lhsT=wv_codes[:, w_cols].bitcast(FP8X4),
+                        lhsT_scale=wv_scales[:, w_cols],
+                        rhs=hs_codes[:, t_cols].bitcast(FP8X4),
+                        rhs_scale=hs_scales[:, t_cols],
+                        start=(g == 0),
+                        stop=(g == CH_PASSES - 1),
+                    )
+                nc.vector.bn_stats(out=six[:, 0, h, :], in_=vT[:])
+                nc.scalar.copy(out=v_bf16[:, h, :], in_=vT[:])
+            for h in range(HEADS):
+                nc.vector.bn_aggr(out=mean_var[:, 0, h, :], in_=six[:, 0, h, :])
+            style_std = stats.tile([P, HEADS], F32)
+            unbiased_variance(style_std[:], mean_var[:, 0, :, 1])
+            nc.scalar.activation(out=style_std[:], in_=style_std[:], func=ACT.Sqrt)
+            for s in range(2, len(key_side)):
+                key_job(s)
+            nc.vector.tensor_scalar_add(out=style_std[:], in0=style_std[:], scalar1=EPS)
 
-            std = stats.tile([P, SEQS, HEADS], F32)
-            gain = stats.tile([P, REFS, HEADS], F32)
-            shift = stats.tile([P, REFS, HEADS], F32)
-            nc.vector.tensor_scalar(
-                out=std[:], in0=mean_var[:, :, :, 1], scalar1=UNBIASED, scalar2=SMALLEST_VARIANCE,
-                op0=ALU.mult, op1=ALU.max,
-            )
-            nc.scalar.activation(out=std[:], in_=std[:], func=ACT.Sqrt)
-            nc.vector.tensor_scalar_add(out=std[:], in0=std[:], scalar1=EPS)
-            nc.vector.reciprocal(out=gain[:], in_=std[:, 1:, :])
-            nc.vector.tensor_mul(out=gain[:], in0=gain[:], in1=std[:, 0:1, :].to_broadcast([P, REFS, HEADS]))
-            nc.vector.tensor_mul(out=shift[:], in0=mean_var[:, 1:, :, 0], in1=gain[:])
-            nc.vector.tensor_sub(
-                out=shift[:], in0=mean_var[:, 0:1, :, 0].to_broadcast([P, REFS, HEADS]), in1=shift[:]
-            )
+            def channel_major(st):
+                return v_bf16[:, QUAD * (st + 2) : QUAD * (st + 3), :] if st < 0 else rv_bf16[st][:]
 
-            jobs = [(g, h0) for g in range(SEQS) for h0 in range(0, HEADS, PAIR)]
+            def adain(st):
+                rv_bf16[st] = stage.tile([P, QUAD, TOKENS], BF16, name="rv_bf16")
+                for j in range(QUAD):
+                    nc.scalar.activation(
+                        out=rv_bf16[st][:, j, :], in_=value_pairs[st][j // PAIR][:, j % PAIR, :], func=ACT.Identity,
+                        scale=gain[st][:, j : j + 1], bias=shift[st][:, j : j + 1],
+                    )
 
-            def fill(job):
-                g, h0 = job
-                return transpose_head_pair(nc, psum, "value_pair", ident_bf16, values[g - 1], h0) if g > 0 else None
+            def keys_to_partitions(st):
+                v_grouped[st] = stage.tile([P, QUAD * HEAD_DIM * PACK], BF16, align_bytes=64, name="v_grouped")
+                for j0 in range(0, QUAD, PAIR):
+                    bank = psum.tile([P, PAIR, HALVES, P], F32, tag="short")
+                    for j in range(PAIR):
+                        transpose_pass(nc, bank[:, j], channel_major(st)[:, j0 + j, :], ident_f32)
+                    group_words(nc.scalar.copy, words_view(v_grouped[st])[:, j0 : j0 + PAIR], bank[:])
 
-            def quantise_quad(g, quad, v_grouped):
-                cols = slice(quad * HEAD_DIM, (quad + 4) * HEAD_DIM)
+            def quantise_values(st):
+                g, h0 = (0, QUAD * (st + 2)) if st < 0 else (st // 2 + 1, QUAD * (st % 2))
+                cols = slice(h0 * HEAD_DIM, (h0 + QUAD) * HEAD_DIM)
                 nc.vector.quantize_mx(
-                    out=v_codes[:, g, cols].bitcast(FP8X4), scales=v_scales[:, g, cols], in_=v_grouped[:]
+                    out=v_codes[:, g, cols].bitcast(FP8X4), scales=v_scales[:, g, cols], in_=v_grouped[st][:]
                 )
 
-            waiting = None
-            pair = fill(jobs[0])
-            for number, (g, h0) in enumerate(jobs):
-                next_pair = fill(jobs[number + 1]) if number + 1 < len(jobs) else None
-                if g == 0:
-                    channel_major = v_bf16[:, h0 : h0 + PAIR, :]
-                else:
-                    rv_bf16 = stage.tile([P, PAIR, TOKENS], BF16)
-                    for j in range(PAIR):
-                        nc.scalar.activation(
-                            out=rv_bf16[:, j, :], in_=pair[:, j, :], func=ACT.Identity,
-                            scale=gain[:, g - 1, h0 + j : h0 + j + 1], bias=shift[:, g - 1, h0 + j : h0 + j + 1],
-                        )
-                    channel_major = rv_bf16[:]
-                quad = h0 - h0 % 4
-                if h0 == quad:
-                    v_grouped = stage.tile([P, 4 * HEAD_DIM * PACK], BF16, align_bytes=64)
-                bank = psum.tile([P, PAIR, HALVES, P], F32, tag="words")
-                for j in range(PAIR):
-                    transpose_pass(nc, bank[:, j], channel_major[:, j, :], ident_f32)
-                group_words(nc.vector.tensor_copy, words_view(v_grouped)[:, h0 - quad : h0 - quad + PAIR], bank[:])
-                if h0 != quad:
-                    if waiting is not None:
-                        quantise_quad(*waiting)
-                    waiting = (g, quad, v_grouped)
-                pair = next_pair
-            quantise_quad(*waiting)
+            steps = REFS * HEADS // QUAD
+            for st in range(-1, steps + 2):
+                independent, chain = [], []
+                if 2 <= st + 2 < steps:
+                    transpose_values(st + 2)
+                    independent = measure_calls(st + 2)
+                if 0 <= st + 1 < steps:
+                    nc.scalar.activation(out=root[st + 1][:], in_=root[st + 1][:], func=ACT.Sqrt)
+                    chain = factor_calls(st + 1)
+                if 0 <= st < steps:
+                    adain(st)
+                if -2 <= st - 1 < steps:
+                    keys_to_partitions(st - 1)
+                if -2 <= st - 2 < steps:
+                    independent.append(lambda: quantise_values(st - 2))
+                if 2 <= st + 2 < steps:
+                    n, h0 = place(st + 2)
+                    independent.append(
+                        lambda: unbiased_variance(root[st + 2][:], mean_var[:, n + 1, h0 : h0 + QUAD, 1])
+                    )
+                deal(independent, chain)
 
         with ExitStack() as attend:
             work = attend.enter_context(tc.tile_pool(name="work", bufs=2, reuse_waits="tile"))
@@ -260,7 +304,7 @@ def tile_sharedattnprocessor_pa_kernel(tc, hidden_states, q, k, ref_key, ref_val
                 )
 
             def score_bank(i, g):
-                h, qt = divmod(i % REAL_UNITS, ROW_TILES)
+                h, qt = divmod(i, ROW_TILES)
                 s_bank = psum.tile([P, TOKENS], F32)
                 nc.tensor.matmul(
                     s_bank[:],
@@ -284,7 +328,7 @@ def tile_sharedattnprocessor_pa_kernel(tc, hidden_states, q, k, ref_key, ref_val
                 )
 
             def weigh_values(i):
-                h = (i % REAL_UNITS) // ROW_TILES
+                h = i // ROW_TILES
                 o_bank[i] = psum.tile([P, HEAD_DIM], F32, name="o_bank")
                 for g in range(SEQS):
                     nc.tensor.matmul_mx(
@@ -298,7 +342,7 @@ def tile_sharedattnprocessor_pa_kernel(tc, hidden_states, q, k, ref_key, ref_val
                     )
 
             def finish(i):
-                h, qt = divmod(i % REAL_UNITS, ROW_TILES)
+                h, qt = divmod(i, ROW_TILES)
                 o = work.tile([P, HEAD_DIM], F32)
                 nc.vector.tensor_scalar_mul(out=o[:], in0=o_bank[i][:], scalar1=inv_sum[i][:])
                 nc.sync.dma_start(out=out[0, qt * P : (qt + 1) * P, h * HEAD_DIM : (h + 1) * HEAD_DIM], in_=o[:])
@@ -311,7 +355,7 @@ def tile_sharedattnprocessor_pa_kernel(tc, hidden_states, q, k, ref_key, ref_val
                 s = i % rounds_of_a_pair
                 keys_to_do = live(i) and next_h0 < HEADS and s < len(key_side)
                 if live(i + 1):
-                    scores[i + 1] = work.tile([P, KEYS], F32, name="scores")
+                    scores[i + 1] = work.tile([P, KEYS], F32, name="scores", bufs=3)
                     bank_max[i + 1] = small.tile([P, SEQS], F32, name="bank_max")
                 if live(i - 1):
                     e_grouped[i - 1] = work.tile([P, KEYS], BF16, align_bytes=64, name="e_grouped")
@@ -324,25 +368,27 @@ def tile_sharedattnprocessor_pa_kernel(tc, hidden_states, q, k, ref_key, ref_val
                         score_bank(i + 1, g)
                     if live(i - 1):
                         if g % 2 == 0:
-                            bank = psum.tile([P, 2, HALVES, P], F32, tag="words")
+                            bank = psum.tile([P, 2, HALVES, P], F32, tag="words", bufs=3)
                         transpose_pass(nc, bank[:, g % 2], e[i - 1][:, g * TOKENS : (g + 1) * TOKENS], ident_f32)
-                        if g % 2 == 1 or g == SEQS - 1:
-                            first = g - g % 2
-                            group_words(nc.scalar.copy, e_words[:, first : g + 1], bank[:, 0 : g + 1 - first])
-                    if g == 0 and live(i - 3):
+                        if g % 2 == 1:
+                            group_words(nc.scalar.copy, e_words[:, g - 1 : g + 1], bank[:])
+                        if g == SEQS - 1:
+                            copy = nc.scalar.copy if keys_to_do else nc.vector.tensor_copy
+                            group_words(copy, e_words[:, g : g + 1], bank[:, 0:1])
+                    if g == 2 and live(i - 3):
                         weigh_values(i - 3)
-                    if g == 1 and keys_to_do:
-                        key_pair = transpose_head_pair(nc, psum, "key_pair", ident_bf16, key_side[s], next_h0)
-                    if g == 1 and live(i - 2):
+                    if g == 3 and keys_to_do:
+                        key_pair = transpose_head_pair(nc, psum, "key_pair", 1, ident_bf16, key_side[s], next_h0)
+                    if g == 0 and live(i - 2):
                         quantise(i - 2, 0, 4)
-                    if g == 2 and live(i - 2):
+                    if g == 1 and live(i - 2):
                         quantise(i - 2, 4, 1)
                         inv_sum[i - 2] = small.tile([P, 1], F32, name="inv_sum")
                         nc.vector.reciprocal(out=inv_sum[i - 2][:], in_=row_sum[i - 2][:])
-                    if g == 3 and keys_to_do:
-                        nc.vector.tensor_copy(out=channel_major_home(s, next_h0), in_=key_pair[:])
-                    if g == 4 and live(i - 3):
+                    if g == 3 and live(i - 3):
                         finish(i - 3)
+                    if g == 4 and keys_to_do:
+                        nc.vector.tensor_copy(out=channel_major_home(s, next_h0), in_=key_pair[:])
                 if live(i + 1):
                     neg_max[i + 1] = small.tile([P, 1], F32, name="neg_max")
                     nc.vector.tensor_reduce(

@@ -101,107 +101,133 @@ def tile_sharedattnprocessor_pa_kernel(tc, hidden_states, q, k, ref_key, ref_val
             wv_scales = stats.tile([P, CH_PASSES * CHANNELS], U8, align_bytes=64)
             six = stats.tile([P, SEQS, HEADS, 6], F32)
             mean_var = stats.tile([P, SEQS, HEADS, 2], F32)
-            value_pairs, root, gain, shift, rv_bf16, v_grouped = {}, {}, {}, {}, {}, {}
+            table_probe = stats.tile([P, 1], F32)
+            nc.gpsimd.memset(table_probe[:], 1.0)
+            nc.scalar.activation(out=table_probe[:], in_=table_probe[:], func=ACT.Sqrt)
+            value_pairs, std, gain, shift, rv_bf16, v_grouped = {}, {}, {}, {}, {}, {}
+
+            steps = REFS * HEADS // QUAD
 
             def place(st):
                 return st // 2, QUAD * (st % 2)
 
             def transpose_values(st):
                 n, h0 = place(st)
+                tag, bufs = ("third", 2) if st % 3 == 2 else ("values", 4)
                 value_pairs[st] = [
-                    transpose_head_pair(nc, psum, "values", 6, ident_bf16, values[n], h0 + PAIR * b)
+                    transpose_head_pair(nc, psum, tag, bufs, ident_bf16, values[n], h0 + PAIR * b)
                     for b in range(QUAD // PAIR)
                 ]
 
-            def measure_calls(st):
+            def measure(st):
                 n, h0 = place(st)
-                root[st] = stats.tile([P, QUAD], F32, name="root", bufs=3)
-                calls = []
                 for j in range(QUAD):
-                    calls.append(
-                        lambda j=j: nc.vector.bn_stats(
-                            out=six[:, n + 1, h0 + j, :], in_=value_pairs[st][j // PAIR][:, j % PAIR, :]
-                        )
+                    nc.vector.bn_stats(
+                        out=six[:, n + 1, h0 + j, :], in_=value_pairs[st][j // PAIR][:, j % PAIR, :]
                     )
-                for j in range(QUAD):
-                    calls.append(
-                        lambda j=j: nc.vector.bn_aggr(out=mean_var[:, n + 1, h0 + j, :], in_=six[:, n + 1, h0 + j, :])
-                    )
-                return calls
+
+            def aggregate(seq, h0, heads):
+                for h in range(h0, h0 + heads):
+                    nc.vector.bn_aggr(out=mean_var[:, seq, h, :], in_=six[:, seq, h, :])
+
+            def variance(st):
+                n, h0 = place(st)
+                std[st] = stats.tile([P, QUAD], F32, name="std", bufs=3)
+                unbiased_variance(std[st][:], mean_var[:, n + 1, h0 : h0 + QUAD, 1])
 
             def unbiased_variance(out, variances):
-                nc.vector.tensor_scalar(
+                nc.gpsimd.tensor_scalar(
                     out=out, in0=variances, scalar1=UNBIASED, scalar2=SMALLEST_VARIANCE, op0=ALU.mult, op1=ALU.max
                 )
 
-            def factor_calls(st):
+            def root(tile):
+                nc.scalar.activation(out=tile[:], in_=tile[:], func=ACT.Sqrt)
+                nc.gpsimd.tensor_scalar(out=tile[:], in0=tile[:], scalar1=EPS, scalar2=None, op0=ALU.add)
+
+            def factors(st):
                 n, h0 = place(st)
                 quad = slice(h0, h0 + QUAD)
                 gain[st] = stats.tile([P, QUAD], F32, name="gain", bufs=3)
                 shift[st] = stats.tile([P, QUAD], F32, name="shift", bufs=3)
-                return [
-                    lambda: nc.vector.tensor_scalar_add(out=root[st][:], in0=root[st][:], scalar1=EPS),
-                    lambda: nc.vector.reciprocal(out=gain[st][:], in_=root[st][:]),
-                    lambda: nc.vector.tensor_mul(out=gain[st][:], in0=gain[st][:], in1=style_std[:, quad]),
-                    lambda: nc.vector.tensor_mul(out=shift[st][:], in0=mean_var[:, n + 1, quad, 0], in1=gain[st][:]),
-                    lambda: nc.vector.tensor_sub(out=shift[st][:], in0=mean_var[:, 0, quad, 0], in1=shift[st][:]),
-                ]
-
-            def deal(independent, chain):
-                dealt = 0
-                for number, call in enumerate(independent):
-                    call()
-                    if number % 2 == 1 and dealt < len(chain):
-                        chain[dealt]()
-                        dealt += 1
-                for call in chain[dealt:]:
-                    call()
+                inverse = stats.tile([P, QUAD], F32, name="inverse", bufs=3)
+                nc.vector.reciprocal(out=inverse[:], in_=std[st][:])
+                nc.gpsimd.tensor_tensor(out=gain[st][:], in0=inverse[:], in1=style_std[:, quad], op=ALU.mult)
+                nc.gpsimd.tensor_tensor(
+                    out=shift[st][:], in0=mean_var[:, n + 1, quad, 0], in1=gain[st][:], op=ALU.mult
+                )
+                nc.gpsimd.tensor_tensor(
+                    out=shift[st][:], in0=mean_var[:, 0, quad, 0], in1=shift[st][:], op=ALU.subtract
+                )
 
             with tc.tile_pool(name="early", bufs=1) as early:
-                hs = load_sequence(nc, early, hidden_states[0], "hs")
+                values = [value_seqs.tile([P, ROW_TILES, CHANNELS], BF16, name="values0")]
+                first_rows = ref_value[0, 0].rearrange("(r p) c -> p r c", p=P)
+                for half in range(2):
+                    cols = slice(half * TOKENS, (half + 1) * TOKENS)
+                    nc.sync.dma_start(out=values[0][:, :, cols], in_=first_rows[:, :, cols])
+                hs = early.tile([P, ROW_TILES, CHANNELS], BF16)
+                hs_rows = hidden_states[0].rearrange("(r p) c -> p r c", p=P)
+                for r in range(ROW_TILES):
+                    nc.sync.dma_start(out=hs[:, r, :], in_=hs_rows[:, r, :])
                 wv_raw = early.tile([P, CH_PASSES * HALVES, 2, CHANNELS], BF16)
                 wv_rows = Wv.rearrange("(a p e) c -> p a e c", p=P, e=2)
                 for g in range(CH_PASSES):
                     places = slice(g * HALVES, (g + 1) * HALVES)
                     nc.sync.dma_start(out=wv_raw[:, places], in_=wv_rows[:, places])
-                values = [load_sequence(nc, value_seqs, ref_value[0, 0], "values0")]
+                values.append(load_sequence(nc, value_seqs, ref_value[0, 1], "values1"))
                 key_side = [load_sequence(nc, key_seqs, q[0], "queries"), load_sequence(nc, key_seqs, k[0], "keys")]
-                for n in range(REFS):
-                    key_side.append(load_sequence(nc, key_seqs, ref_key[0, n], "ref_keys%d" % n))
-                for n in range(1, REFS):
-                    values.append(load_sequence(nc, value_seqs, ref_value[0, n], "values%d" % n))
+                key_side.append(load_sequence(nc, key_seqs, ref_key[0, 0], "ref_keys0"))
+                values.append(load_sequence(nc, value_seqs, ref_value[0, 2], "values2"))
+                key_side.append(load_sequence(nc, key_seqs, ref_key[0, 1], "ref_keys1"))
+                values.append(load_sequence(nc, value_seqs, ref_value[0, 3], "values3"))
+                key_side.append(load_sequence(nc, key_seqs, ref_key[0, 2], "ref_keys2"))
+                key_side.append(load_sequence(nc, key_seqs, ref_key[0, 3], "ref_keys3"))
 
+                transpose_values(0)
+                measure(0)
+                transpose_values(1)
+                measure(1)
+                aggregate(1, 0, HEADS)
                 hs_grouped = early.tile([P, CH_PASSES * TOKENS * PACK], BF16, align_bytes=64)
                 hs_words = words_view(hs_grouped)
-                for g in range(CH_PASSES):
-                    for r in range(0, ROW_TILES, 2):
+                for r in range(0, ROW_TILES, 2):
+                    for g in range(CH_PASSES):
                         bank = psum.tile([P, 2, HALVES, P], F32, tag="short")
                         for j in range(2):
                             transpose_pass(nc, bank[:, j], hs[:, r + j, g * TOKENS : (g + 1) * TOKENS], ident_f32)
                         b0 = g * ROW_TILES + r
                         group_words(nc.scalar.copy, hs_words[:, b0 : b0 + 2], bank[:])
-                nc.vector.quantize_mx(out=hs_codes[:].bitcast(FP8X4), scales=hs_scales[:], in_=hs_grouped[:])
+                for st in range(2):
+                    variance(st)
+                    root(std[st])
 
-                transpose_values(0)
-                transpose_values(1)
-                for g in range(CH_PASSES):
+                wv_grouped = {}
+
+                def group_weights(copy, g, half):
                     four_rows = wv_raw[:, g * HALVES : (g + 1) * HALVES].rearrange("p a e c -> p (a e) c")
-                    for half in range(2):
-                        wv_grouped = early.tile([P, TOKENS, PACK], BF16, align_bytes=64, bufs=4)
-                        nc.scalar.copy(
-                            out=wv_grouped[:].rearrange("p (c i) t -> p c t i", i=4),
-                            in_=four_rows[:, :, half * TOKENS : (half + 1) * TOKENS].rearrange(
-                                "p t (c i) -> p c t i", i=4
-                            ),
-                        )
-                        words = slice(g * CHANNELS + half * TOKENS, g * CHANNELS + (half + 1) * TOKENS)
-                        nc.vector.quantize_mx(
-                            out=wv_codes[:, words].bitcast(FP8X4),
-                            scales=wv_scales[:, words],
-                            in_=wv_grouped[:].rearrange("p c t -> p (c t)"),
-                        )
-                    deal(measure_calls(g), [])
-                    unbiased_variance(root[g][:], mean_var[:, 1, QUAD * g : QUAD * (g + 1), 1])
+                    wv_grouped[g, half] = early.tile([P, TOKENS, PACK], BF16, align_bytes=64, bufs=4, name="wv_grouped")
+                    copy(
+                        out=wv_grouped[g, half][:].rearrange("p (c i) t -> p c t i", i=4),
+                        in_=four_rows[:, :, half * TOKENS : (half + 1) * TOKENS].rearrange("p t (c i) -> p c t i", i=4),
+                    )
+
+                def quantise_weights(g, half):
+                    words = slice(g * CHANNELS + half * TOKENS, g * CHANNELS + (half + 1) * TOKENS)
+                    nc.vector.quantize_mx(
+                        out=wv_codes[:, words].bitcast(FP8X4),
+                        scales=wv_scales[:, words],
+                        in_=wv_grouped[g, half][:].rearrange("p c t -> p (c t)"),
+                    )
+
+                for g in range(CH_PASSES):
+                    group_weights(nc.scalar.copy, g, 0)
+                    group_weights(nc.vector.tensor_copy, g, 1)
+                    if g == 0:
+                        nc.vector.quantize_mx(out=hs_codes[:].bitcast(FP8X4), scales=hs_scales[:], in_=hs_grouped[:])
+                        quantise_weights(0, 1)
+                for g in range(CH_PASSES):
+                    quantise_weights(g, 0)
+                quantise_weights(1, 1)
 
             stage = prepare.enter_context(tc.tile_pool(name="stage", bufs=3, reuse_waits="tile"))
 
@@ -209,44 +235,23 @@ def tile_sharedattnprocessor_pa_kernel(tc, hidden_states, q, k, ref_key, ref_val
                 pair = transpose_head_pair(nc, psum, "short", 2, ident_bf16, key_side[s], 0)
                 nc.scalar.copy(out=channel_major_home(s, 0), in_=pair[:])
 
-            key_job(0)
-            key_job(1)
-            v_bf16 = stage.tile([P, HEADS, TOKENS], BF16, bufs=1)
-            for h in range(HEADS):
-                vT = psum.tile([P, TOKENS], F32, tag="short")
-                for g in range(CH_PASSES):
-                    w_cols = slice(g * CHANNELS + h * HEAD_DIM, g * CHANNELS + (h + 1) * HEAD_DIM)
-                    t_cols = slice(g * TOKENS, (g + 1) * TOKENS)
-                    nc.tensor.matmul_mx(
-                        out=vT[:],
-                        lhsT=wv_codes[:, w_cols].bitcast(FP8X4),
-                        lhsT_scale=wv_scales[:, w_cols],
-                        rhs=hs_codes[:, t_cols].bitcast(FP8X4),
-                        rhs_scale=hs_scales[:, t_cols],
-                        start=(g == 0),
-                        stop=(g == CH_PASSES - 1),
-                    )
-                nc.vector.bn_stats(out=six[:, 0, h, :], in_=vT[:])
-                nc.scalar.copy(out=v_bf16[:, h, :], in_=vT[:])
-            for h in range(HEADS):
-                nc.vector.bn_aggr(out=mean_var[:, 0, h, :], in_=six[:, 0, h, :])
-            style_std = stats.tile([P, HEADS], F32)
-            unbiased_variance(style_std[:], mean_var[:, 0, :, 1])
-            nc.scalar.activation(out=style_std[:], in_=style_std[:], func=ACT.Sqrt)
-            for s in range(2, len(key_side)):
-                key_job(s)
-            nc.vector.tensor_scalar_add(out=style_std[:], in0=style_std[:], scalar1=EPS)
-
             def channel_major(st):
                 return v_bf16[:, QUAD * (st + 2) : QUAD * (st + 3), :] if st < 0 else rv_bf16[st][:]
 
             def adain(st):
                 rv_bf16[st] = stage.tile([P, QUAD, TOKENS], BF16, name="rv_bf16")
                 for j in range(QUAD):
-                    nc.scalar.activation(
-                        out=rv_bf16[st][:, j, :], in_=value_pairs[st][j // PAIR][:, j % PAIR, :], func=ACT.Identity,
-                        scale=gain[st][:, j : j + 1], bias=shift[st][:, j : j + 1],
-                    )
+                    x = value_pairs[st][j // PAIR][:, j % PAIR, :]
+                    if j >= PAIR and st >= 2:
+                        nc.vector.tensor_scalar(
+                            out=rv_bf16[st][:, j, :], in0=x, scalar1=gain[st][:, j : j + 1],
+                            scalar2=shift[st][:, j : j + 1], op0=ALU.mult, op1=ALU.add,
+                        )
+                    else:
+                        nc.scalar.activation(
+                            out=rv_bf16[st][:, j, :], in_=x, func=ACT.Identity,
+                            scale=gain[st][:, j : j + 1], bias=shift[st][:, j : j + 1],
+                        )
 
             def keys_to_partitions(st):
                 v_grouped[st] = stage.tile([P, QUAD * HEAD_DIM * PACK], BF16, align_bytes=64, name="v_grouped")
@@ -263,27 +268,61 @@ def tile_sharedattnprocessor_pa_kernel(tc, hidden_states, q, k, ref_key, ref_val
                     out=v_codes[:, g, cols].bitcast(FP8X4), scales=v_scales[:, g, cols], in_=v_grouped[st][:]
                 )
 
-            steps = REFS * HEADS // QUAD
-            for st in range(-1, steps + 2):
-                independent, chain = [], []
-                if 2 <= st + 2 < steps:
-                    transpose_values(st + 2)
-                    independent = measure_calls(st + 2)
-                if 0 <= st + 1 < steps:
-                    nc.scalar.activation(out=root[st + 1][:], in_=root[st + 1][:], func=ACT.Sqrt)
-                    chain = factor_calls(st + 1)
-                if 0 <= st < steps:
-                    adain(st)
-                if -2 <= st - 1 < steps:
-                    keys_to_partitions(st - 1)
-                if -2 <= st - 2 < steps:
-                    independent.append(lambda: quantise_values(st - 2))
-                if 2 <= st + 2 < steps:
-                    n, h0 = place(st + 2)
-                    independent.append(
-                        lambda: unbiased_variance(root[st + 2][:], mean_var[:, n + 1, h0 : h0 + QUAD, 1])
+            v_bf16 = stage.tile([P, HEADS, TOKENS], BF16, bufs=1)
+            for h in range(HEADS):
+                vT = psum.tile([P, TOKENS], F32, tag=("short", "third")[h % 2])
+                for g in range(CH_PASSES):
+                    w_cols = slice(g * CHANNELS + h * HEAD_DIM, g * CHANNELS + (h + 1) * HEAD_DIM)
+                    t_cols = slice(g * TOKENS, (g + 1) * TOKENS)
+                    nc.tensor.matmul_mx(
+                        out=vT[:],
+                        lhsT=wv_codes[:, w_cols].bitcast(FP8X4),
+                        lhsT_scale=wv_scales[:, w_cols],
+                        rhs=hs_codes[:, t_cols].bitcast(FP8X4),
+                        rhs_scale=hs_scales[:, t_cols],
+                        start=(g == 0),
+                        stop=(g == CH_PASSES - 1),
                     )
-                deal(independent, chain)
+                nc.vector.bn_stats(out=six[:, 0, h, :], in_=vT[:])
+                nc.scalar.copy(out=v_bf16[:, h, :], in_=vT[:])
+            transpose_values(2)
+            aggregate(0, 0, HEADS)
+            style_std = stats.tile([P, HEADS], F32)
+            unbiased_variance(style_std[:], mean_var[:, 0, :, 1])
+            root(style_std)
+            keys_to_partitions(-2)
+            key_job(0)
+            keys_to_partitions(-1)
+            factors(0)
+            factors(1)
+            key_job(1)
+            measure(2)
+            aggregate(2, 0, QUAD)
+            variance(2)
+            quantise_values(-2)
+            quantise_values(-1)
+
+            for st in range(steps + 2):
+                if 3 <= st + 2 < steps:
+                    transpose_values(st + 2)
+                if 2 <= st + 1 < steps:
+                    root(std[st + 1])
+                if st < steps:
+                    adain(st)
+                if 3 <= st + 2 < steps:
+                    measure(st + 2)
+                if 2 <= st + 1 < steps:
+                    factors(st + 1)
+                if 0 <= st - 1 < steps:
+                    keys_to_partitions(st - 1)
+                if 2 <= st < len(key_side):
+                    key_job(st)
+                if 0 <= st - 2:
+                    quantise_values(st - 2)
+                if 3 <= st + 2 < steps:
+                    n, h0 = place(st + 2)
+                    aggregate(n + 1, h0, QUAD)
+                    variance(st + 2)
 
         with ExitStack() as attend:
             work = attend.enter_context(tc.tile_pool(name="work", bufs=2, reuse_waits="tile"))

@@ -329,7 +329,7 @@ def tile_sharedattnprocessor_pa_kernel(tc, hidden_states, q, k, ref_key, ref_val
             small = attend.enter_context(tc.tile_pool(name="small", bufs=3, reuse_waits="tile"))
             psum = attend.enter_context(tc.psum_pool(name="psum_attend", bufs=2, reuse_waits="tile"))
             scores, bank_max, neg_max, e, row_sum, inv_sum = {}, {}, {}, {}, {}, {}
-            e_grouped, e_codes, e_scales, o_bank = {}, {}, {}, {}
+            e_grouped, e_codes, e_scales, o_bank, s_bank, banks = {}, {}, {}, {}, {}, {}
 
             def live(unit):
                 return 0 <= unit < UNITS
@@ -342,18 +342,20 @@ def tile_sharedattnprocessor_pa_kernel(tc, hidden_states, q, k, ref_key, ref_val
                     accum_out=row_sum[i][:],
                 )
 
-            def score_bank(i, g):
+            def score(i, g):
                 h, qt = divmod(i, ROW_TILES)
-                s_bank = psum.tile([P, TOKENS], F32)
+                s_bank[g] = psum.tile([P, TOKENS], F32, name="s_bank", bufs=3)
                 nc.tensor.matmul(
-                    s_bank[:],
+                    s_bank[g][:],
                     lhsT=qT[:, h, qt * P : (qt + 1) * P],
                     rhs=kT[:, h, g * TOKENS : (g + 1) * TOKENS],
                     start=True,
                     stop=True,
                 )
+
+            def evacuate(i, g):
                 nc.vector.tensor_scalar(
-                    out=scores[i][:, g * TOKENS : (g + 1) * TOKENS], in0=s_bank[:],
+                    out=scores[i][:, g * TOKENS : (g + 1) * TOKENS], in0=s_bank[g][:],
                     scalar1=SCORE_SCALE, scalar2=None, op0=ALU.mult, op1=ALU.max,
                     accum_out=bank_max[i][:, g : g + 1],
                 )
@@ -368,7 +370,7 @@ def tile_sharedattnprocessor_pa_kernel(tc, hidden_states, q, k, ref_key, ref_val
 
             def weigh_values(i):
                 h = i // ROW_TILES
-                o_bank[i] = psum.tile([P, HEAD_DIM], F32, name="o_bank")
+                o_bank[i] = psum.tile([P, HEAD_DIM], F32, name="o_bank", tag="misc")
                 for g in range(SEQS):
                     nc.tensor.matmul_mx(
                         out=o_bank[i][:],
@@ -402,32 +404,47 @@ def tile_sharedattnprocessor_pa_kernel(tc, hidden_states, q, k, ref_key, ref_val
                 if live(i - 2):
                     e_codes[i - 2] = work.tile([P, SEQS * P], U32, align_bytes=64, name="e_codes")
                     e_scales[i - 2] = work.tile([P, SEQS * P], U8, align_bytes=64, name="e_scales")
-                for g in range(SEQS):
+                def scores_of(first, count):
                     if live(i + 1):
-                        score_bank(i + 1, g)
-                    if live(i - 1):
+                        for g in range(first, first + count):
+                            score(i + 1, g)
+
+                def leave(g):
+                    if live(i + 1):
+                        evacuate(i + 1, g)
+
+                scores_of(0, 3)
+                leave(0)
+                leave(1)
+                if live(i - 1):
+                    for g in range(SEQS - 1):
                         if g % 2 == 0:
-                            bank = psum.tile([P, 2, HALVES, P], F32, tag="words", bufs=3)
-                        transpose_pass(nc, bank[:, g % 2], e[i - 1][:, g * TOKENS : (g + 1) * TOKENS], ident_f32)
-                        if g % 2 == 1:
-                            group_words(nc.scalar.copy, e_words[:, g - 1 : g + 1], bank[:])
-                        if g == SEQS - 1:
-                            copy = nc.scalar.copy if keys_to_do else nc.vector.tensor_copy
-                            group_words(copy, e_words[:, g : g + 1], bank[:, 0:1])
-                    if g == 2 and live(i - 3):
-                        weigh_values(i - 3)
-                    if g == 3 and keys_to_do:
-                        key_pair = transpose_head_pair(nc, psum, "key_pair", 1, ident_bf16, key_side[s], next_h0)
-                    if g == 0 and live(i - 2):
-                        quantise(i - 2, 0, 4)
-                    if g == 1 and live(i - 2):
-                        quantise(i - 2, 4, 1)
-                        inv_sum[i - 2] = small.tile([P, 1], F32, name="inv_sum")
-                        nc.vector.reciprocal(out=inv_sum[i - 2][:], in_=row_sum[i - 2][:])
-                    if g == 3 and live(i - 3):
-                        finish(i - 3)
-                    if g == 4 and keys_to_do:
-                        nc.vector.tensor_copy(out=channel_major_home(s, next_h0), in_=key_pair[:])
+                            banks[g // 2] = psum.tile([P, 2, HALVES, P], F32, name="bank", tag="words", bufs=3)
+                        transpose_pass(nc, banks[g // 2][:, g % 2], e[i - 1][:, g * TOKENS : (g + 1) * TOKENS], ident_f32)
+                    for b in range(2):
+                        group_words(nc.scalar.copy, e_words[:, 2 * b : 2 * b + 2], banks[b][:])
+                if live(i - 2):
+                    quantise(i - 2, 0, 4)
+                leave(2)
+                scores_of(3, 2)
+                if live(i - 2):
+                    quantise(i - 2, 4, 1)
+                    inv_sum[i - 2] = small.tile([P, 1], F32, name="inv_sum")
+                    nc.vector.reciprocal(out=inv_sum[i - 2][:], in_=row_sum[i - 2][:])
+                leave(3)
+                if live(i - 3):
+                    weigh_values(i - 3)
+                leave(4)
+                if live(i - 1):
+                    banks[2] = psum.tile([P, 2, HALVES, P], F32, name="bank", tag="words", bufs=3)
+                    transpose_pass(nc, banks[2][:, 0], e[i - 1][:, 4 * TOKENS :], ident_f32)
+                    copy = nc.vector.tensor_copy if keys_to_do else nc.scalar.copy
+                    group_words(copy, e_words[:, 4:5], banks[2][:, 0:1])
+                if keys_to_do:
+                    key_pair = transpose_head_pair(nc, psum, "misc", 2, ident_bf16, key_side[s], next_h0)
+                    nc.scalar.copy(out=channel_major_home(s, next_h0), in_=key_pair[:])
+                if live(i - 3):
+                    finish(i - 3)
                 if live(i + 1):
                     neg_max[i + 1] = small.tile([P, 1], F32, name="neg_max")
                     nc.vector.tensor_reduce(

@@ -28,7 +28,6 @@ HALVES = 2
 CH_PASSES = CHANNELS // TOKENS
 EPS = 1e-5
 SCORE_SCALE = HEAD_DIM**-0.5
-UNBIASED = TOKENS / (TOKENS - 1.0)
 SMALLEST_VARIANCE = 1e-30
 
 UNITS = HEADS * ROW_TILES
@@ -92,79 +91,89 @@ def tile_sharedattnprocessor_pa_kernel(tc, hidden_states, q, k, ref_key, ref_val
             return kT[:, h0 : h0 + PAIR, (s - 1) * TOKENS : s * TOKENS]
 
         with ExitStack() as prepare:
-            value_seqs = prepare.enter_context(tc.tile_pool(name="value_seqs", bufs=1))
+            value_seqs = prepare.enter_context(tc.tile_pool(name="value_seqs", bufs=3))
             stats = prepare.enter_context(tc.tile_pool(name="stats", bufs=1))
-            psum = prepare.enter_context(tc.psum_pool(name="psum_prepare", bufs=2))
+            psum = prepare.enter_context(tc.psum_pool(name="psum_prepare", bufs=4))
             hs_codes = stats.tile([P, CH_PASSES * TOKENS], U32, align_bytes=64)
             hs_scales = stats.tile([P, CH_PASSES * TOKENS], U8, align_bytes=64)
             wv_codes = stats.tile([P, CH_PASSES * CHANNELS], U32, align_bytes=64)
             wv_scales = stats.tile([P, CH_PASSES * CHANNELS], U8, align_bytes=64)
-            six = stats.tile([P, SEQS, HEADS, 6], F32)
-            mean_var = stats.tile([P, SEQS, HEADS, 2], F32)
+            tiny = stats.tile([P, 1], F32)
+            nc.gpsimd.memset(tiny[:], SMALLEST_VARIANCE)
             table_probe = stats.tile([P, 1], F32)
-            nc.gpsimd.memset(table_probe[:], 1.0)
-            nc.scalar.activation(out=table_probe[:], in_=table_probe[:], func=ACT.Sqrt)
-            value_pairs, std, gain, shift, rv_bf16, v_grouped = {}, {}, {}, {}, {}, {}
+            nc.scalar.activation(out=table_probe[:], in_=tiny[:], func=ACT.Sqrt)
 
-            steps = REFS * HEADS // QUAD
+            sums, neg_mean, squares, std, inverse, gain, shift = {}, {}, {}, {}, {}, {}, {}
+            for seq in range(SEQS):
+                for name, column in (("sums", sums), ("neg_mean", neg_mean), ("squares", squares), ("std", std)):
+                    column[seq] = stats.tile([P, HEADS], F32, name="%s%d" % (name, seq))
+            value_cm, grouped = {}, {}
 
-            def place(st):
-                return st // 2, QUAD * (st % 2)
+            def copy_and_sum(seq, h, out, bank):
+                nc.vector.tensor_scalar(
+                    out=out, in0=bank, scalar1=1.0, scalar2=None, op0=ALU.mult, op1=ALU.add,
+                    accum_out=sums[seq][:, h : h + 1],
+                )
 
-            def transpose_values(st):
-                n, h0 = place(st)
-                tag, bufs = ("third", 2) if st % 3 == 2 else ("values", 4)
-                value_pairs[st] = [
-                    transpose_head_pair(nc, psum, tag, bufs, ident_bf16, values[n], h0 + PAIR * b)
-                    for b in range(QUAD // PAIR)
-                ]
+            def negative_mean(seq, heads):
+                nc.gpsimd.tensor_scalar(
+                    out=neg_mean[seq][:, heads], in0=sums[seq][:, heads], scalar1=-1.0 / TOKENS, scalar2=None,
+                    op0=ALU.mult,
+                )
 
-            def measure(st):
-                n, h0 = place(st)
-                for j in range(QUAD):
-                    nc.vector.bn_stats(
-                        out=six[:, n + 1, h0 + j, :], in_=value_pairs[st][j // PAIR][:, j % PAIR, :]
+            def square(seq, h, source):
+                distance = stats.tile([P, TOKENS], F32, name="distance", bufs=2)
+                nc.scalar.activation(
+                    out=distance[:], in_=source, func=ACT.Square, bias=neg_mean[seq][:, h : h + 1], scale=1.0,
+                    accum_out=squares[seq][:, h : h + 1],
+                )
+
+            def deviation(seq):
+                nc.scalar.activation(
+                    out=std[seq][:], in_=squares[seq][:], func=ACT.Sqrt, scale=1.0 / (TOKENS - 1), bias=tiny[:]
+                )
+                nc.gpsimd.tensor_scalar(out=std[seq][:], in0=std[seq][:], scalar1=EPS, scalar2=None, op0=ALU.add)
+
+            def value_home(n, pool):
+                value_cm[n] = pool.tile([P, HEADS, TOKENS], BF16, name="value_cm%d" % n, bufs=1)
+
+            def bring_values(n):
+                for h0 in range(0, HEADS, PAIR):
+                    pair = transpose_head_pair(nc, psum, "values", 4, ident_bf16, values[n], h0)
+                    for j in range(PAIR):
+                        copy_and_sum(n + 1, h0 + j, value_cm[n][:, h0 + j, :], pair[:, j, :])
+                    if h0 % QUAD == PAIR:
+                        negative_mean(n + 1, slice(h0 + PAIR - QUAD, h0 + PAIR))
+
+            def measure_values(n):
+                for h in range(HEADS):
+                    square(n + 1, h, value_cm[n][:, h, :])
+                deviation(n + 1)
+
+            def factors(n):
+                seq = n + 1
+                inverse[n] = stats.tile([P, HEADS], F32, name="inverse%d" % n)
+                gain[n] = stats.tile([P, HEADS], F32, name="gain%d" % n)
+                shift[n] = stats.tile([P, HEADS], F32, name="shift%d" % n)
+                nc.vector.reciprocal(out=inverse[n][:], in_=std[seq][:])
+                nc.gpsimd.tensor_tensor(out=gain[n][:], in0=inverse[n][:], in1=std[0][:], op=ALU.mult)
+                nc.gpsimd.tensor_tensor(out=shift[n][:], in0=neg_mean[seq][:], in1=gain[n][:], op=ALU.mult)
+                nc.gpsimd.tensor_tensor(out=shift[n][:], in0=shift[n][:], in1=neg_mean[0][:], op=ALU.subtract)
+
+            def adain(n):
+                for h in range(HEADS):
+                    nc.vector.tensor_scalar(
+                        out=value_cm[n][:, h, :], in0=value_cm[n][:, h, :], scalar1=gain[n][:, h : h + 1],
+                        scalar2=shift[n][:, h : h + 1], op0=ALU.mult, op1=ALU.add,
                     )
 
-            def aggregate(seq, h0, heads):
-                for h in range(h0, h0 + heads):
-                    nc.vector.bn_aggr(out=mean_var[:, seq, h, :], in_=six[:, seq, h, :])
-
-            def variance(st):
-                n, h0 = place(st)
-                std[st] = stats.tile([P, QUAD], F32, name="std", bufs=3)
-                unbiased_variance(std[st][:], mean_var[:, n + 1, h0 : h0 + QUAD, 1])
-
-            def unbiased_variance(out, variances):
-                nc.gpsimd.tensor_scalar(
-                    out=out, in0=variances, scalar1=UNBIASED, scalar2=SMALLEST_VARIANCE, op0=ALU.mult, op1=ALU.max
-                )
-
-            def root(tile):
-                nc.scalar.activation(out=tile[:], in_=tile[:], func=ACT.Sqrt)
-                nc.gpsimd.tensor_scalar(out=tile[:], in0=tile[:], scalar1=EPS, scalar2=None, op0=ALU.add)
-
-            def factors(st):
-                n, h0 = place(st)
-                quad = slice(h0, h0 + QUAD)
-                gain[st] = stats.tile([P, QUAD], F32, name="gain", bufs=3)
-                shift[st] = stats.tile([P, QUAD], F32, name="shift", bufs=3)
-                inverse = stats.tile([P, QUAD], F32, name="inverse", bufs=3)
-                nc.vector.reciprocal(out=inverse[:], in_=std[st][:])
-                nc.gpsimd.tensor_tensor(out=gain[st][:], in0=inverse[:], in1=style_std[:, quad], op=ALU.mult)
-                nc.gpsimd.tensor_tensor(
-                    out=shift[st][:], in0=mean_var[:, n + 1, quad, 0], in1=gain[st][:], op=ALU.mult
-                )
-                nc.gpsimd.tensor_tensor(
-                    out=shift[st][:], in0=mean_var[:, 0, quad, 0], in1=shift[st][:], op=ALU.subtract
-                )
-
             with tc.tile_pool(name="early", bufs=1) as early:
-                values = [value_seqs.tile([P, ROW_TILES, CHANNELS], BF16, name="values0")]
+                first_values = value_seqs.tile([P, ROW_TILES, CHANNELS], BF16, name="values")
                 first_rows = ref_value[0, 0].rearrange("(r p) c -> p r c", p=P)
                 for half in range(2):
                     cols = slice(half * TOKENS, (half + 1) * TOKENS)
-                    nc.sync.dma_start(out=values[0][:, :, cols], in_=first_rows[:, :, cols])
+                    nc.sync.dma_start(out=first_values[:, :, cols], in_=first_rows[:, :, cols])
+                values = [first_values]
                 hs = early.tile([P, ROW_TILES, CHANNELS], BF16)
                 hs_rows = hidden_states[0].rearrange("(r p) c -> p r c", p=P)
                 for r in range(ROW_TILES):
@@ -174,20 +183,17 @@ def tile_sharedattnprocessor_pa_kernel(tc, hidden_states, q, k, ref_key, ref_val
                 for g in range(CH_PASSES):
                     places = slice(g * HALVES, (g + 1) * HALVES)
                     nc.sync.dma_start(out=wv_raw[:, places], in_=wv_rows[:, places])
-                values.append(load_sequence(nc, value_seqs, ref_value[0, 1], "values1"))
+                values.append(load_sequence(nc, value_seqs, ref_value[0, 1], "values"))
                 key_side = [load_sequence(nc, key_seqs, q[0], "queries"), load_sequence(nc, key_seqs, k[0], "keys")]
-                key_side.append(load_sequence(nc, key_seqs, ref_key[0, 0], "ref_keys0"))
-                values.append(load_sequence(nc, value_seqs, ref_value[0, 2], "values2"))
-                key_side.append(load_sequence(nc, key_seqs, ref_key[0, 1], "ref_keys1"))
-                values.append(load_sequence(nc, value_seqs, ref_value[0, 3], "values3"))
-                key_side.append(load_sequence(nc, key_seqs, ref_key[0, 2], "ref_keys2"))
-                key_side.append(load_sequence(nc, key_seqs, ref_key[0, 3], "ref_keys3"))
+                values.append(load_sequence(nc, value_seqs, ref_value[0, 2], "values"))
 
-                transpose_values(0)
-                measure(0)
-                transpose_values(1)
-                measure(1)
-                aggregate(1, 0, HEADS)
+                value_home(0, stats)
+                value_home(1, stats)
+                bring_values(0)
+                measure_values(0)
+                values.append(load_sequence(nc, value_seqs, ref_value[0, 3], "values"))
+                for n in range(REFS):
+                    key_side.append(load_sequence(nc, key_seqs, ref_key[0, n], "ref_keys%d" % n))
                 hs_grouped = early.tile([P, CH_PASSES * TOKENS * PACK], BF16, align_bytes=64)
                 hs_words = words_view(hs_grouped)
                 for r in range(0, ROW_TILES, 2):
@@ -197,15 +203,12 @@ def tile_sharedattnprocessor_pa_kernel(tc, hidden_states, q, k, ref_key, ref_val
                             transpose_pass(nc, bank[:, j], hs[:, r + j, g * TOKENS : (g + 1) * TOKENS], ident_f32)
                         b0 = g * ROW_TILES + r
                         group_words(nc.scalar.copy, hs_words[:, b0 : b0 + 2], bank[:])
-                for st in range(2):
-                    variance(st)
-                    root(std[st])
 
                 wv_grouped = {}
 
                 def group_weights(copy, g, half):
                     four_rows = wv_raw[:, g * HALVES : (g + 1) * HALVES].rearrange("p a e c -> p (a e) c")
-                    wv_grouped[g, half] = early.tile([P, TOKENS, PACK], BF16, align_bytes=64, bufs=4, name="wv_grouped")
+                    wv_grouped[g, half] = early.tile([P, TOKENS, PACK], BF16, align_bytes=64, bufs=3, name="wv_grouped")
                     copy(
                         out=wv_grouped[g, half][:].rearrange("p (c i) t -> p c t i", i=4),
                         in_=four_rows[:, :, half * TOKENS : (half + 1) * TOKENS].rearrange("p t (c i) -> p c t i", i=4),
@@ -219,58 +222,47 @@ def tile_sharedattnprocessor_pa_kernel(tc, hidden_states, q, k, ref_key, ref_val
                         in_=wv_grouped[g, half][:].rearrange("p c t -> p (c t)"),
                     )
 
-                for g in range(CH_PASSES):
-                    group_weights(nc.scalar.copy, g, 0)
-                    group_weights(nc.vector.tensor_copy, g, 1)
-                    if g == 0:
-                        nc.vector.quantize_mx(out=hs_codes[:].bitcast(FP8X4), scales=hs_scales[:], in_=hs_grouped[:])
-                        quantise_weights(0, 1)
-                for g in range(CH_PASSES):
-                    quantise_weights(g, 0)
+                group_weights(nc.scalar.copy, 0, 0)
+                group_weights(nc.vector.tensor_copy, 0, 1)
+                group_weights(nc.vector.tensor_copy, 1, 0)
+                nc.vector.quantize_mx(out=hs_codes[:].bitcast(FP8X4), scales=hs_scales[:], in_=hs_grouped[:])
+                quantise_weights(1, 0)
+                quantise_weights(0, 1)
+                group_weights(nc.vector.tensor_copy, 1, 1)
+                quantise_weights(0, 0)
                 quantise_weights(1, 1)
 
             stage = prepare.enter_context(tc.tile_pool(name="stage", bufs=3, reuse_waits="tile"))
+            v_bf16 = stage.tile([P, HEADS, TOKENS], BF16, bufs=1)
+            value_home(2, stage)
+            value_home(3, stage)
 
             def key_job(s):
-                pair = transpose_head_pair(nc, psum, "short", 2, ident_bf16, key_side[s], 0)
+                pair = transpose_head_pair(nc, psum, "short", 4, ident_bf16, key_side[s], 0)
                 nc.scalar.copy(out=channel_major_home(s, 0), in_=pair[:])
 
-            def channel_major(st):
-                return v_bf16[:, QUAD * (st + 2) : QUAD * (st + 3), :] if st < 0 else rv_bf16[st][:]
-
-            def adain(st):
-                rv_bf16[st] = stage.tile([P, QUAD, TOKENS], BF16, name="rv_bf16")
-                for j in range(QUAD):
-                    x = value_pairs[st][j // PAIR][:, j % PAIR, :]
-                    if j >= PAIR and st >= 2:
-                        nc.vector.tensor_scalar(
-                            out=rv_bf16[st][:, j, :], in0=x, scalar1=gain[st][:, j : j + 1],
-                            scalar2=shift[st][:, j : j + 1], op0=ALU.mult, op1=ALU.add,
+            def keys_to_partitions(seq, channel_major):
+                for h0 in range(0, HEADS, PAIR):
+                    if h0 % QUAD == 0:
+                        grouped[seq, h0 // QUAD] = stage.tile(
+                            [P, QUAD * HEAD_DIM * PACK], BF16, align_bytes=64, name="grouped"
                         )
-                    else:
-                        nc.scalar.activation(
-                            out=rv_bf16[st][:, j, :], in_=x, func=ACT.Identity,
-                            scale=gain[st][:, j : j + 1], bias=shift[st][:, j : j + 1],
-                        )
-
-            def keys_to_partitions(st):
-                v_grouped[st] = stage.tile([P, QUAD * HEAD_DIM * PACK], BF16, align_bytes=64, name="v_grouped")
-                for j0 in range(0, QUAD, PAIR):
                     bank = psum.tile([P, PAIR, HALVES, P], F32, tag="short")
                     for j in range(PAIR):
-                        transpose_pass(nc, bank[:, j], channel_major(st)[:, j0 + j, :], ident_f32)
-                    group_words(nc.scalar.copy, words_view(v_grouped[st])[:, j0 : j0 + PAIR], bank[:])
+                        transpose_pass(nc, bank[:, j], channel_major[:, h0 + j, :], ident_f32)
+                    j0 = h0 % QUAD
+                    group_words(nc.scalar.copy, words_view(grouped[seq, h0 // QUAD])[:, j0 : j0 + PAIR], bank[:])
 
-            def quantise_values(st):
-                g, h0 = (0, QUAD * (st + 2)) if st < 0 else (st // 2 + 1, QUAD * (st % 2))
-                cols = slice(h0 * HEAD_DIM, (h0 + QUAD) * HEAD_DIM)
-                nc.vector.quantize_mx(
-                    out=v_codes[:, g, cols].bitcast(FP8X4), scales=v_scales[:, g, cols], in_=v_grouped[st][:]
-                )
+            def quantise_values(seq):
+                for half in range(HEADS // QUAD):
+                    cols = slice(half * QUAD * HEAD_DIM, (half + 1) * QUAD * HEAD_DIM)
+                    nc.vector.quantize_mx(
+                        out=v_codes[:, seq, cols].bitcast(FP8X4), scales=v_scales[:, seq, cols],
+                        in_=grouped[seq, half][:],
+                    )
 
-            v_bf16 = stage.tile([P, HEADS, TOKENS], BF16, bufs=1)
             for h in range(HEADS):
-                vT = psum.tile([P, TOKENS], F32, tag=("short", "third")[h % 2])
+                vT = psum.tile([P, TOKENS], F32, tag="short")
                 for g in range(CH_PASSES):
                     w_cols = slice(g * CHANNELS + h * HEAD_DIM, g * CHANNELS + (h + 1) * HEAD_DIM)
                     t_cols = slice(g * TOKENS, (g + 1) * TOKENS)
@@ -283,46 +275,28 @@ def tile_sharedattnprocessor_pa_kernel(tc, hidden_states, q, k, ref_key, ref_val
                         start=(g == 0),
                         stop=(g == CH_PASSES - 1),
                     )
-                nc.vector.bn_stats(out=six[:, 0, h, :], in_=vT[:])
-                nc.scalar.copy(out=v_bf16[:, h, :], in_=vT[:])
-            transpose_values(2)
-            aggregate(0, 0, HEADS)
-            style_std = stats.tile([P, HEADS], F32)
-            unbiased_variance(style_std[:], mean_var[:, 0, :, 1])
-            root(style_std)
-            keys_to_partitions(-2)
-            key_job(0)
-            keys_to_partitions(-1)
+                copy_and_sum(0, h, v_bf16[:, h, :], vT[:])
+                negative_mean(0, slice(h, h + 1))
+                square(0, h, vT[:])
+            deviation(0)
+            bring_values(1)
+            keys_to_partitions(0, v_bf16)
             factors(0)
-            factors(1)
+            key_job(0)
             key_job(1)
-            measure(2)
-            aggregate(2, 0, QUAD)
-            variance(2)
-            quantise_values(-2)
-            quantise_values(-1)
+            measure_values(1)
+            quantise_values(0)
 
-            for st in range(steps + 2):
-                if 3 <= st + 2 < steps:
-                    transpose_values(st + 2)
-                if 2 <= st + 1 < steps:
-                    root(std[st + 1])
-                if st < steps:
-                    adain(st)
-                if 3 <= st + 2 < steps:
-                    measure(st + 2)
-                if 2 <= st + 1 < steps:
-                    factors(st + 1)
-                if 0 <= st - 1 < steps:
-                    keys_to_partitions(st - 1)
-                if 2 <= st < len(key_side):
-                    key_job(st)
-                if 0 <= st - 2:
-                    quantise_values(st - 2)
-                if 3 <= st + 2 < steps:
-                    n, h0 = place(st + 2)
-                    aggregate(n + 1, h0, QUAD)
-                    variance(st + 2)
+            for n in range(REFS):
+                adain(n)
+                keys_to_partitions(n + 1, value_cm[n])
+                if n + 1 < REFS:
+                    factors(n + 1)
+                if n + 2 < REFS:
+                    bring_values(n + 2)
+                    measure_values(n + 2)
+                key_job(n + 2)
+                quantise_values(n + 1)
 
         with ExitStack() as attend:
             work = attend.enter_context(tc.tile_pool(name="work", bufs=2, reuse_waits="tile"))

@@ -74,6 +74,7 @@ def tile_sharedattnprocessor_pa_kernel(tc, hidden_states, q, k, ref_key, ref_val
         const = whole.enter_context(tc.tile_pool(name="const", bufs=1))
         keep = whole.enter_context(tc.tile_pool(name="keep", bufs=1))
         key_seqs = whole.enter_context(tc.tile_pool(name="key_seqs", bufs=1))
+        psum = whole.enter_context(tc.psum_pool(name="psum", bufs=3, reuse_waits="tile"))
 
         ident_bf16 = const.tile([P, P], BF16)
         make_identity(nc, ident_bf16[:])
@@ -90,83 +91,111 @@ def tile_sharedattnprocessor_pa_kernel(tc, hidden_states, q, k, ref_key, ref_val
                 return qT[:, h0 : h0 + PAIR, :]
             return kT[:, h0 : h0 + PAIR, (s - 1) * TOKENS : s * TOKENS]
 
-        with ExitStack() as prepare:
-            value_seqs = prepare.enter_context(tc.tile_pool(name="value_seqs", bufs=3))
-            stats = prepare.enter_context(tc.tile_pool(name="stats", bufs=1))
-            psum = prepare.enter_context(tc.psum_pool(name="psum_prepare", bufs=4))
-            hs_codes = stats.tile([P, CH_PASSES * TOKENS], U32, align_bytes=64)
-            hs_scales = stats.tile([P, CH_PASSES * TOKENS], U8, align_bytes=64)
-            wv_codes = stats.tile([P, CH_PASSES * CHANNELS], U32, align_bytes=64)
-            wv_scales = stats.tile([P, CH_PASSES * CHANNELS], U8, align_bytes=64)
-            tiny = stats.tile([P, 1], F32)
-            nc.gpsimd.memset(tiny[:], SMALLEST_VARIANCE)
-            table_probe = stats.tile([P, 1], F32)
-            nc.scalar.activation(out=table_probe[:], in_=tiny[:], func=ACT.Sqrt)
+        packing = whole.enter_context(tc.tile_pool(name="packing", bufs=2, reuse_waits="tile"))
+        grouped = {}
 
-            sums, neg_mean, squares, std, inverse, gain, shift = {}, {}, {}, {}, {}, {}, {}
-            for seq in range(SEQS):
-                for name, column in (("sums", sums), ("neg_mean", neg_mean), ("squares", squares), ("std", std)):
-                    column[seq] = stats.tile([P, HEADS], F32, name="%s%d" % (name, seq))
-            value_cm, grouped = {}, {}
-
-            def copy_and_sum(seq, h, out, bank):
-                nc.vector.tensor_scalar(
-                    out=out, in0=bank, scalar1=1.0, scalar2=None, op0=ALU.mult, op1=ALU.add,
-                    accum_out=sums[seq][:, h : h + 1],
+        def quantise_values(seq):
+            for half in range(HEADS // QUAD):
+                cols = slice(half * QUAD * HEAD_DIM, (half + 1) * QUAD * HEAD_DIM)
+                nc.vector.quantize_mx(
+                    out=v_codes[:, seq, cols].bitcast(FP8X4), scales=v_scales[:, seq, cols], in_=grouped[seq, half][:]
                 )
 
-            def negative_mean(seq, heads):
-                nc.gpsimd.tensor_scalar(
-                    out=neg_mean[seq][:, heads], in0=sums[seq][:, heads], scalar1=-1.0 / TOKENS, scalar2=None,
-                    op0=ALU.mult,
-                )
+        cm_pool = whole.enter_context(tc.tile_pool(name="cm_pool", bufs=4, reuse_waits="tile"))
+        stats = whole.enter_context(tc.tile_pool(name="stats", bufs=1))
+        tiny = stats.tile([P, 1], F32)
+        nc.gpsimd.memset(tiny[:], SMALLEST_VARIANCE)
+        table_probe = stats.tile([P, 1], F32)
+        nc.scalar.activation(out=table_probe[:], in_=tiny[:], func=ACT.Sqrt)
 
-            def square(seq, h, source):
-                distance = stats.tile([P, TOKENS], F32, name="distance", bufs=2)
-                nc.scalar.activation(
-                    out=distance[:], in_=source, func=ACT.Square, bias=neg_mean[seq][:, h : h + 1], scale=1.0,
-                    accum_out=squares[seq][:, h : h + 1],
-                )
+        sums, neg_mean, squares, std, inverse, gain, shift = {}, {}, {}, {}, {}, {}, {}
+        for seq in range(SEQS):
+            for name, column in (("sums", sums), ("neg_mean", neg_mean), ("squares", squares), ("std", std)):
+                column[seq] = stats.tile([P, HEADS], F32, name="%s%d" % (name, seq))
+        value_cm = {}
 
-            def deviation(seq):
-                nc.scalar.activation(
-                    out=std[seq][:], in_=squares[seq][:], func=ACT.Sqrt, scale=1.0 / (TOKENS - 1), bias=tiny[:]
-                )
-                nc.gpsimd.tensor_scalar(out=std[seq][:], in0=std[seq][:], scalar1=EPS, scalar2=None, op0=ALU.add)
+        def copy_and_sum(seq, h, out, bank):
+            nc.vector.tensor_scalar(
+                out=out, in0=bank, scalar1=1.0, scalar2=None, op0=ALU.mult, op1=ALU.add,
+                accum_out=sums[seq][:, h : h + 1],
+            )
 
-            def value_home(n, pool):
-                value_cm[n] = pool.tile([P, HEADS, TOKENS], BF16, name="value_cm%d" % n, bufs=1)
+        def negative_mean(seq, heads):
+            nc.gpsimd.tensor_scalar(
+                out=neg_mean[seq][:, heads], in0=sums[seq][:, heads], scalar1=-1.0 / TOKENS, scalar2=None,
+                op0=ALU.mult,
+            )
 
-            def bring_values(n):
-                for h0 in range(0, HEADS, PAIR):
-                    pair = transpose_head_pair(nc, psum, "values", 4, ident_bf16, values[n], h0)
-                    for j in range(PAIR):
-                        copy_and_sum(n + 1, h0 + j, value_cm[n][:, h0 + j, :], pair[:, j, :])
-                    if h0 % QUAD == PAIR:
-                        negative_mean(n + 1, slice(h0 + PAIR - QUAD, h0 + PAIR))
+        def square(seq, h, source):
+            distance = stats.tile([P, TOKENS], BF16, name="distance", bufs=2)
+            nc.scalar.activation(
+                out=distance[:], in_=source, func=ACT.Square, bias=neg_mean[seq][:, h : h + 1], scale=1.0,
+                accum_out=squares[seq][:, h : h + 1],
+            )
 
-            def measure_values(n):
-                for h in range(HEADS):
-                    square(n + 1, h, value_cm[n][:, h, :])
+        def deviation(seq):
+            nc.scalar.activation(
+                out=std[seq][:], in_=squares[seq][:], func=ACT.Sqrt, scale=1.0 / (TOKENS - 1), bias=tiny[:]
+            )
+            nc.gpsimd.tensor_scalar(out=std[seq][:], in0=std[seq][:], scalar1=EPS, scalar2=None, op0=ALU.add)
+
+        def bring_values(n):
+            value_cm[n] = cm_pool.tile([P, HEADS, TOKENS], BF16, name="cm")
+            for h0 in range(0, HEADS, PAIR):
+                pair = transpose_head_pair(nc, psum, "misc", 2, ident_bf16, values[n], h0)
+                for j in range(PAIR):
+                    copy_and_sum(n + 1, h0 + j, value_cm[n][:, h0 + j, :], pair[:, j, :])
+                if h0 % QUAD == PAIR:
+                    negative_mean(n + 1, slice(h0 + PAIR - QUAD, h0 + PAIR))
+
+        def measure_values(n, first=0, last=HEADS):
+            for h in range(first, last):
+                square(n + 1, h, value_cm[n][:, h, :])
+            if last == HEADS:
                 deviation(n + 1)
 
-            def factors(n):
-                seq = n + 1
-                inverse[n] = stats.tile([P, HEADS], F32, name="inverse%d" % n)
-                gain[n] = stats.tile([P, HEADS], F32, name="gain%d" % n)
-                shift[n] = stats.tile([P, HEADS], F32, name="shift%d" % n)
-                nc.vector.reciprocal(out=inverse[n][:], in_=std[seq][:])
-                nc.gpsimd.tensor_tensor(out=gain[n][:], in0=inverse[n][:], in1=std[0][:], op=ALU.mult)
-                nc.gpsimd.tensor_tensor(out=shift[n][:], in0=neg_mean[seq][:], in1=gain[n][:], op=ALU.mult)
-                nc.gpsimd.tensor_tensor(out=shift[n][:], in0=shift[n][:], in1=neg_mean[0][:], op=ALU.subtract)
+        def factors(n):
+            seq = n + 1
+            inverse[n] = stats.tile([P, HEADS], F32, name="inverse%d" % n)
+            gain[n] = stats.tile([P, HEADS], F32, name="gain%d" % n)
+            shift[n] = stats.tile([P, HEADS], F32, name="shift%d" % n)
+            nc.vector.reciprocal(out=inverse[n][:], in_=std[seq][:])
+            nc.gpsimd.tensor_tensor(out=gain[n][:], in0=inverse[n][:], in1=std[0][:], op=ALU.mult)
+            nc.gpsimd.tensor_tensor(out=shift[n][:], in0=neg_mean[seq][:], in1=gain[n][:], op=ALU.mult)
+            nc.gpsimd.tensor_tensor(out=shift[n][:], in0=shift[n][:], in1=neg_mean[0][:], op=ALU.subtract)
 
-            def adain(n):
-                for h in range(HEADS):
-                    nc.vector.tensor_scalar(
-                        out=value_cm[n][:, h, :], in0=value_cm[n][:, h, :], scalar1=gain[n][:, h : h + 1],
-                        scalar2=shift[n][:, h : h + 1], op0=ALU.mult, op1=ALU.add,
+        def adain(n):
+            for h in range(HEADS):
+                nc.vector.tensor_scalar(
+                    out=value_cm[n][:, h, :], in0=value_cm[n][:, h, :], scalar1=gain[n][:, h : h + 1],
+                    scalar2=shift[n][:, h : h + 1], op0=ALU.mult, op1=ALU.add,
+                )
+
+        def keys_to_partitions(seq, channel_major):
+            banks = []
+            for h0 in range(0, HEADS, PAIR):
+                if h0 % QUAD == 0:
+                    grouped[seq, h0 // QUAD] = packing.tile(
+                        [P, QUAD * HEAD_DIM * PACK], BF16, align_bytes=64, name="grouped"
                     )
+                bank = psum.tile([P, PAIR, HALVES, P], F32, tag="words", bufs=3)
+                for j in range(PAIR):
+                    transpose_pass(nc, bank[:, j], channel_major[:, h0 + j, :], ident_f32)
+                banks.append(bank)
+            return banks
 
+        def regroup(seq, banks, first, last, copy):
+            for b in range(first, last):
+                half, j0 = divmod(b * PAIR, QUAD)
+                group_words(copy, words_view(grouped[seq, half])[:, j0 : j0 + PAIR], banks[b][:])
+
+        with ExitStack() as prepare:
+            value_seqs = prepare.enter_context(tc.tile_pool(name="value_seqs", bufs=2))
+            projection = prepare.enter_context(tc.tile_pool(name="projection", bufs=1))
+            hs_codes = projection.tile([P, CH_PASSES * TOKENS], U32, align_bytes=64)
+            hs_scales = projection.tile([P, CH_PASSES * TOKENS], U8, align_bytes=64)
+            wv_codes = projection.tile([P, CH_PASSES * CHANNELS], U32, align_bytes=64)
+            wv_scales = projection.tile([P, CH_PASSES * CHANNELS], U8, align_bytes=64)
             with tc.tile_pool(name="early", bufs=1) as early:
                 first_values = value_seqs.tile([P, ROW_TILES, CHANNELS], BF16, name="values")
                 first_rows = ref_value[0, 0].rearrange("(r p) c -> p r c", p=P)
@@ -185,20 +214,16 @@ def tile_sharedattnprocessor_pa_kernel(tc, hidden_states, q, k, ref_key, ref_val
                     nc.sync.dma_start(out=wv_raw[:, places], in_=wv_rows[:, places])
                 values.append(load_sequence(nc, value_seqs, ref_value[0, 1], "values"))
                 key_side = [load_sequence(nc, key_seqs, q[0], "queries"), load_sequence(nc, key_seqs, k[0], "keys")]
-                values.append(load_sequence(nc, value_seqs, ref_value[0, 2], "values"))
 
-                value_home(0, stats)
-                value_home(1, stats)
                 bring_values(0)
-                measure_values(0)
-                values.append(load_sequence(nc, value_seqs, ref_value[0, 3], "values"))
-                for n in range(REFS):
+                values.append(load_sequence(nc, value_seqs, ref_value[0, 2], "values"))
+                for n in range(2):
                     key_side.append(load_sequence(nc, key_seqs, ref_key[0, n], "ref_keys%d" % n))
                 hs_grouped = early.tile([P, CH_PASSES * TOKENS * PACK], BF16, align_bytes=64)
                 hs_words = words_view(hs_grouped)
                 for r in range(0, ROW_TILES, 2):
                     for g in range(CH_PASSES):
-                        bank = psum.tile([P, 2, HALVES, P], F32, tag="short")
+                        bank = psum.tile([P, 2, HALVES, P], F32, tag="words", bufs=3)
                         for j in range(2):
                             transpose_pass(nc, bank[:, j], hs[:, r + j, g * TOKENS : (g + 1) * TOKENS], ident_f32)
                         b0 = g * ROW_TILES + r
@@ -208,7 +233,7 @@ def tile_sharedattnprocessor_pa_kernel(tc, hidden_states, q, k, ref_key, ref_val
 
                 def group_weights(copy, g, half):
                     four_rows = wv_raw[:, g * HALVES : (g + 1) * HALVES].rearrange("p a e c -> p (a e) c")
-                    wv_grouped[g, half] = early.tile([P, TOKENS, PACK], BF16, align_bytes=64, bufs=3, name="wv_grouped")
+                    wv_grouped[g, half] = early.tile([P, TOKENS, PACK], BF16, align_bytes=64, bufs=2, name="wv_grouped")
                     copy(
                         out=wv_grouped[g, half][:].rearrange("p (c i) t -> p c t i", i=4),
                         in_=four_rows[:, :, half * TOKENS : (half + 1) * TOKENS].rearrange("p t (c i) -> p c t i", i=4),
@@ -222,47 +247,24 @@ def tile_sharedattnprocessor_pa_kernel(tc, hidden_states, q, k, ref_key, ref_val
                         in_=wv_grouped[g, half][:].rearrange("p c t -> p (c t)"),
                     )
 
-                group_weights(nc.scalar.copy, 0, 0)
                 group_weights(nc.vector.tensor_copy, 0, 1)
-                group_weights(nc.vector.tensor_copy, 1, 0)
+                group_weights(nc.scalar.copy, 0, 0)
+                measure_values(0, 0, QUAD)
                 nc.vector.quantize_mx(out=hs_codes[:].bitcast(FP8X4), scales=hs_scales[:], in_=hs_grouped[:])
-                quantise_weights(1, 0)
                 quantise_weights(0, 1)
-                group_weights(nc.vector.tensor_copy, 1, 1)
+                group_weights(nc.vector.tensor_copy, 1, 0)
                 quantise_weights(0, 0)
+                quantise_weights(1, 0)
+                group_weights(nc.vector.tensor_copy, 1, 1)
                 quantise_weights(1, 1)
 
-            stage = prepare.enter_context(tc.tile_pool(name="stage", bufs=3, reuse_waits="tile"))
-            v_bf16 = stage.tile([P, HEADS, TOKENS], BF16, bufs=1)
-            value_home(2, stage)
-            value_home(3, stage)
-
             def key_job(s):
-                pair = transpose_head_pair(nc, psum, "short", 4, ident_bf16, key_side[s], 0)
+                pair = transpose_head_pair(nc, psum, "words", 3, ident_bf16, key_side[s], 0)
                 nc.scalar.copy(out=channel_major_home(s, 0), in_=pair[:])
 
-            def keys_to_partitions(seq, channel_major):
-                for h0 in range(0, HEADS, PAIR):
-                    if h0 % QUAD == 0:
-                        grouped[seq, h0 // QUAD] = stage.tile(
-                            [P, QUAD * HEAD_DIM * PACK], BF16, align_bytes=64, name="grouped"
-                        )
-                    bank = psum.tile([P, PAIR, HALVES, P], F32, tag="short")
-                    for j in range(PAIR):
-                        transpose_pass(nc, bank[:, j], channel_major[:, h0 + j, :], ident_f32)
-                    j0 = h0 % QUAD
-                    group_words(nc.scalar.copy, words_view(grouped[seq, h0 // QUAD])[:, j0 : j0 + PAIR], bank[:])
-
-            def quantise_values(seq):
-                for half in range(HEADS // QUAD):
-                    cols = slice(half * QUAD * HEAD_DIM, (half + 1) * QUAD * HEAD_DIM)
-                    nc.vector.quantize_mx(
-                        out=v_codes[:, seq, cols].bitcast(FP8X4), scales=v_scales[:, seq, cols],
-                        in_=grouped[seq, half][:],
-                    )
-
+            v_bf16 = cm_pool.tile([P, HEADS, TOKENS], BF16, name="cm")
             for h in range(HEADS):
-                vT = psum.tile([P, TOKENS], F32, tag="short")
+                vT = psum.tile([P, TOKENS], F32, tag="s_bank", bufs=3)
                 for g in range(CH_PASSES):
                     w_cols = slice(g * CHANNELS + h * HEAD_DIM, g * CHANNELS + (h + 1) * HEAD_DIM)
                     t_cols = slice(g * TOKENS, (g + 1) * TOKENS)
@@ -279,31 +281,35 @@ def tile_sharedattnprocessor_pa_kernel(tc, hidden_states, q, k, ref_key, ref_val
                 negative_mean(0, slice(h, h + 1))
                 square(0, h, vT[:])
             deviation(0)
+            measure_values(0, QUAD, HEADS)
             bring_values(1)
-            keys_to_partitions(0, v_bf16)
-            factors(0)
+            values.append(load_sequence(nc, value_seqs, ref_value[0, 3], "values"))
+            for n in range(2, REFS):
+                key_side.append(load_sequence(nc, key_seqs, ref_key[0, n], "ref_keys%d" % n))
+            v_banks = keys_to_partitions(0, v_bf16)
+            regroup(0, v_banks, 0, len(v_banks), nc.vector.tensor_copy)
             key_job(0)
             key_job(1)
+            factors(0)
             measure_values(1)
-            quantise_values(0)
 
-            for n in range(REFS):
+            for n in range(REFS - 2):
                 adain(n)
-                keys_to_partitions(n + 1, value_cm[n])
-                if n + 1 < REFS:
-                    factors(n + 1)
-                if n + 2 < REFS:
-                    bring_values(n + 2)
-                    measure_values(n + 2)
-                key_job(n + 2)
-                quantise_values(n + 1)
+                quantise_values(n)
+                bring_values(n + 2)
+                factors(n + 1)
+                banks = keys_to_partitions(n + 1, value_cm[n])
+                regroup(n + 1, banks, 0, 2, nc.scalar.copy)
+                key_job(2 * n + 2)
+                key_job(2 * n + 3)
+                measure_values(n + 2)
+                regroup(n + 1, banks, 2, 4, nc.vector.tensor_copy)
 
         with ExitStack() as attend:
             work = attend.enter_context(tc.tile_pool(name="work", bufs=2, reuse_waits="tile"))
             small = attend.enter_context(tc.tile_pool(name="small", bufs=3, reuse_waits="tile"))
-            psum = attend.enter_context(tc.psum_pool(name="psum_attend", bufs=2, reuse_waits="tile"))
             scores, bank_max, neg_max, e, row_sum, inv_sum = {}, {}, {}, {}, {}, {}
-            e_grouped, e_codes, e_scales, o_bank, s_bank, banks = {}, {}, {}, {}, {}, {}
+            e_grouped, e_codes, e_scales, o_bank, s_bank, banks, later_sums = {}, {}, {}, {}, {}, {}, {}
 
             def live(unit):
                 return 0 <= unit < UNITS
@@ -311,10 +317,17 @@ def tile_sharedattnprocessor_pa_kernel(tc, hidden_states, q, k, ref_key, ref_val
             def exponential(i):
                 e[i] = work.tile([P, KEYS], BF16, name="e")
                 row_sum[i] = small.tile([P, 1], F32, name="row_sum", bufs=5)
-                nc.scalar.activation(
-                    out=e[i][:], in_=scores[i][:], func=ACT.Exp, bias=neg_max[i][:], scale=1.0,
-                    accum_out=row_sum[i][:],
-                )
+                parts = (0, KEYS) if i < UNITS - 1 else (0, 2 * TOKENS, KEYS)
+                sums_of_parts = [row_sum[i]]
+                for part in range(1, len(parts) - 1):
+                    sums_of_parts.append(small.tile([P, 1], F32, name="part_sum", bufs=1))
+                for part, total in enumerate(sums_of_parts):
+                    columns = slice(parts[part], parts[part + 1])
+                    nc.scalar.activation(
+                        out=e[i][:, columns], in_=scores[i][:, columns], func=ACT.Exp, bias=neg_max[i][:], scale=1.0,
+                        accum_out=total[:],
+                    )
+                later_sums[i] = sums_of_parts[1:]
 
             def score(i, g):
                 h, qt = divmod(i, ROW_TILES)
@@ -344,7 +357,7 @@ def tile_sharedattnprocessor_pa_kernel(tc, hidden_states, q, k, ref_key, ref_val
 
             def weigh_values(i):
                 h = i // ROW_TILES
-                o_bank[i] = psum.tile([P, HEAD_DIM], F32, name="o_bank", tag="misc")
+                o_bank[i] = psum.tile([P, HEAD_DIM], F32, name="o_bank", tag="misc", bufs=2)
                 for g in range(SEQS):
                     nc.tensor.matmul_mx(
                         out=o_bank[i][:],
@@ -387,38 +400,51 @@ def tile_sharedattnprocessor_pa_kernel(tc, hidden_states, q, k, ref_key, ref_val
                     if live(i + 1):
                         evacuate(i + 1, g)
 
+                late = {0: REFS - 2, 1: REFS - 1}.get(i)
+                if late is not None:
+                    adain(late)
+                if 0 <= i <= 2:
+                    quantise_values(REFS - 2 + i)
                 scores_of(0, 3)
                 leave(0)
                 leave(1)
                 if live(i - 1):
-                    for g in range(SEQS - 1):
+                    for g in range(SEQS):
                         if g % 2 == 0:
                             banks[g // 2] = psum.tile([P, 2, HALVES, P], F32, name="bank", tag="words", bufs=3)
                         transpose_pass(nc, banks[g // 2][:, g % 2], e[i - 1][:, g * TOKENS : (g + 1) * TOKENS], ident_f32)
-                    for b in range(2):
-                        group_words(nc.scalar.copy, e_words[:, 2 * b : 2 * b + 2], banks[b][:])
+                if keys_to_do:
+                    key_pair = transpose_head_pair(nc, psum, "misc", 2, ident_bf16, key_side[s], next_h0)
+                if live(i - 1):
+                    group_words(nc.scalar.copy, e_words[:, 0:2], banks[0][:])
+                    copy = nc.scalar.copy if live(i + 1) else nc.vector.tensor_copy
+                    group_words(copy, e_words[:, 2:4], banks[1][:])
+                if keys_to_do:
+                    nc.scalar.copy(out=channel_major_home(s, next_h0), in_=key_pair[:])
                 if live(i - 2):
                     quantise(i - 2, 0, 4)
                 leave(2)
                 scores_of(3, 2)
+                if live(i - 1):
+                    copy = nc.scalar.copy if live(i + 1) and not keys_to_do else nc.vector.tensor_copy
+                    group_words(copy, e_words[:, 4:5], banks[2][:, 0:1])
                 if live(i - 2):
                     quantise(i - 2, 4, 1)
+                    for total in later_sums[i - 2]:
+                        nc.vector.tensor_add(out=row_sum[i - 2][:], in0=row_sum[i - 2][:], in1=total[:])
                     inv_sum[i - 2] = small.tile([P, 1], F32, name="inv_sum")
                     nc.vector.reciprocal(out=inv_sum[i - 2][:], in_=row_sum[i - 2][:])
                 leave(3)
                 if live(i - 3):
                     weigh_values(i - 3)
                 leave(4)
-                if live(i - 1):
-                    banks[2] = psum.tile([P, 2, HALVES, P], F32, name="bank", tag="words", bufs=3)
-                    transpose_pass(nc, banks[2][:, 0], e[i - 1][:, 4 * TOKENS :], ident_f32)
-                    copy = nc.vector.tensor_copy if keys_to_do else nc.scalar.copy
-                    group_words(copy, e_words[:, 4:5], banks[2][:, 0:1])
-                if keys_to_do:
-                    key_pair = transpose_head_pair(nc, psum, "misc", 2, ident_bf16, key_side[s], next_h0)
-                    nc.scalar.copy(out=channel_major_home(s, next_h0), in_=key_pair[:])
                 if live(i - 3):
                     finish(i - 3)
+                if late is not None:
+                    late_banks = keys_to_partitions(late + 1, value_cm[late])
+                    regroup(late + 1, late_banks, 0, len(late_banks), nc.scalar.copy)
+                    if late + 1 < REFS:
+                        factors(late + 1)
                 if live(i + 1):
                     neg_max[i + 1] = small.tile([P, 1], F32, name="neg_max")
                     nc.vector.tensor_reduce(

@@ -139,10 +139,12 @@ def tile_sharedattnprocessor_pa_kernel(tc, hidden_states, q, k, ref_key, ref_val
             )
             nc.gpsimd.tensor_scalar(out=std[seq][:], in0=std[seq][:], scalar1=EPS, scalar2=None, op0=ALU.add)
 
-        def bring_values(n):
-            value_cm[n] = cm_pool.tile([P, HEADS, TOKENS], BF16, name="cm")
-            for h0 in range(0, HEADS, PAIR):
-                pair = transpose_head_pair(nc, psum, "misc", 2, ident_bf16, values[n], h0)
+        def bring_values(n, first=0, last=HEADS):
+            if first == 0:
+                value_cm[n] = cm_pool.tile([P, HEADS, TOKENS], BF16, name="cm")
+            for h0 in range(first, last, PAIR):
+                seq, local = (first_values[h0 // QUAD], h0 % QUAD) if n == 0 else (values[n], h0)
+                pair = transpose_head_pair(nc, psum, "misc", 2, ident_bf16, seq, local)
                 for j in range(PAIR):
                     copy_and_sum(n + 1, h0 + j, value_cm[n][:, h0 + j, :], pair[:, j, :])
                 if h0 % QUAD == PAIR:
@@ -171,9 +173,9 @@ def tile_sharedattnprocessor_pa_kernel(tc, hidden_states, q, k, ref_key, ref_val
                     scalar2=shift[n][:, h : h + 1], op0=ALU.mult, op1=ALU.add,
                 )
 
-        def keys_to_partitions(seq, channel_major):
+        def keys_to_partitions(seq, channel_major, first=0, last=HEADS):
             banks = []
-            for h0 in range(0, HEADS, PAIR):
+            for h0 in range(first, last, PAIR):
                 if h0 % QUAD == 0:
                     grouped[seq, h0 // QUAD] = packing.tile(
                         [P, QUAD * HEAD_DIM * PACK], BF16, align_bytes=64, name="grouped"
@@ -187,7 +189,7 @@ def tile_sharedattnprocessor_pa_kernel(tc, hidden_states, q, k, ref_key, ref_val
         def regroup(seq, banks, first, last, copy):
             for b in range(first, last):
                 half, j0 = divmod(b * PAIR, QUAD)
-                group_words(copy, words_view(grouped[seq, half])[:, j0 : j0 + PAIR], banks[b][:])
+                group_words(copy, words_view(grouped[seq, half])[:, j0 : j0 + PAIR], banks[b - first][:])
 
         with ExitStack() as prepare:
             value_seqs = prepare.enter_context(tc.tile_pool(name="value_seqs", bufs=2))
@@ -196,71 +198,74 @@ def tile_sharedattnprocessor_pa_kernel(tc, hidden_states, q, k, ref_key, ref_val
             hs_scales = projection.tile([P, CH_PASSES * TOKENS], U8, align_bytes=64)
             wv_codes = projection.tile([P, CH_PASSES * CHANNELS], U32, align_bytes=64)
             wv_scales = projection.tile([P, CH_PASSES * CHANNELS], U8, align_bytes=64)
-            with tc.tile_pool(name="early", bufs=1) as early:
-                first_values = value_seqs.tile([P, ROW_TILES, CHANNELS], BF16, name="values")
-                first_rows = ref_value[0, 0].rearrange("(r p) c -> p r c", p=P)
-                for half in range(2):
-                    cols = slice(half * TOKENS, (half + 1) * TOKENS)
-                    nc.sync.dma_start(out=first_values[:, :, cols], in_=first_rows[:, :, cols])
-                values = [first_values]
-                hs = early.tile([P, ROW_TILES, CHANNELS], BF16)
-                hs_rows = hidden_states[0].rearrange("(r p) c -> p r c", p=P)
-                for r in range(ROW_TILES):
-                    nc.sync.dma_start(out=hs[:, r, :], in_=hs_rows[:, r, :])
-                wv_raw = early.tile([P, CH_PASSES * HALVES, 2, CHANNELS], BF16)
-                wv_rows = Wv.rearrange("(a p e) c -> p a e c", p=P, e=2)
+            early = prepare.enter_context(tc.tile_pool(name="early", bufs=1))
+            def load_first_values(half):
+                tile = value_seqs.tile([P, ROW_TILES, TOKENS], BF16, name="values")
+                rows = ref_value[0, 0].rearrange("(r p) c -> p r c", p=P)
+                nc.sync.dma_start(out=tile[:], in_=rows[:, :, half * TOKENS : (half + 1) * TOKENS])
+                return tile
+
+            wv_raw = early.tile([P, CH_PASSES * HALVES, 2, CHANNELS], BF16)
+            wv_rows = Wv.rearrange("(a p e) c -> p a e c", p=P, e=2)
+
+            def load_weights(g):
+                places = slice(g * HALVES, (g + 1) * HALVES)
+                nc.sync.dma_start(out=wv_raw[:, places], in_=wv_rows[:, places])
+
+            first_values = [load_first_values(0)]
+            load_weights(0)
+            hs = early.tile([P, ROW_TILES, CHANNELS], BF16)
+            hs_rows = hidden_states[0].rearrange("(r p) c -> p r c", p=P)
+            for r in range(ROW_TILES):
+                nc.sync.dma_start(out=hs[:, r, :], in_=hs_rows[:, r, :])
+            load_weights(1)
+            first_values.append(load_first_values(1))
+            values = {}
+
+            bring_values(0, 0, QUAD)
+            values[1] = load_sequence(nc, value_seqs, ref_value[0, 1], "values")
+            key_side = [load_sequence(nc, key_seqs, q[0], "queries"), load_sequence(nc, key_seqs, k[0], "keys")]
+
+            wv_grouped = {}
+
+            def group_weights(copy, g, half):
+                four_rows = wv_raw[:, g * HALVES : (g + 1) * HALVES].rearrange("p a e c -> p (a e) c")
+                wv_grouped[g, half] = early.tile([P, TOKENS, PACK], BF16, align_bytes=64, bufs=2, name="wv_grouped")
+                copy(
+                    out=wv_grouped[g, half][:].rearrange("p (c i) t -> p c t i", i=4),
+                    in_=four_rows[:, :, half * TOKENS : (half + 1) * TOKENS].rearrange("p t (c i) -> p c t i", i=4),
+                )
+
+            def quantise_weights(g, half):
+                words = slice(g * CHANNELS + half * TOKENS, g * CHANNELS + (half + 1) * TOKENS)
+                nc.vector.quantize_mx(
+                    out=wv_codes[:, words].bitcast(FP8X4),
+                    scales=wv_scales[:, words],
+                    in_=wv_grouped[g, half][:].rearrange("p c t -> p (c t)"),
+                )
+
+            group_weights(nc.vector.tensor_copy, 0, 1)
+            group_weights(nc.scalar.copy, 0, 0)
+            quantise_weights(0, 1)
+            group_weights(nc.vector.tensor_copy, 1, 0)
+            quantise_weights(0, 0)
+            hs_grouped = early.tile([P, CH_PASSES * TOKENS * PACK], BF16, align_bytes=64)
+            hs_words = words_view(hs_grouped)
+            for r in range(0, ROW_TILES, 2):
                 for g in range(CH_PASSES):
-                    places = slice(g * HALVES, (g + 1) * HALVES)
-                    nc.sync.dma_start(out=wv_raw[:, places], in_=wv_rows[:, places])
-                values.append(load_sequence(nc, value_seqs, ref_value[0, 1], "values"))
-                key_side = [load_sequence(nc, key_seqs, q[0], "queries"), load_sequence(nc, key_seqs, k[0], "keys")]
-
-                bring_values(0)
-                values.append(load_sequence(nc, value_seqs, ref_value[0, 2], "values"))
-                for n in range(2):
-                    key_side.append(load_sequence(nc, key_seqs, ref_key[0, n], "ref_keys%d" % n))
-                hs_grouped = early.tile([P, CH_PASSES * TOKENS * PACK], BF16, align_bytes=64)
-                hs_words = words_view(hs_grouped)
-                for r in range(0, ROW_TILES, 2):
-                    for g in range(CH_PASSES):
-                        bank = psum.tile([P, 2, HALVES, P], F32, tag="words", bufs=3)
-                        for j in range(2):
-                            transpose_pass(nc, bank[:, j], hs[:, r + j, g * TOKENS : (g + 1) * TOKENS], ident_f32)
-                        b0 = g * ROW_TILES + r
-                        group_words(nc.scalar.copy, hs_words[:, b0 : b0 + 2], bank[:])
-
-                wv_grouped = {}
-
-                def group_weights(copy, g, half):
-                    four_rows = wv_raw[:, g * HALVES : (g + 1) * HALVES].rearrange("p a e c -> p (a e) c")
-                    wv_grouped[g, half] = early.tile([P, TOKENS, PACK], BF16, align_bytes=64, bufs=2, name="wv_grouped")
-                    copy(
-                        out=wv_grouped[g, half][:].rearrange("p (c i) t -> p c t i", i=4),
-                        in_=four_rows[:, :, half * TOKENS : (half + 1) * TOKENS].rearrange("p t (c i) -> p c t i", i=4),
-                    )
-
-                def quantise_weights(g, half):
-                    words = slice(g * CHANNELS + half * TOKENS, g * CHANNELS + (half + 1) * TOKENS)
-                    nc.vector.quantize_mx(
-                        out=wv_codes[:, words].bitcast(FP8X4),
-                        scales=wv_scales[:, words],
-                        in_=wv_grouped[g, half][:].rearrange("p c t -> p (c t)"),
-                    )
-
-                group_weights(nc.vector.tensor_copy, 0, 1)
-                group_weights(nc.scalar.copy, 0, 0)
-                measure_values(0, 0, QUAD)
-                nc.vector.quantize_mx(out=hs_codes[:].bitcast(FP8X4), scales=hs_scales[:], in_=hs_grouped[:])
-                quantise_weights(0, 1)
-                group_weights(nc.vector.tensor_copy, 1, 0)
-                quantise_weights(0, 0)
-                quantise_weights(1, 0)
-                group_weights(nc.vector.tensor_copy, 1, 1)
-                quantise_weights(1, 1)
+                    bank = psum.tile([P, 2, HALVES, P], F32, tag="words", bufs=3)
+                    for j in range(2):
+                        transpose_pass(nc, bank[:, j], hs[:, r + j, g * TOKENS : (g + 1) * TOKENS], ident_f32)
+                    b0 = g * ROW_TILES + r
+                    group_words(nc.scalar.copy, hs_words[:, b0 : b0 + 2], bank[:])
+            nc.vector.quantize_mx(out=hs_codes[:].bitcast(FP8X4), scales=hs_scales[:], in_=hs_grouped[:])
+            quantise_weights(1, 0)
+            group_weights(nc.scalar.copy, 1, 1)
+            measure_values(0, 0, QUAD)
 
             def key_job(s):
                 pair = transpose_head_pair(nc, psum, "words", 3, ident_bf16, key_side[s], 0)
-                nc.scalar.copy(out=channel_major_home(s, 0), in_=pair[:])
+                nc.vector.tensor_copy(out=channel_major_home(s, 0), in_=pair[:])
 
             v_bf16 = cm_pool.tile([P, HEADS, TOKENS], BF16, name="cm")
             for h in range(HEADS):
@@ -280,14 +285,22 @@ def tile_sharedattnprocessor_pa_kernel(tc, hidden_states, q, k, ref_key, ref_val
                 copy_and_sum(0, h, v_bf16[:, h, :], vT[:])
                 negative_mean(0, slice(h, h + 1))
                 square(0, h, vT[:])
+                if h == 2:
+                    quantise_weights(1, 1)
+                if h == QUAD - 1:
+                    bring_values(0, QUAD, HEADS)
+                    values[2] = load_sequence(nc, value_seqs, ref_value[0, 2], "values")
+                    for n in range(2):
+                        key_side.append(load_sequence(nc, key_seqs, ref_key[0, n], "ref_keys%d" % n))
             deviation(0)
             measure_values(0, QUAD, HEADS)
             bring_values(1)
-            values.append(load_sequence(nc, value_seqs, ref_value[0, 3], "values"))
+            values[3] = load_sequence(nc, value_seqs, ref_value[0, 3], "values")
             for n in range(2, REFS):
                 key_side.append(load_sequence(nc, key_seqs, ref_key[0, n], "ref_keys%d" % n))
             v_banks = keys_to_partitions(0, v_bf16)
-            regroup(0, v_banks, 0, len(v_banks), nc.vector.tensor_copy)
+            regroup(0, v_banks, 0, 2, nc.vector.tensor_copy)
+            regroup(0, v_banks[2:], 2, len(v_banks), nc.scalar.copy)
             key_job(0)
             key_job(1)
             factors(0)
@@ -295,15 +308,15 @@ def tile_sharedattnprocessor_pa_kernel(tc, hidden_states, q, k, ref_key, ref_val
 
             for n in range(REFS - 2):
                 adain(n)
+                bring_values(n + 2, 0, QUAD)
                 quantise_values(n)
-                bring_values(n + 2)
+                regroup(n + 1, keys_to_partitions(n + 1, value_cm[n], 0, 3 * PAIR), 0, 3, nc.scalar.copy)
+                bring_values(n + 2, QUAD, HEADS)
+                regroup(n + 1, keys_to_partitions(n + 1, value_cm[n], 3 * PAIR), 3, 4, nc.scalar.copy)
                 factors(n + 1)
-                banks = keys_to_partitions(n + 1, value_cm[n])
-                regroup(n + 1, banks, 0, 2, nc.scalar.copy)
                 key_job(2 * n + 2)
                 key_job(2 * n + 3)
                 measure_values(n + 2)
-                regroup(n + 1, banks, 2, 4, nc.vector.tensor_copy)
 
         with ExitStack() as attend:
             work = attend.enter_context(tc.tile_pool(name="work", bufs=2, reuse_waits="tile"))
@@ -419,14 +432,14 @@ def tile_sharedattnprocessor_pa_kernel(tc, hidden_states, q, k, ref_key, ref_val
                     group_words(nc.scalar.copy, e_words[:, 0:2], banks[0][:])
                     copy = nc.scalar.copy if live(i + 1) else nc.vector.tensor_copy
                     group_words(copy, e_words[:, 2:4], banks[1][:])
-                if keys_to_do:
-                    nc.scalar.copy(out=channel_major_home(s, next_h0), in_=key_pair[:])
                 if live(i - 2):
                     quantise(i - 2, 0, 4)
                 leave(2)
                 scores_of(3, 2)
+                if keys_to_do:
+                    nc.vector.tensor_copy(out=channel_major_home(s, next_h0), in_=key_pair[:])
                 if live(i - 1):
-                    copy = nc.scalar.copy if live(i + 1) and not keys_to_do else nc.vector.tensor_copy
+                    copy = nc.scalar.copy if live(i + 1) else nc.vector.tensor_copy
                     group_words(copy, e_words[:, 4:5], banks[2][:, 0:1])
                 if live(i - 2):
                     quantise(i - 2, 4, 1)

@@ -55,15 +55,16 @@ def group_words(copy, grouped_words, bank):
     copy(out=grouped_words, in_=bank.rearrange("p b u r -> p b r u"))
 
 
-def transpose_head_pair(nc, psum, tag, bufs, ident_bf16, seq, h0):
+def transpose_head_pair(nc, psum, tag, bufs, ident_bf16, seq, h0, multiply=False):
     pair = psum.tile([P, PAIR, TOKENS], BF16, tag=tag, bufs=bufs)
     for j in range(PAIR):
         for r in range(ROW_TILES):
-            nc.tensor.transpose(
-                pair[:, j, r * P : (r + 1) * P],
-                seq[:, r, (h0 + j) * HEAD_DIM : (h0 + j + 1) * HEAD_DIM],
-                ident_bf16[:],
-            )
+            place = pair[:, j, r * P : (r + 1) * P]
+            block = seq[:, r, (h0 + j) * HEAD_DIM : (h0 + j + 1) * HEAD_DIM]
+            if multiply:
+                nc.tensor.matmul(place, lhsT=block, rhs=ident_bf16[:], start=True, stop=True)
+            else:
+                nc.tensor.transpose(place, block, ident_bf16[:])
     return pair
 
 
@@ -144,7 +145,7 @@ def tile_sharedattnprocessor_pa_kernel(tc, hidden_states, q, k, ref_key, ref_val
                 value_cm[n] = cm_pool.tile([P, HEADS, TOKENS], BF16, name="cm")
             for h0 in range(first, last, PAIR):
                 seq, local = (first_values[h0 // QUAD], h0 % QUAD) if n == 0 else (values[n], h0)
-                pair = transpose_head_pair(nc, psum, "misc", 2, ident_bf16, seq, local)
+                pair = transpose_head_pair(nc, psum, "misc", 2, ident_bf16, seq, local, multiply=n >= 2)
                 for j in range(PAIR):
                     copy_and_sum(n + 1, h0 + j, value_cm[n][:, h0 + j, :], pair[:, j, :])
                 if h0 % QUAD == PAIR:
@@ -180,6 +181,8 @@ def tile_sharedattnprocessor_pa_kernel(tc, hidden_states, q, k, ref_key, ref_val
                     grouped[seq, h0 // QUAD] = packing.tile(
                         [P, QUAD * HEAD_DIM * PACK], BF16, align_bytes=64, name="grouped"
                     )
+                if seq < REFS - 1:
+                    keep_clock()
                 bank = psum.tile([P, PAIR, HALVES, P], F32, tag="words", bufs=3)
                 for j in range(PAIR):
                     transpose_pass(nc, bank[:, j], channel_major[:, h0 + j, :], ident_f32)
@@ -263,7 +266,20 @@ def tile_sharedattnprocessor_pa_kernel(tc, hidden_states, q, k, ref_key, ref_val
             group_weights(nc.scalar.copy, 1, 1)
             measure_values(0, 0, QUAD)
 
+            def keep_clock():
+                unread = psum.tile([P, TOKENS], F32, tag="s_bank", bufs=3)
+                nc.tensor.matmul_mx(
+                    out=unread[:],
+                    lhsT=wv_codes[:, 0:P].bitcast(FP8X4),
+                    lhsT_scale=wv_scales[:, 0:P],
+                    rhs=hs_codes[:, 0:TOKENS].bitcast(FP8X4),
+                    rhs_scale=hs_scales[:, 0:TOKENS],
+                    start=True,
+                    stop=True,
+                )
+
             def key_job(s):
+                keep_clock()
                 pair = transpose_head_pair(nc, psum, "words", 3, ident_bf16, key_side[s], 0)
                 nc.vector.tensor_copy(out=channel_major_home(s, 0), in_=pair[:])
 
@@ -432,14 +448,14 @@ def tile_sharedattnprocessor_pa_kernel(tc, hidden_states, q, k, ref_key, ref_val
                     group_words(nc.scalar.copy, e_words[:, 0:2], banks[0][:])
                     copy = nc.scalar.copy if live(i + 1) else nc.vector.tensor_copy
                     group_words(copy, e_words[:, 2:4], banks[1][:])
+                if keys_to_do:
+                    nc.scalar.copy(out=channel_major_home(s, next_h0), in_=key_pair[:])
                 if live(i - 2):
                     quantise(i - 2, 0, 4)
                 leave(2)
                 scores_of(3, 2)
-                if keys_to_do:
-                    nc.vector.tensor_copy(out=channel_major_home(s, next_h0), in_=key_pair[:])
                 if live(i - 1):
-                    copy = nc.scalar.copy if live(i + 1) else nc.vector.tensor_copy
+                    copy = nc.scalar.copy if live(i + 1) and not keys_to_do else nc.vector.tensor_copy
                     group_words(copy, e_words[:, 4:5], banks[2][:, 0:1])
                 if live(i - 2):
                     quantise(i - 2, 4, 1)

from contextlib import ExitStack

import concourse.mybir as mybir
from concourse.masks import make_identity

BF16 = mybir.dt.bfloat16
F32 = mybir.dt.float32
U32 = mybir.dt.uint32
U8 = mybir.dt.uint8
FP8X4 = mybir.dt.float8_e4m3fn_x4
ALU = mybir.AluOpType
ACT = mybir.ActivationFunctionType
AXIS = mybir.AxisListType

P = 128
TOKENS = 512
CHANNELS = 1024
HEADS = 8
HEAD_DIM = CHANNELS // HEADS
REFS = 4
SEQS = REFS + 1
KEYS = SEQS * TOKENS
ROW_TILES = TOKENS // P
PACK = 4
PAIR = 2
QUAD = 4
HALVES = 2
CH_PASSES = CHANNELS // TOKENS
EPS = 1e-5
SCORE_SCALE = HEAD_DIM**-0.5
SMALLEST_VARIANCE = 1e-30

UNITS = HEADS * ROW_TILES

FLOPS = 2 * TOKENS * CHANNELS * CHANNELS + 2 * (2 * HEADS * TOKENS * KEYS * HEAD_DIM)


def load_sequence(nc, pool, rows, name):
    seq = pool.tile([P, ROW_TILES, CHANNELS], BF16, name=name)
    nc.sync.dma_start(out=seq[:], in_=rows.rearrange("(r p) c -> p r c", p=P))
    return seq


def words_view(grouped):
    return grouped[:].bitcast(F32).rearrange("p (b r u) -> p b r u", r=P, u=HALVES)


def transpose_pass(nc, half_bank, block, ident_f32):
    block_words = block.bitcast(F32)
    for u in range(HALVES):
        nc.tensor.transpose(half_bank[:, u, :], block_words[:, u * P : (u + 1) * P], ident_f32[:])


def group_words(copy, grouped_words, bank):
    copy(out=grouped_words, in_=bank.rearrange("p b u r -> p b r u"))


def transpose_head_pair(nc, psum, tag, bufs, ident_bf16, seq, h0, multiply=False):
    pair = psum.tile([P, PAIR, TOKENS], BF16, tag=tag, bufs=bufs)
    for j in range(PAIR):
        for r in range(ROW_TILES):
            place = pair[:, j, r * P : (r + 1) * P]
            block = seq[:, r, (h0 + j) * HEAD_DIM : (h0 + j + 1) * HEAD_DIM]
            if multiply:
                nc.tensor.matmul(place, lhsT=block, rhs=ident_bf16[:], start=True, stop=True)
            else:
                nc.tensor.transpose(place, block, ident_bf16[:])
    return pair


def tile_sharedattnprocessor_pa_kernel(tc, hidden_states, q, k, ref_key, ref_value, Wv, out):
    nc = tc.nc
    with ExitStack() as whole:
        whole.enter_context(tc.manual_schedule())
        const = whole.enter_context(tc.tile_pool(name="const", bufs=1))
        keep = whole.enter_context(tc.tile_pool(name="keep", bufs=1))
        key_seqs = whole.enter_context(tc.tile_pool(name="key_seqs", bufs=1))
        psum = whole.enter_context(tc.psum_pool(name="psum", bufs=3, reuse_waits="tile"))

        ident_bf16 = const.tile([P, P], BF16)
        make_identity(nc, ident_bf16[:])
        ident_f32 = const.tile([P, P], F32)
        make_identity(nc, ident_f32[:])

        qT = keep.tile([P, HEADS, TOKENS], BF16)
        kT = keep.tile([P, HEADS, KEYS], BF16)
        v_codes = keep.tile([P, SEQS, CHANNELS], U32, align_bytes=64)
        v_scales = keep.tile([P, SEQS, CHANNELS], U8, align_bytes=64)

        def channel_major_home(s, h0):
            if s == 0:
                return qT[:, h0 : h0 + PAIR, :]
            return kT[:, h0 : h0 + PAIR, (s - 1) * TOKENS : s * TOKENS]

        packing = whole.enter_context(tc.tile_pool(name="packing", bufs=2, reuse_waits="tile"))
        grouped = {}

        def quantise_values(seq):
            for half in range(HEADS // QUAD):
                cols = slice(half * QUAD * HEAD_DIM, (half + 1) * QUAD * HEAD_DIM)
                nc.vector.quantize_mx(
                    out=v_codes[:, seq, cols].bitcast(FP8X4), scales=v_scales[:, seq, cols], in_=grouped[seq, half][:]
                )

        cm_pool = whole.enter_context(tc.tile_pool(name="cm_pool", bufs=4, reuse_waits="tile"))
        stats = whole.enter_context(tc.tile_pool(name="stats", bufs=1))
        tiny = stats.tile([P, 1], F32)
        nc.gpsimd.memset(tiny[:], SMALLEST_VARIANCE)
        table_probe = stats.tile([P, 1], F32)
        nc.scalar.activation(out=table_probe[:], in_=tiny[:], func=ACT.Sqrt)

        sums, neg_mean, squares, std, inverse, gain, shift = {}, {}, {}, {}, {}, {}, {}
        for seq in range(SEQS):
            for name, column in (("sums", sums), ("neg_mean", neg_mean), ("squares", squares), ("std", std)):
                column[seq] = stats.tile([P, HEADS], F32, name="%s%d" % (name, seq))
        value_cm = {}

        def copy_and_sum(seq, h, out, bank):
            nc.vector.tensor_scalar(
                out=out, in0=bank, scalar1=1.0, scalar2=None, op0=ALU.mult, op1=ALU.add,
                accum_out=sums[seq][:, h : h + 1],
            )

        def negative_mean(seq, heads):
            nc.gpsimd.tensor_scalar(
                out=neg_mean[seq][:, heads], in0=sums[seq][:, heads], scalar1=-1.0 / TOKENS, scalar2=None,
                op0=ALU.mult,
            )

        def square(seq, h, source):
            distance = stats.tile([P, TOKENS], BF16, name="distance", bufs=2)
            nc.scalar.activation(
                out=distance[:], in_=source, func=ACT.Square, bias=neg_mean[seq][:, h : h + 1], scale=1.0,
                accum_out=squares[seq][:, h : h + 1],
            )

        def deviation(seq):
            nc.scalar.activation(
                out=std[seq][:], in_=squares[seq][:], func=ACT.Sqrt, scale=1.0 / (TOKENS - 1), bias=tiny[:]
            )
            nc.gpsimd.tensor_scalar(out=std[seq][:], in0=std[seq][:], scalar1=EPS, scalar2=None, op0=ALU.add)

        def bring_values(n, first=0, last=HEADS):
            if first == 0:
                value_cm[n] = cm_pool.tile([P, HEADS, TOKENS], BF16, name="cm")
            for h0 in range(first, last, PAIR):
                seq, local = (first_values[h0 // QUAD], h0 % QUAD) if n == 0 else (values[n], h0)
                pair = transpose_head_pair(nc, psum, "misc", 2, ident_bf16, seq, local, multiply=n >= 2)
                for j in range(PAIR):
                    copy_and_sum(n + 1, h0 + j, value_cm[n][:, h0 + j, :], pair[:, j, :])
                if h0 % QUAD == PAIR:
                    negative_mean(n + 1, slice(h0 + PAIR - QUAD, h0 + PAIR))

        def measure_values(n, first=0, last=HEADS):
            for h in range(first, last):
                square(n + 1, h, value_cm[n][:, h, :])
            if last == HEADS:
                deviation(n + 1)

        def factors(n):
            seq = n + 1
            inverse[n] = stats.tile([P, HEADS], F32, name="inverse%d" % n)
            gain[n] = stats.tile([P, HEADS], F32, name="gain%d" % n)
            shift[n] = stats.tile([P, HEADS], F32, name="shift%d" % n)
            nc.vector.reciprocal(out=inverse[n][:], in_=std[seq][:])
            nc.gpsimd.tensor_tensor(out=gain[n][:], in0=inverse[n][:], in1=std[0][:], op=ALU.mult)
            nc.gpsimd.tensor_tensor(out=shift[n][:], in0=neg_mean[seq][:], in1=gain[n][:], op=ALU.mult)
            nc.gpsimd.tensor_tensor(out=shift[n][:], in0=shift[n][:], in1=neg_mean[0][:], op=ALU.subtract)

        def adain(n):
            for h in range(HEADS):
                nc.vector.tensor_scalar(
                    out=value_cm[n][:, h, :], in0=value_cm[n][:, h, :], scalar1=gain[n][:, h : h + 1],
                    scalar2=shift[n][:, h : h + 1], op0=ALU.mult, op1=ALU.add,
                )

        def keys_to_partitions(seq, channel_major, first=0, last=HEADS):
            banks = []
            for h0 in range(first, last, PAIR):
                if h0 % QUAD == 0:
                    grouped[seq, h0 // QUAD] = packing.tile(
                        [P, QUAD * HEAD_DIM * PACK], BF16, align_bytes=64, name="grouped"
                    )
                if seq < REFS - 1:
                    keep_clock()
                bank = psum.tile([P, PAIR, HALVES, P], F32, tag="words", bufs=3)
                for j in range(PAIR):
                    transpose_pass(nc, bank[:, j], channel_major[:, h0 + j, :], ident_f32)
                banks.append(bank)
            return banks

        def regroup(seq, banks, first, last, copy):
            for b in range(first, last):
                half, j0 = divmod(b * PAIR, QUAD)
                group_words(copy, words_view(grouped[seq, half])[:, j0 : j0 + PAIR], banks[b - first][:])

        with ExitStack() as prepare:
            value_seqs = prepare.enter_context(tc.tile_pool(name="value_seqs", bufs=2))
            projection = prepare.enter_context(tc.tile_pool(name="projection", bufs=1))
            hs_codes = projection.tile([P, CH_PASSES * TOKENS], U32, align_bytes=64)
            hs_scales = projection.tile([P, CH_PASSES * TOKENS], U8, align_bytes=64)
            wv_codes = projection.tile([P, CH_PASSES * CHANNELS], U32, align_bytes=64)
            wv_scales = projection.tile([P, CH_PASSES * CHANNELS], U8, align_bytes=64)
            early = prepare.enter_context(tc.tile_pool(name="early", bufs=1))
            def load_first_values(half):
                tile = value_seqs.tile([P, ROW_TILES, TOKENS], BF16, name="values")
                rows = ref_value[0, 0].rearrange("(r p) c -> p r c", p=P)
                nc.sync.dma_start(out=tile[:], in_=rows[:, :, half * TOKENS : (half + 1) * TOKENS])
                return tile

            wv_raw = early.tile([P, CH_PASSES * HALVES, 2, CHANNELS], BF16)
            wv_rows = Wv.rearrange("(a p e) c -> p a e c", p=P, e=2)

            def load_weights(g):
                places = slice(g * HALVES, (g + 1) * HALVES)
                nc.sync.dma_start(out=wv_raw[:, places], in_=wv_rows[:, places])

            first_values = [load_first_values(0)]
            load_weights(0)
            hs = early.tile([P, ROW_TILES, CHANNELS], BF16)
            hs_rows = hidden_states[0].rearrange("(r p) c -> p r c", p=P)
            for r in range(ROW_TILES):
                nc.sync.dma_start(out=hs[:, r, :], in_=hs_rows[:, r, :])
            load_weights(1)
            first_values.append(load_first_values(1))
            values = {}

            bring_values(0, 0, QUAD)
            values[1] = load_sequence(nc, value_seqs, ref_value[0, 1], "values")
            key_side = [load_sequence(nc, key_seqs, q[0], "queries"), load_sequence(nc, key_seqs, k[0], "keys")]

            wv_grouped = {}

            def group_weights(copy, g, half):
                four_rows = wv_raw[:, g * HALVES : (g + 1) * HALVES].rearrange("p a e c -> p (a e) c")
                wv_grouped[g, half] = early.tile([P, TOKENS, PACK], BF16, align_bytes=64, bufs=2, name="wv_grouped")
                copy(
                    out=wv_grouped[g, half][:].rearrange("p (c i) t -> p c t i", i=4),
                    in_=four_rows[:, :, half * TOKENS : (half + 1) * TOKENS].rearrange("p t (c i) -> p c t i", i=4),
                )

            def quantise_weights(g, half):
                words = slice(g * CHANNELS + half * TOKENS, g * CHANNELS + (half + 1) * TOKENS)
                nc.vector.quantize_mx(
                    out=wv_codes[:, words].bitcast(FP8X4),
                    scales=wv_scales[:, words],
                    in_=wv_grouped[g, half][:].rearrange("p c t -> p (c t)"),
                )

            group_weights(nc.vector.tensor_copy, 0, 1)
            group_weights(nc.scalar.copy, 0, 0)
            quantise_weights(0, 1)
            group_weights(nc.vector.tensor_copy, 1, 0)
            quantise_weights(0, 0)
            hs_grouped = early.tile([P, CH_PASSES * TOKENS * PACK], BF16, align_bytes=64)
            hs_words = words_view(hs_grouped)
            for r in range(0, ROW_TILES, 2):
                for g in range(CH_PASSES):
                    bank = psum.tile([P, 2, HALVES, P], F32, tag="words", bufs=3)
                    for j in range(2):
                        transpose_pass(nc, bank[:, j], hs[:, r + j, g * TOKENS : (g + 1) * TOKENS], ident_f32)
                    b0 = g * ROW_TILES + r
                    group_words(nc.scalar.copy, hs_words[:, b0 : b0 + 2], bank[:])
            nc.vector.quantize_mx(out=hs_codes[:].bitcast(FP8X4), scales=hs_scales[:], in_=hs_grouped[:])
            quantise_weights(1, 0)
            group_weights(nc.scalar.copy, 1, 1)
            measure_values(0, 0, QUAD)

            def keep_clock():
                unread = psum.tile([P, TOKENS], F32, tag="s_bank", bufs=3)
                nc.tensor.matmul_mx(
                    out=unread[:],
                    lhsT=wv_codes[:, 0:P].bitcast(FP8X4),
                    lhsT_scale=wv_scales[:, 0:P],
                    rhs=hs_codes[:, 0:TOKENS].bitcast(FP8X4),
                    rhs_scale=hs_scales[:, 0:TOKENS],
                    start=True,
                    stop=True,
                )

            def key_job(s):
                keep_clock()
                pair = transpose_head_pair(nc, psum, "words", 3, ident_bf16, key_side[s], 0)
                nc.vector.tensor_copy(out=channel_major_home(s, 0), in_=pair[:])

            v_bf16 = cm_pool.tile([P, HEADS, TOKENS], BF16, name="cm")
            for h in range(HEADS):
                vT = psum.tile([P, TOKENS], F32, tag="s_bank", bufs=3)
                for g in range(CH_PASSES):
                    w_cols = slice(g * CHANNELS + h * HEAD_DIM, g * CHANNELS + (h + 1) * HEAD_DIM)
                    t_cols = slice(g * TOKENS, (g + 1) * TOKENS)
                    nc.tensor.matmul_mx(
                        out=vT[:],
                        lhsT=wv_codes[:, w_cols].bitcast(FP8X4),
                        lhsT_scale=wv_scales[:, w_cols],
                        rhs=hs_codes[:, t_cols].bitcast(FP8X4),
                        rhs_scale=hs_scales[:, t_cols],
                        start=(g == 0),
                        stop=(g == CH_PASSES - 1),
                    )
                copy_and_sum(0, h, v_bf16[:, h, :], vT[:])
                negative_mean(0, slice(h, h + 1))
                square(0, h, vT[:])
                if h == 2:
                    quantise_weights(1, 1)
                if h == QUAD - 1:
                    bring_values(0, QUAD, HEADS)
                    values[2] = load_sequence(nc, value_seqs, ref_value[0, 2], "values")
                    for n in range(2):
                        key_side.append(load_sequence(nc, key_seqs, ref_key[0, n], "ref_keys%d" % n))
            deviation(0)
            measure_values(0, QUAD, HEADS)
            bring_values(1)
            values[3] = load_sequence(nc, value_seqs, ref_value[0, 3], "values")
            for n in range(2, REFS):
                key_side.append(load_sequence(nc, key_seqs, ref_key[0, n], "ref_keys%d" % n))
            v_banks = keys_to_partitions(0, v_bf16)
            regroup(0, v_banks, 0, 2, nc.vector.tensor_copy)
            regroup(0, v_banks[2:], 2, len(v_banks), nc.scalar.copy)
            key_job(0)
            key_job(1)
            factors(0)
            measure_values(1)

            for n in range(REFS - 2):
                adain(n)
                bring_values(n + 2, 0, QUAD)
                quantise_values(n)
                regroup(n + 1, keys_to_partitions(n + 1, value_cm[n], 0, 3 * PAIR), 0, 3, nc.scalar.copy)
                bring_values(n + 2, QUAD, HEADS)
                regroup(n + 1, keys_to_partitions(n + 1, value_cm[n], 3 * PAIR), 3, 4, nc.scalar.copy)
                factors(n + 1)
                key_job(2 * n + 2)
                key_job(2 * n + 3)
                measure_values(n + 2)

        with ExitStack() as attend:
            work = attend.enter_context(tc.tile_pool(name="work", bufs=2, reuse_waits="tile"))
            small = attend.enter_context(tc.tile_pool(name="small", bufs=3, reuse_waits="tile"))
            scores, bank_max, neg_max, e, row_sum, inv_sum = {}, {}, {}, {}, {}, {}
            e_grouped, e_codes, e_scales, o_bank, s_bank, banks, later_sums = {}, {}, {}, {}, {}, {}, {}

            def live(unit):
                return 0 <= unit < UNITS

            def exponential(i):
                e[i] = work.tile([P, KEYS], BF16, name="e")
                row_sum[i] = small.tile([P, 1], F32, name="row_sum", bufs=5)
                parts = (0, KEYS) if i < UNITS - 1 else (0, 2 * TOKENS, KEYS)
                sums_of_parts = [row_sum[i]]
                for part in range(1, len(parts) - 1):
                    sums_of_parts.append(small.tile([P, 1], F32, name="part_sum", bufs=1))
                for part, total in enumerate(sums_of_parts):
                    columns = slice(parts[part], parts[part + 1])
                    nc.scalar.activation(
                        out=e[i][:, columns], in_=scores[i][:, columns], func=ACT.Exp, bias=neg_max[i][:], scale=1.0,
                        accum_out=total[:],
                    )
                later_sums[i] = sums_of_parts[1:]

            def score(i, g):
                h, qt = divmod(i, ROW_TILES)
                s_bank[g] = psum.tile([P, TOKENS], F32, name="s_bank", bufs=3)
                nc.tensor.matmul(
                    s_bank[g][:],
                    lhsT=qT[:, h, qt * P : (qt + 1) * P],
                    rhs=kT[:, h, g * TOKENS : (g + 1) * TOKENS],
                    start=True,
                    stop=True,
                )

            def evacuate(i, g):
                nc.vector.tensor_scalar(
                    out=scores[i][:, g * TOKENS : (g + 1) * TOKENS], in0=s_bank[g][:],
                    scalar1=SCORE_SCALE, scalar2=None, op0=ALU.mult, op1=ALU.max,
                    accum_out=bank_max[i][:, g : g + 1],
                )

            def quantise(i, first, count):
                cols = slice(first * P, (first + count) * P)
                nc.vector.quantize_mx(
                    out=e_codes[i][:, cols].bitcast(FP8X4),
                    scales=e_scales[i][:, cols],
                    in_=e_grouped[i][:, first * P * PACK : (first + count) * P * PACK],
                )

            def weigh_values(i):
                h = i // ROW_TILES
                o_bank[i] = psum.tile([P, HEAD_DIM], F32, name="o_bank", tag="misc", bufs=2)
                for g in range(SEQS):
                    nc.tensor.matmul_mx(
                        out=o_bank[i][:],
                        lhsT=e_codes[i][:, g * P : (g + 1) * P].bitcast(FP8X4),
                        lhsT_scale=e_scales[i][:, g * P : (g + 1) * P],
                        rhs=v_codes[:, g, h * HEAD_DIM : (h + 1) * HEAD_DIM].bitcast(FP8X4),
                        rhs_scale=v_scales[:, g, h * HEAD_DIM : (h + 1) * HEAD_DIM],
                        start=(g == 0),
                        stop=(g == SEQS - 1),
                    )

            def finish(i):
                h, qt = divmod(i, ROW_TILES)
                o = work.tile([P, HEAD_DIM], F32)
                nc.vector.tensor_scalar_mul(out=o[:], in0=o_bank[i][:], scalar1=inv_sum[i][:])
                nc.sync.dma_start(out=out[0, qt * P : (qt + 1) * P, h * HEAD_DIM : (h + 1) * HEAD_DIM], in_=o[:])

            rounds_of_a_pair = PAIR * ROW_TILES
            for i in range(-1, UNITS + 3):
                if live(i):
                    exponential(i)
                next_h0 = (i // rounds_of_a_pair + 1) * PAIR
                s = i % rounds_of_a_pair
                keys_to_do = live(i) and next_h0 < HEADS and s < len(key_side)
                if live(i + 1):
                    scores[i + 1] = work.tile([P, KEYS], F32, name="scores", bufs=3)
                    bank_max[i + 1] = small.tile([P, SEQS], F32, name="bank_max")
                if live(i - 1):
                    e_grouped[i - 1] = work.tile([P, KEYS], BF16, align_bytes=64, name="e_grouped")
                    e_words = words_view(e_grouped[i - 1])
                if live(i - 2):
                    e_codes[i - 2] = work.tile([P, SEQS * P], U32, align_bytes=64, name="e_codes")
                    e_scales[i - 2] = work.tile([P, SEQS * P], U8, align_bytes=64, name="e_scales")
                def scores_of(first, count):
                    if live(i + 1):
                        for g in range(first, first + count):
                            score(i + 1, g)

                def leave(g):
                    if live(i + 1):
                        evacuate(i + 1, g)

                late = {0: REFS - 2, 1: REFS - 1}.get(i)
                if late is not None:
                    adain(late)
                if 0 <= i <= 2:
                    quantise_values(REFS - 2 + i)
                scores_of(0, 3)
                leave(0)
                leave(1)
                if live(i - 1):
                    for g in range(SEQS):
                        if g % 2 == 0:
                            banks[g // 2] = psum.tile([P, 2, HALVES, P], F32, name="bank", tag="words", bufs=3)
                        transpose_pass(nc, banks[g // 2][:, g % 2], e[i - 1][:, g * TOKENS : (g + 1) * TOKENS], ident_f32)
                if keys_to_do:
                    key_pair = transpose_head_pair(nc, psum, "misc", 2, ident_bf16, key_side[s], next_h0)
                if live(i - 1):
                    group_words(nc.scalar.copy, e_words[:, 0:2], banks[0][:])
                    copy = nc.scalar.copy if live(i + 1) else nc.vector.tensor_copy
                    group_words(copy, e_words[:, 2:4], banks[1][:])
                if keys_to_do:
                    nc.scalar.copy(out=channel_major_home(s, next_h0), in_=key_pair[:])
                if live(i - 2):
                    quantise(i - 2, 0, 4)
                leave(2)
                scores_of(3, 2)
                if live(i - 1):
                    copy = nc.scalar.copy if live(i + 1) and not keys_to_do else nc.vector.tensor_copy
                    group_words(copy, e_words[:, 4:5], banks[2][:, 0:1])
                if live(i - 2):
                    quantise(i - 2, 4, 1)
                    for total in later_sums[i - 2]:
                        nc.vector.tensor_add(out=row_sum[i - 2][:], in0=row_sum[i - 2][:], in1=total[:])
                    inv_sum[i - 2] = small.tile([P, 1], F32, name="inv_sum")
                    nc.vector.reciprocal(out=inv_sum[i - 2][:], in_=row_sum[i - 2][:])
                leave(3)
                if live(i - 3):
                    weigh_values(i - 3)
                leave(4)
                if live(i - 3):
                    finish(i - 3)
                if late is not None:
                    late_banks = keys_to_partitions(late + 1, value_cm[late])
                    regroup(late + 1, late_banks, 0, len(late_banks), nc.scalar.copy)
                    if late + 1 < REFS:
                        factors(late + 1)
                if live(i + 1):
                    neg_max[i + 1] = small.tile([P, 1], F32, name="neg_max")
                    nc.vector.tensor_reduce(
                        out=neg_max[i + 1][:], in_=bank_max[i + 1][:], axis=AXIS.X, op=ALU.max, negate=True
                    )
